import numpy as np
import ml_dtypes


def mxq(x, axis, fmt="e4m3"):
    dtype, down = {"e4m3": (ml_dtypes.float8_e4m3fn, 7), "e5m2": (ml_dtypes.float8_e5m2, 14)}[fmt]
    v = np.moveaxis(np.asarray(x, np.float32).astype(ml_dtypes.bfloat16).astype(np.float64), axis, -1)
    blocks = v.reshape(v.shape[:-1] + (-1, 32))
    amax = np.abs(blocks).max(-1, keepdims=True)
    byte = np.maximum(np.where(amax > 0, np.frexp(amax)[1] - 1 + 127, 0) - down, 1)
    scale = np.exp2(byte - 127.0)
    codes = (blocks / scale).astype(np.float32).astype(dtype).astype(np.float64)
    return np.moveaxis((codes * scale).reshape(v.shape), -1, axis)


WIDE = False


def mx_kscale(k):
    if not WIDE:
        return np.ones(k)
    levels = np.array([10, -10, 5, -5, 0])
    if k % 512:
        return np.exp2(np.random.permutation(np.resize(levels, k // 32))).repeat(32)
    a = np.empty((k // 512, 16))
    for p in range(k // 512):
        a[p, :8] = np.random.permutation(np.resize(levels, 8))
        for g in range(8):
            far = levels[np.abs(levels - a[p, g]) >= 10]
            a[p, g + 8] = far[np.random.randint(len(far))]
    return np.exp2(a.ravel()).repeat(32)


BF16 = ml_dtypes.bfloat16


def bf(x):
    return np.asarray(x, np.float32).astype(BF16)


def f64(x):
    return np.asarray(x).astype(np.float64)


B, S, D, H, DH, DL, DR = 2, 2048, 1024, 2, 128, 512, 64
ROPE_BASE = 10000.0


def rope_cos_sin():
    inv_freq = 1.0 / ROPE_BASE ** (np.arange(0, DR, 2) / DR)
    freqs = np.arange(S)[:, None] * inv_freq[None, :]
    emb = np.concatenate([freqs, freqs], axis=-1)
    return np.cos(emb)[None, :, None, :], np.sin(emb)[None, :, None, :]


def rotate_half(u):
    u1, u2 = np.split(u, 2, axis=-1)
    return np.concatenate([-u2, u1], axis=-1)


def draw0():
    s, t = mx_kscale(D), mx_kscale(DL)
    return {"x": bf(np.random.standard_normal((B, S, D)) * s),
            "W_kv_down": bf(np.random.standard_normal((D, DL)) / np.sqrt(D) / s[:, None] * t),
            "W_kv_up": bf(np.random.standard_normal((DL, H * (DH + DR + DH))) / np.sqrt(DL) / t[:, None])}


def core(x, W_kv_down, W_kv_up):
    kv_latent = mxq(f64(x), 2, "e4m3") @ mxq(f64(W_kv_down), 0, "e4m3")
    kv_full = (mxq(kv_latent, 2, "e4m3") @ mxq(f64(W_kv_up), 0, "e4m3")).reshape(B, S, H, DH + DR + DH)
    k_content = kv_full[..., :DH]
    k_rope = kv_full[..., DH:DH + DR]
    v = kv_full[..., DH + DR:]
    cos, sin = rope_cos_sin()
    k_rope = k_rope * cos + rotate_half(k_rope) * sin
    k = np.concatenate([k_content, k_rope], axis=-1)
    return k, v


def e4m3fn_bytes(y):
    return np.clip(np.asarray(y, np.float64), -448.0, 448.0).astype(np.float32).astype(ml_dtypes.float8_e4m3fn).view(np.uint8)


def e4m3fn_values(b):
    return np.asarray(b, np.uint8).view(ml_dtypes.float8_e4m3fn).astype(np.float64)


def setup_inputs():
    d = draw0()
    x0 = np.asarray(d['x']).astype(np.float64)
    s = (np.max(np.abs(x0), axis=(0, 1), keepdims=True) / 448.0).astype(np.float32)
    out = {}
    for k, v in d.items():
        if k == 'x':
            out['x_bytes'] = e4m3fn_bytes(x0 / s.astype(np.float64))
            out['x_scale'] = s
        else:
            out[k] = v
    return out


def reference(x_bytes, x_scale, W_kv_down, W_kv_up):
    return core(e4m3fn_values(x_bytes) * x_scale.astype(np.float64), W_kv_down, W_kv_up)

@@ -1,0 +1,329 @@
+import math
+from contextlib import ExitStack
+
+import concourse.mybir as mybir
+from concourse.masks import make_identity
+
+F32 = mybir.dt.float32
+BF16 = mybir.dt.bfloat16
+U32 = mybir.dt.uint32
+I32 = mybir.dt.int32
+U8 = mybir.dt.uint8
+FP8 = mybir.dt.float8_e4m3fn
+FP8X4 = mybir.dt.float8_e4m3fn_x4
+ALU = mybir.AluOpType
+ACT = mybir.ActivationFunctionType
+
+B, S, D, H, DH, DL, DR = 2, 2048, 1024, 2, 128, 512, 64
+N_UP = H * (2 * DH + DR)
+FLOPS = 2 * B * S * D * DL + 2 * B * S * DL * N_UP
+
+P = 128
+GROUP = 4
+HALF = DR // 2
+N_GROUPS = B * S // (P * GROUP)
+POS_GROUPS = S // (P * GROUP)
+STEPS = N_GROUPS * 2
+TURN = 0.15915496
+C1 = 6.28125
+C2 = 2 * math.pi - C1
+
+
+def tile_multilatentattention_pa_t_kernel(tc, x_bytes, x_scale, w_down, w_up, out_k, out_v):
+    nc = tc.nc
+    x_view = x_bytes.rearrange("b (g q i) d -> (b g) q i d", q=P, i=GROUP)
+    k_view = out_k.rearrange("b (g q i) h f -> (b g) q i (h f)", q=P, i=GROUP)
+    v_view = out_v.rearrange("b (g q i) h f -> (b g) q i h f", q=P, i=GROUP)
+    wd_view = w_down.rearrange("(g p j) c -> g p j c", p=P, j=4)
+
+    with ExitStack() as ctx:
+        const = ctx.enter_context(tc.tile_pool(name="const", bufs=1))
+        xin = ctx.enter_context(tc.tile_pool(name="xin", bufs=N_GROUPS))
+        work = ctx.enter_context(tc.tile_pool(name="work", bufs=3))
+        outp = ctx.enter_context(tc.tile_pool(name="outp", bufs=3))
+        psum = ctx.enter_context(tc.psum_pool(name="psum", bufs=2))
+        ctx.enter_context(tc.manual_schedule())
+
+        wd_raw = const.tile([P, 2, 4, DL], BF16)
+        wu_raw = const.tile([P, 4, N_UP], BF16)
+        x_tiles = []
+        for g in range(N_GROUPS):
+            xb = xin.tile([P, GROUP, D], U8, name="xb")
+            x_tiles.append(xb)
+        scale_cols = const.tile([P, 2, 4], F32)
+        nc.sync.dma_start(out=scale_cols[:], in_=x_scale.rearrange("a b (g p t) -> p (a b g) t", p=P, t=4))
+        nc.sync.dma_start(out=x_tiles[0][:, 0:2], in_=x_view[0][:, 0:2])
+        nc.sync.dma_start(out=wd_raw[:, 0], in_=wd_view[0])
+        nc.sync.dma_start(out=wd_raw[:, 1], in_=wd_view[1])
+        nc.sync.dma_start(out=x_tiles[0][:, 2:4], in_=x_view[0][:, 2:4])
+        nc.sync.dma_start(out=wu_raw[:], in_=w_up.rearrange("(p j) n -> p j n", j=4))
+        nc.sync.dma_start(out=x_tiles[1][:], in_=x_view[1])
+        for g in range(2, N_GROUPS):
+            nc.sync.dma_start(out=x_tiles[g][:], in_=x_view[g])
+
+        warm = const.tile([P, 1], F32)
+        nc.vector.memset(warm[:], 0.0)
+        nc.scalar.activation(out=warm[:], in_=warm[:], func=ACT.Sin)
+        pos = const.tile([P, POS_GROUPS, GROUP], F32)
+        nc.gpsimd.iota(pos[:], pattern=[[P * GROUP, POS_GROUPS], [1, GROUP]], base=0, channel_multiplier=GROUP, allow_small_or_imprecise_dtypes=True)
+        ident = const.tile([P, P], F32)
+        make_identity(nc, ident[:])
+        freq = const.tile([P, HALF], F32)
+        nc.vector.memset(freq[:], 1.0)
+        for b in range(5):
+            f = freq[:].rearrange("p (x y z) -> p x y z", y=2, z=2 ** b)[:, :, 1, :]
+            nc.vector.tensor_scalar(out=f, in0=f, scalar1=10000.0 ** (-(2 ** b) / HALF), scalar2=None, op0=ALU.mult)
+        shape = [P, POS_GROUPS * GROUP, HALF]
+        ang = const.tile(shape, F32)
+        turns = const.tile(shape, I32)
+        turns_f = const.tile(shape, F32)
+        red = const.tile(shape, F32)
+        red2 = const.tile(shape, F32)
+        mag = const.tile(shape, F32)
+        sin = const.tile([P, POS_GROUPS * GROUP, 2, HALF], F32)
+        cos = const.tile(shape, F32)
+        nc.vector.tensor_tensor(
+            out=ang[:],
+            in0=pos[:].rearrange("p a b -> p (a b)").unsqueeze(2).to_broadcast(shape),
+            in1=freq[:].unsqueeze(1).to_broadcast(shape),
+            op=ALU.mult,
+        )
+        nc.vector.tensor_scalar(out=turns[:], in0=ang[:], scalar1=TURN, scalar2=None, op0=ALU.mult)
+        nc.vector.tensor_copy(out=turns_f[:], in_=turns[:])
+        nc.vector.scalar_tensor_tensor(out=red[:], in0=turns_f[:], scalar=-C1, in1=ang[:], op0=ALU.mult, op1=ALU.add)
+        nc.vector.scalar_tensor_tensor(out=red2[:], in0=turns_f[:], scalar=-C2, in1=red[:], op0=ALU.mult, op1=ALU.add)
+
+        wd_grp = const.tile([P, 2, DL * 4], BF16, align_bytes=64)
+        wd_codes = const.tile([P, 2, DL], U32, align_bytes=64)
+        wd_scales = const.tile([P, 2, DL], U8, align_bytes=64)
+        wu_main_grp = const.tile([P, 2, H, DH, 4], BF16, align_bytes=64)
+        wu_rope_grp = const.tile([P, H, DR, 4], BF16, align_bytes=64)
+        wu_main_codes = const.tile([P, 4 * DH], U32, align_bytes=64)
+        wu_main_scales = const.tile([P, 4 * DH], U8, align_bytes=64)
+        wu_rope_codes = const.tile([P, H * DR], U32, align_bytes=64)
+        wu_rope_scales = const.tile([P, H * DR], U8, align_bytes=64)
+
+        def group_down(g, copy):
+            copy(
+                out=wd_grp[:, g].rearrange("p (t m j) -> p t m j", t=4, j=4),
+                in_=wd_raw[:, g].rearrange("p j (m t) -> p t m j", t=4),
+            )
+
+        def quant_down(g):
+            nc.vector.quantize_mx(out=wd_codes[:, g].bitcast(FP8X4), scales=wd_scales[:, g], in_=wd_grp[:, g])
+
+        group_down(0, nc.vector.tensor_copy)
+        quant_down(0)
+        up = wu_raw[:].rearrange("p j (h f) -> p h f j", h=H)
+
+        def group_up():
+            for dst, src in (
+                (wu_main_grp[:, 0], up[:, :, 0:DH, :]),
+                (wu_main_grp[:, 1], up[:, :, DH + DR:, :]),
+                (wu_rope_grp[:], up[:, :, DH:DH + DR, :]),
+            ):
+                nc.scalar.copy(out=dst, in_=src)
+
+        def tables():
+            nc.scalar.activation(out=mag[:], in_=red2[:], func=ACT.Abs)
+            nc.scalar.activation(out=cos[:], in_=mag[:], func=ACT.Sin, scale=-1.0, bias=math.pi / 2)
+            nc.scalar.activation(out=sin[:, :, 0], in_=red2[:], func=ACT.Sin)
+            nc.scalar.activation(out=sin[:, :, 1], in_=red2[:], func=ACT.Sin, scale=-1.0)
+
+        def quant_up():
+            nc.vector.quantize_mx(out=wu_main_codes[:].bitcast(FP8X4), scales=wu_main_scales[:], in_=wu_main_grp[:].rearrange("p a h f j -> p (a h f j)"))
+            nc.vector.quantize_mx(out=wu_rope_codes[:].bitcast(FP8X4), scales=wu_rope_scales[:], in_=wu_rope_grp[:].rearrange("p h f j -> p (h f j)"))
+
+        xbf = {}
+        xt = {}
+        xg = {}
+        xc = {}
+        lat = {}
+        lg = {}
+        lc = {}
+        main = {}
+        rope = {}
+        kv = {}
+
+        def widen(s, i):
+            t = work.tile([P, D], BF16, name="xbf", bufs=8)
+            xbf[s, i] = t
+            nc.scalar.copy(out=t[:], in_=x_tiles[s // 2][:, 2 * (s % 2) + i].bitcast(FP8))
+
+        def turn(s, i):
+            bank = psum.tile([P, 2, 2, P], F32, name="xt")
+            xt[s, i] = bank
+            words = xbf[s, i][:].bitcast(F32)
+            for g in range(2):
+                for u in range(2):
+                    nc.tensor.transpose(bank[:, u, g, :], words[:, 256 * g + u:256 * (g + 1):2], ident[:])
+
+        def empty_turn(s, i):
+            if i == 0:
+                xg[s] = work.tile([P, 2, 2, P * 4], BF16, name="xg", align_bytes=64)
+            nc.vector.tensor_tensor(
+                out=xg[s][:, i].rearrange("p g (r u e) -> p g r u e", u=2, e=2),
+                in0=xt[s, i][:].bitcast(BF16).rearrange("p u g (r e) -> p g r u e", e=2),
+                in1=scale_cols[:].rearrange("p g (u e) -> p g u e", u=2).unsqueeze(2).to_broadcast([P, 2, P, 2, 2]),
+                op=ALU.mult,
+            )
+
+        def quant_x(s):
+            codes = work.tile([P, 2, 2, P], U32, name="xcodes", align_bytes=64)
+            scales = work.tile([P, 2, 2, P], U8, name="xscales", align_bytes=64)
+            xc[s] = (codes, scales)
+            nc.vector.quantize_mx(
+                out=codes[:].rearrange("p i g r -> p (i g r)").bitcast(FP8X4),
+                scales=scales[:].rearrange("p i g r -> p (i g r)"),
+                in_=xg[s][:].rearrange("p i g c -> p (i g c)"),
+            )
+
+        def down(s, i):
+            bank = psum.tile([P, 4, P], F32, name="lat")
+            lat[s, i] = bank
+            codes, scales = xc[s]
+            for t in range(4):
+                for g in range(2):
+                    nc.tensor.matmul_mx(
+                        out=bank[:, t, :],
+                        lhsT=wd_codes[:, g, t * P:(t + 1) * P].bitcast(FP8X4),
+                        lhsT_scale=wd_scales[:, g, t * P:(t + 1) * P],
+                        rhs=codes[:, i, g].bitcast(FP8X4),
+                        rhs_scale=scales[:, i, g],
+                        start=(g == 0),
+                        stop=(g == 1),
+                    )
+
+        def empty_down(s, i):
+            if i == 0:
+                lg[s] = work.tile([P, 2, P, 4], BF16, name="lg", align_bytes=64, bufs=4)
+            nc.scalar.copy(out=lg[s][:, i], in_=lat[s, i][:].rearrange("p t r -> p r t"))
+
+        def quant_lat(s):
+            codes = work.tile([P, 2, P], U32, name="lcodes", align_bytes=64)
+            scales = work.tile([P, 2, P], U8, name="lscales", align_bytes=64)
+            lc[s] = (codes, scales)
+            nc.vector.quantize_mx(
+                out=codes[:].rearrange("p i r -> p (i r)").bitcast(FP8X4),
+                scales=scales[:].rearrange("p i r -> p (i r)"),
+                in_=lg[s][:].rearrange("p i r t -> p (i r t)"),
+            )
+
+        def expand(s, i):
+            if s % 2 == 0 and i == 0:
+                rope[s // 2] = psum.tile([P, GROUP, H, 2, HALF], F32, name="rope")
+            bank = psum.tile([P, 4, DH], F32, name="main")
+            main[s, i] = bank
+            codes, scales = lc[s]
+            nc.tensor.matmul_mx(
+                out=bank[:].rearrange("p a f -> p (a f)"),
+                lhsT=codes[:, i].bitcast(FP8X4), lhsT_scale=scales[:, i],
+                rhs=wu_main_codes[:].bitcast(FP8X4), rhs_scale=wu_main_scales[:],
+                start=True, stop=True,
+            )
+            nc.tensor.matmul_mx(
+                out=rope[s // 2][:, 2 * (s % 2) + i].rearrange("p h a f -> p (h a f)"),
+                lhsT=codes[:, i].bitcast(FP8X4), lhsT_scale=scales[:, i],
+                rhs=wu_rope_codes[:].bitcast(FP8X4), rhs_scale=wu_rope_scales[:],
+                start=True, stop=True,
+            )
+
+        def empty_main(s, i):
+            if s % 2 == 0 and i == 0:
+                kv[s // 2] = outp.tile([P, GROUP, 4, DH + DR], F32, name="kv")
+            nc.scalar.copy(out=kv[s // 2][:, 2 * (s % 2) + i, :, 0:DH], in_=main[s, i][:])
+
+        rot = {}
+
+        def rope_mul(g, lo, n):
+            a = work.tile([P, n, H, 2, HALF], F32, name="rot_a", bufs=3)
+            b = work.tile([P, n, H, 2, HALF], F32, name="rot_b", bufs=3)
+            rot[g, lo] = (a, b)
+            first = (g % POS_GROUPS) * GROUP + lo
+            bank = rope[g][:, lo:lo + n]
+            nc.vector.tensor_tensor(
+                out=a[:].rearrange("p i h a f -> p i (h a) f"),
+                in0=bank.rearrange("p i h a f -> p i (h a) f"),
+                in1=cos[:, first:first + n].unsqueeze(2).to_broadcast([P, n, 2 * H, HALF]),
+                op=ALU.mult,
+            )
+            nc.vector.tensor_tensor(
+                out=b[:].rearrange("p i h a f -> p i h (a f)"),
+                in0=bank.rearrange("p i h a f -> p i h (a f)"),
+                in1=sin[:, first:first + n].rearrange("p i a f -> p i (a f)").unsqueeze(2).to_broadcast([P, n, H, DR]),
+                op=ALU.mult,
+            )
+
+        def rope_add(g, lo, n):
+            a, b = rot[g, lo]
+            nc.vector.tensor_tensor(
+                out=kv[g][:, lo:lo + n, 0:H, DH:].rearrange("p i h (a f) -> p i h a f", a=2),
+                in0=a[:], in1=b[:, :, :, ::-1, :], op=ALU.add,
+            )
+
+        def rope_add_beside(g):
+            a, b = rot[g, 0]
+            for half in range(2):
+                nc.gpsimd.tensor_tensor(
+                    out=kv[g][:, :, 0:H, DH + half * HALF:DH + (half + 1) * HALF],
+                    in0=a[:, :, :, half], in1=b[:, :, :, 1 - half], op=ALU.add,
+                )
+
+        def store_v(g):
+            for h in range(H):
+                nc.sync.dma_start(out=v_view[g][:, :, h], in_=kv[g][:, :, 2 + h, 0:DH])
+
+        def store_k(g, lo, n):
+            nc.sync.dma_start(out=k_view[g][:, lo:lo + n], in_=kv[g][:, lo:lo + n, 0:2, :].rearrange("p i h f -> p i (h f)"))
+
+        for it in range(-2, STEPS + 4):
+            wide, now, mid, lat_q, old, mul = it + 2, it, it - 1, it - 3, it - 4, it - 5
+            if it == 1:
+                quant_down(1)
+            if 0 <= now < STEPS:
+                turn(now, 0)
+            if 0 <= lat_q < STEPS:
+                quant_lat(lat_q)
+            if 0 <= old < STEPS:
+                expand(old, 0)
+                expand(old, 1)
+            if 0 <= now < STEPS:
+                turn(now, 1)
+            if 0 <= mid < STEPS:
+                quant_x(mid)
+                down(mid, 0)
+                down(mid, 1)
+            if 0 <= mul < STEPS - 1 and mul % 2:
+                rope_mul(mul // 2, 0, GROUP)
+                rope_add_beside(mul // 2)
+            if 0 <= now < STEPS:
+                empty_turn(now, 0)
+                empty_turn(now, 1)
+            if it == 2:
+                quant_up()
+            if 0 <= old < STEPS:
+                empty_main(old, 0)
+                empty_main(old, 1)
+                if old % 2:
+                    store_v(old // 2)
+            if wide < STEPS:
+                widen(wide, 0)
+            if 0 <= mid < STEPS:
+                empty_down(mid, 0)
+                empty_down(mid, 1)
+            if wide < STEPS:
+                widen(wide, 1)
+            if it == -2:
+                group_down(1, nc.scalar.copy)
+            if it == 0:
+                group_up()
+            if it == 3:
+                tables()
+            if 0 <= mul < STEPS - 1 and mul % 2:
+                store_k(mul // 2, 0, GROUP)
+        last = N_GROUPS - 1
+        rope_mul(last, 0, 2)
+        rope_mul(last, 2, 2)
+        for lo in (0, 2):
+            rope_add(last, lo, 2)
+            store_k(last, lo, 2)

@@ -24,76 +24,86 @@ HALF = DR // 2
 N_GROUPS = B * S // (P * GROUP)
 POS_GROUPS = S // (P * GROUP)
 STEPS = N_GROUPS * 2
-TURN = 0.15915496
-C1 = 6.28125
-C2 = 2 * math.pi - C1
+AHEAD = 5
 
 
 def tile_multilatentattention_pa_t_kernel(tc, x_bytes, x_scale, w_down, w_up, out_k, out_v):
     nc = tc.nc
     x_view = x_bytes.rearrange("b (g q i) d -> (b g) q i d", q=P, i=GROUP)
     k_view = out_k.rearrange("b (g q i) h f -> (b g) q i (h f)", q=P, i=GROUP)
-    v_view = out_v.rearrange("b (g q i) h f -> (b g) q i h f", q=P, i=GROUP)
+    v_view = out_v.rearrange("b (g q i) h f -> (b g) q (i h) f", q=P, i=GROUP)
     wd_view = w_down.rearrange("(g p j) c -> g p j c", p=P, j=4)
 
     with ExitStack() as ctx:
         const = ctx.enter_context(tc.tile_pool(name="const", bufs=1))
         xin = ctx.enter_context(tc.tile_pool(name="xin", bufs=N_GROUPS))
         work = ctx.enter_context(tc.tile_pool(name="work", bufs=3))
-        outp = ctx.enter_context(tc.tile_pool(name="outp", bufs=3))
+        outp = ctx.enter_context(tc.tile_pool(name="outp", bufs=6))
         psum = ctx.enter_context(tc.psum_pool(name="psum", bufs=2))
         ctx.enter_context(tc.manual_schedule())
 
-        wd_raw = const.tile([P, 2, 4, DL], BF16)
+        wd_raw = [const.tile([P, 4, DL], BF16, name="wd_raw%d" % g) for g in range(2)]
         wu_raw = const.tile([P, 4, N_UP], BF16)
-        x_tiles = []
-        for g in range(N_GROUPS):
-            xb = xin.tile([P, GROUP, D], U8, name="xb")
-            x_tiles.append(xb)
+        x_tiles = [xin.tile([P, GROUP, D], U8, name="xb") for g in range(N_GROUPS)]
         scale_cols = const.tile([P, 2, 4], F32)
+        nc.sync.dma_start(out=x_tiles[0][:, 0:1], in_=x_view[0][:, 0:1])
         nc.sync.dma_start(out=scale_cols[:], in_=x_scale.rearrange("a b (g p t) -> p (a b g) t", p=P, t=4))
-        nc.sync.dma_start(out=x_tiles[0][:, 0:2], in_=x_view[0][:, 0:2])
-        nc.sync.dma_start(out=wd_raw[:, 0], in_=wd_view[0])
-        nc.sync.dma_start(out=wd_raw[:, 1], in_=wd_view[1])
+        nc.sync.dma_start(out=x_tiles[0][:, 1:2], in_=x_view[0][:, 1:2])
         nc.sync.dma_start(out=x_tiles[0][:, 2:4], in_=x_view[0][:, 2:4])
-        nc.sync.dma_start(out=wu_raw[:], in_=w_up.rearrange("(p j) n -> p j n", j=4))
+        nc.sync.dma_start(out=wd_raw[0][:], in_=wd_view[0])
         nc.sync.dma_start(out=x_tiles[1][:], in_=x_view[1])
-        for g in range(2, N_GROUPS):
+        nc.sync.dma_start(out=wd_raw[1][:], in_=wd_view[1])
+        nc.sync.dma_start(out=x_tiles[2][:], in_=x_view[2])
+        nc.sync.dma_start(out=wu_raw[:], in_=w_up.rearrange("(p j) n -> p j n", j=4))
+        for g in range(3, N_GROUPS):
             nc.sync.dma_start(out=x_tiles[g][:], in_=x_view[g])
 
         warm = const.tile([P, 1], F32)
         nc.vector.memset(warm[:], 0.0)
         nc.scalar.activation(out=warm[:], in_=warm[:], func=ACT.Sin)
+        ident = const.tile([P, P], F32)
         pos = const.tile([P, POS_GROUPS, GROUP], F32)
         nc.gpsimd.iota(pos[:], pattern=[[P * GROUP, POS_GROUPS], [1, GROUP]], base=0, channel_multiplier=GROUP, allow_small_or_imprecise_dtypes=True)
-        ident = const.tile([P, P], F32)
         make_identity(nc, ident[:])
-        freq = const.tile([P, HALF], F32)
-        nc.vector.memset(freq[:], 1.0)
-        for b in range(5):
-            f = freq[:].rearrange("p (x y z) -> p x y z", y=2, z=2 ** b)[:, :, 1, :]
-            nc.vector.tensor_scalar(out=f, in0=f, scalar1=10000.0 ** (-(2 ** b) / HALF), scalar2=None, op0=ALU.mult)
-        shape = [P, POS_GROUPS * GROUP, HALF]
-        ang = const.tile(shape, F32)
-        turns = const.tile(shape, I32)
-        turns_f = const.tile(shape, F32)
-        red = const.tile(shape, F32)
-        red2 = const.tile(shape, F32)
-        mag = const.tile(shape, F32)
-        sin = const.tile([P, POS_GROUPS * GROUP, 2, HALF], F32)
-        cos = const.tile(shape, F32)
-        nc.vector.tensor_tensor(
-            out=ang[:],
-            in0=pos[:].rearrange("p a b -> p (a b)").unsqueeze(2).to_broadcast(shape),
-            in1=freq[:].unsqueeze(1).to_broadcast(shape),
-            op=ALU.mult,
-        )
-        nc.vector.tensor_scalar(out=turns[:], in0=ang[:], scalar1=TURN, scalar2=None, op0=ALU.mult)
-        nc.vector.tensor_copy(out=turns_f[:], in_=turns[:])
-        nc.vector.scalar_tensor_tensor(out=red[:], in0=turns_f[:], scalar=-C1, in1=ang[:], op0=ALU.mult, op1=ALU.add)
-        nc.vector.scalar_tensor_tensor(out=red2[:], in0=turns_f[:], scalar=-C2, in1=red[:], op0=ALU.mult, op1=ALU.add)
+        ones = const.tile([P, 1], F32)
+        nc.vector.memset(ones[:], 1.0)
+        freq = const.tile([P, HALF // 4, 4], F32)
+        for a in range(4):
+            nc.vector.tensor_scalar(out=freq[:, 0, a:a + 1], in0=ones[:], scalar1=10000.0 ** (-a / HALF) / (2 * math.pi), scalar2=None, op0=ALU.mult)
+        for b in range(1, HALF // 4):
+            nc.vector.tensor_scalar(out=freq[:, b], in0=freq[:, 0], scalar1=10000.0 ** (-4 * b / HALF), scalar2=None, op0=ALU.mult)
+        n_pos = POS_GROUPS * GROUP
+        turns = const.tile([P, n_pos, HALF], F32)
+        whole = const.tile([P, n_pos, HALF], I32)
+        frac = const.tile([P, n_pos, HALF], F32)
+        mag = const.tile([P, 2, n_pos, HALF], F32)
+        trig = const.tile([P, n_pos, 3, HALF], F32)
+        halves = [slice(0, n_pos // 2), slice(n_pos // 2, n_pos)]
+        shape = [P, n_pos // 2, HALF]
+        for h in halves:
+            nc.vector.tensor_tensor(
+                out=turns[:, h],
+                in0=pos[:].rearrange("p a b -> p (a b)")[:, h].unsqueeze(2).to_broadcast(shape),
+                in1=freq[:].rearrange("p a b -> p (a b)").unsqueeze(1).to_broadcast(shape),
+                op=ALU.mult,
+            )
+        for h in halves:
+            nc.vector.tensor_scalar(out=whole[:, h], in0=turns[:, h], scalar1=-0.125, scalar2=None, op0=ALU.add)
+        for h in halves:
+            nc.vector.tensor_tensor(out=frac[:, h], in0=turns[:, h], in1=whole[:, h], op=ALU.subtract)
 
-        wd_grp = const.tile([P, 2, DL * 4], BF16, align_bytes=64)
+        def table_args():
+            nc.scalar.activation(out=mag[:, 0], in_=frac[:], func=ACT.Abs, scale=2 * math.pi)
+            nc.scalar.activation(out=mag[:, 1], in_=frac[:], func=ACT.Abs, scale=2 * math.pi, bias=-math.pi / 2)
+
+        def table_cos():
+            nc.scalar.activation(out=trig[:, :, 0], in_=mag[:, 0], func=ACT.Sin, scale=-1.0, bias=math.pi / 2)
+
+        def table_sin():
+            nc.scalar.activation(out=trig[:, :, 1], in_=mag[:, 1], func=ACT.Sin, scale=1.0, bias=-math.pi / 2)
+            nc.scalar.activation(out=trig[:, :, 2], in_=mag[:, 1], func=ACT.Sin, scale=-1.0, bias=math.pi / 2)
+
+        wd_grp = [const.tile([P, DL * 4], BF16, align_bytes=64, name="wd_grp%d" % g) for g in range(2)]
         wd_codes = const.tile([P, 2, DL], U32, align_bytes=64)
         wd_scales = const.tile([P, 2, DL], U8, align_bytes=64)
         wu_main_grp = const.tile([P, 2, H, DH, 4], BF16, align_bytes=64)
@@ -103,32 +113,27 @@ def tile_multilatentattention_pa_t_kernel(tc, x_bytes, x_scale, w_down, w_up, ou
         wu_rope_codes = const.tile([P, H * DR], U32, align_bytes=64)
         wu_rope_scales = const.tile([P, H * DR], U8, align_bytes=64)
 
+        def pool_copy(out, in_):
+            nc.gpsimd.tensor_scalar(out=out, in0=in_, scalar1=1.0, scalar2=0.0, op0=ALU.mult, op1=ALU.add)
+
         def group_down(g, copy):
             copy(
-                out=wd_grp[:, g].rearrange("p (t m j) -> p t m j", t=4, j=4),
-                in_=wd_raw[:, g].rearrange("p j (m t) -> p t m j", t=4),
+                out=wd_grp[g][:].rearrange("p (t m j) -> p t m j", t=4, j=4),
+                in_=wd_raw[g][:].rearrange("p j (m t) -> p t m j", t=4),
             )
 
         def quant_down(g):
-            nc.vector.quantize_mx(out=wd_codes[:, g].bitcast(FP8X4), scales=wd_scales[:, g], in_=wd_grp[:, g])
+            nc.vector.quantize_mx(out=wd_codes[:, g].bitcast(FP8X4), scales=wd_scales[:, g], in_=wd_grp[g][:])
 
-        group_down(0, nc.vector.tensor_copy)
-        quant_down(0)
         up = wu_raw[:].rearrange("p j (h f) -> p h f j", h=H)
 
-        def group_up():
+        def group_up(copy):
             for dst, src in (
                 (wu_main_grp[:, 0], up[:, :, 0:DH, :]),
                 (wu_main_grp[:, 1], up[:, :, DH + DR:, :]),
                 (wu_rope_grp[:], up[:, :, DH:DH + DR, :]),
             ):
-                nc.scalar.copy(out=dst, in_=src)
-
-        def tables():
-            nc.scalar.activation(out=mag[:], in_=red2[:], func=ACT.Abs)
-            nc.scalar.activation(out=cos[:], in_=mag[:], func=ACT.Sin, scale=-1.0, bias=math.pi / 2)
-            nc.scalar.activation(out=sin[:, :, 0], in_=red2[:], func=ACT.Sin)
-            nc.scalar.activation(out=sin[:, :, 1], in_=red2[:], func=ACT.Sin, scale=-1.0)
+                copy(out=dst, in_=src)
 
         def quant_up():
             nc.vector.quantize_mx(out=wu_main_codes[:].bitcast(FP8X4), scales=wu_main_scales[:], in_=wu_main_grp[:].rearrange("p a h f j -> p (a h f j)"))
@@ -144,23 +149,28 @@ def tile_multilatentattention_pa_t_kernel(tc, x_bytes, x_scale, w_down, w_up, ou
         main = {}
         rope = {}
         kv = {}
+        rot = {}
 
-        def widen(s, i):
-            t = work.tile([P, D], BF16, name="xbf", bufs=8)
-            xbf[s, i] = t
-            nc.scalar.copy(out=t[:], in_=x_tiles[s // 2][:, 2 * (s % 2) + i].bitcast(FP8))
+        def widen(s, lo, n):
+            if lo == 0:
+                xbf[s] = work.tile([P, 2, D], BF16, name="xbf", bufs=4)
+            first = 2 * (s % 2) + lo
+            nc.scalar.copy(
+                out=xbf[s][:, lo:lo + n].rearrange("p i d -> p (i d)"),
+                in_=x_tiles[s // 2][:, first:first + n].rearrange("p i d -> p (i d)").bitcast(FP8),
+            )
 
         def turn(s, i):
-            bank = psum.tile([P, 2, 2, P], F32, name="xt")
+            bank = psum.tile([P, 2, 2, P], F32, name="xt", bufs=3)
             xt[s, i] = bank
-            words = xbf[s, i][:].bitcast(F32)
+            words = xbf[s][:, i].bitcast(F32)
             for g in range(2):
                 for u in range(2):
                     nc.tensor.transpose(bank[:, u, g, :], words[:, 256 * g + u:256 * (g + 1):2], ident[:])
 
         def empty_turn(s, i):
             if i == 0:
-                xg[s] = work.tile([P, 2, 2, P * 4], BF16, name="xg", align_bytes=64)
+                xg[s] = work.tile([P, 2, 2, P * 4], BF16, name="xg", align_bytes=64, bufs=4)
             nc.vector.tensor_tensor(
                 out=xg[s][:, i].rearrange("p g (r u e) -> p g r u e", u=2, e=2),
                 in0=xt[s, i][:].bitcast(BF16).rearrange("p u g (r e) -> p g r u e", e=2),
@@ -168,14 +178,16 @@ def tile_multilatentattention_pa_t_kernel(tc, x_bytes, x_scale, w_down, w_up, ou
                 op=ALU.mult,
             )
 
-        def quant_x(s):
-            codes = work.tile([P, 2, 2, P], U32, name="xcodes", align_bytes=64)
-            scales = work.tile([P, 2, 2, P], U8, name="xscales", align_bytes=64)
-            xc[s] = (codes, scales)
+        def quant_x(s, lo, n):
+            if lo == 0:
+                codes = work.tile([P, 2, 2, P], U32, name="xcodes", align_bytes=64, bufs=4)
+                scales = work.tile([P, 2, 2, P], U8, name="xscales", align_bytes=64, bufs=4)
+                xc[s] = (codes, scales)
+            codes, scales = xc[s]
             nc.vector.quantize_mx(
-                out=codes[:].rearrange("p i g r -> p (i g r)").bitcast(FP8X4),
-                scales=scales[:].rearrange("p i g r -> p (i g r)"),
-                in_=xg[s][:].rearrange("p i g c -> p (i g c)"),
+                out=codes[:, lo:lo + n].rearrange("p i g r -> p (i g r)").bitcast(FP8X4),
+                scales=scales[:, lo:lo + n].rearrange("p i g r -> p (i g r)"),
+                in_=xg[s][:, lo:lo + n].rearrange("p i g c -> p (i g c)"),
             )
 
         def down(s, i):
@@ -199,131 +211,208 @@ def tile_multilatentattention_pa_t_kernel(tc, x_bytes, x_scale, w_down, w_up, ou
                 lg[s] = work.tile([P, 2, P, 4], BF16, name="lg", align_bytes=64, bufs=4)
             nc.scalar.copy(out=lg[s][:, i], in_=lat[s, i][:].rearrange("p t r -> p r t"))
 
-        def quant_lat(s):
-            codes = work.tile([P, 2, P], U32, name="lcodes", align_bytes=64)
-            scales = work.tile([P, 2, P], U8, name="lscales", align_bytes=64)
-            lc[s] = (codes, scales)
+        def quant_lat(s, lo, n):
+            if lo == 0:
+                codes = work.tile([P, 2, P], U32, name="lcodes", align_bytes=64, bufs=4)
+                scales = work.tile([P, 2, P], U8, name="lscales", align_bytes=64, bufs=4)
+                lc[s] = (codes, scales)
+            codes, scales = lc[s]
             nc.vector.quantize_mx(
-                out=codes[:].rearrange("p i r -> p (i r)").bitcast(FP8X4),
-                scales=scales[:].rearrange("p i r -> p (i r)"),
-                in_=lg[s][:].rearrange("p i r t -> p (i r t)"),
+                out=codes[:, lo:lo + n].rearrange("p i r -> p (i r)").bitcast(FP8X4),
+                scales=scales[:, lo:lo + n].rearrange("p i r -> p (i r)"),
+                in_=lg[s][:, lo:lo + n].rearrange("p i r t -> p (i r t)"),
             )
 
-        def expand(s, i):
-            if s % 2 == 0 and i == 0:
-                rope[s // 2] = psum.tile([P, GROUP, H, 2, HALF], F32, name="rope")
-            bank = psum.tile([P, 4, DH], F32, name="main")
-            main[s, i] = bank
+        def expand(out, s, i, w_codes, w_scales):
             codes, scales = lc[s]
             nc.tensor.matmul_mx(
-                out=bank[:].rearrange("p a f -> p (a f)"),
+                out=out,
                 lhsT=codes[:, i].bitcast(FP8X4), lhsT_scale=scales[:, i],
-                rhs=wu_main_codes[:].bitcast(FP8X4), rhs_scale=wu_main_scales[:],
+                rhs=w_codes[:].bitcast(FP8X4), rhs_scale=w_scales[:],
                 start=True, stop=True,
             )
-            nc.tensor.matmul_mx(
-                out=rope[s // 2][:, 2 * (s % 2) + i].rearrange("p h a f -> p (h a f)"),
-                lhsT=codes[:, i].bitcast(FP8X4), lhsT_scale=scales[:, i],
-                rhs=wu_rope_codes[:].bitcast(FP8X4), rhs_scale=wu_rope_scales[:],
-                start=True, stop=True,
-            )
+
+        def expand_main(s, i, tag="main", bufs=2):
+            main[s, i] = psum.tile([P, 4, DH], F32, name=tag, bufs=bufs)
+            expand(main[s, i][:].rearrange("p a f -> p (a f)"), s, i, wu_main_codes, wu_main_scales)
+
+        def expand_rope(s, i, tag="rope", bufs=1):
+            if i == 0:
+                kv[s] = outp.tile([P, 2, 2, H, DH + DR], F32, name="kv")
+                rope[s] = psum.tile([P, 2, H, 2, HALF], F32, name=tag, bufs=bufs)
+            expand(rope[s][:, i].rearrange("p h a f -> p (h a f)"), s, i, wu_rope_codes, wu_rope_scales)
 
         def empty_main(s, i):
-            if s % 2 == 0 and i == 0:
-                kv[s // 2] = outp.tile([P, GROUP, 4, DH + DR], F32, name="kv")
-            nc.scalar.copy(out=kv[s // 2][:, 2 * (s % 2) + i, :, 0:DH], in_=main[s, i][:])
+            nc.scalar.copy(out=kv[s][:, :, i, :, 0:DH], in_=main[s, i][:].rearrange("p (a h) f -> p a h f", h=H))
 
-        rot = {}
-
-        def rope_mul(g, lo, n):
-            a = work.tile([P, n, H, 2, HALF], F32, name="rot_a", bufs=3)
-            b = work.tile([P, n, H, 2, HALF], F32, name="rot_b", bufs=3)
-            rot[g, lo] = (a, b)
-            first = (g % POS_GROUPS) * GROUP + lo
-            bank = rope[g][:, lo:lo + n]
+        def rope_mul(s, lo, n):
+            prod = work.tile([P, 2, n, H, 2, HALF], F32, name="prod", bufs=3)
+            rot[s, lo] = prod
+            first = (2 * s) % n_pos + lo
+            bank = rope[s][:, lo:lo + n]
             nc.vector.tensor_tensor(
-                out=a[:].rearrange("p i h a f -> p i (h a) f"),
+                out=prod[:, 0].rearrange("p i h a f -> p i (h a) f"),
                 in0=bank.rearrange("p i h a f -> p i (h a) f"),
-                in1=cos[:, first:first + n].unsqueeze(2).to_broadcast([P, n, 2 * H, HALF]),
+                in1=trig[:, first:first + n, 0].unsqueeze(2).to_broadcast([P, n, 2 * H, HALF]),
                 op=ALU.mult,
             )
             nc.vector.tensor_tensor(
-                out=b[:].rearrange("p i h a f -> p i h (a f)"),
-                in0=bank.rearrange("p i h a f -> p i h (a f)"),
-                in1=sin[:, first:first + n].rearrange("p i a f -> p i (a f)").unsqueeze(2).to_broadcast([P, n, H, DR]),
+                out=prod[:, 1],
+                in0=bank[:, :, :, ::-1, :],
+                in1=trig[:, first:first + n, 1:3].unsqueeze(2).to_broadcast([P, n, H, 2, HALF]),
                 op=ALU.mult,
             )
 
-        def rope_add(g, lo, n):
-            a, b = rot[g, lo]
-            nc.vector.tensor_tensor(
-                out=kv[g][:, lo:lo + n, 0:H, DH:].rearrange("p i h (a f) -> p i h a f", a=2),
-                in0=a[:], in1=b[:, :, :, ::-1, :], op=ALU.add,
+        def rope_add(s, lo, n, engine):
+            prod = rot[s, lo]
+            engine.tensor_tensor(
+                out=kv[s][:, 0, lo:lo + n, :, DH:],
+                in0=prod[:, 0].rearrange("p i h a f -> p i h (a f)"),
+                in1=prod[:, 1].rearrange("p i h a f -> p i h (a f)"),
+                op=ALU.add,
             )
 
-        def rope_add_beside(g):
-            a, b = rot[g, 0]
-            for half in range(2):
-                nc.gpsimd.tensor_tensor(
-                    out=kv[g][:, :, 0:H, DH + half * HALF:DH + (half + 1) * HALF],
-                    in0=a[:, :, :, half], in1=b[:, :, :, 1 - half], op=ALU.add,
-                )
+        def store_v(s, lo, n):
+            first = 2 * (s % 2) + lo
+            nc.sync.dma_start(out=v_view[s // 2][:, H * first:H * (first + n)], in_=kv[s][:, 1, lo:lo + n, :, 0:DH].rearrange("p i h f -> p (i h) f"))
 
-        def store_v(g):
-            for h in range(H):
-                nc.sync.dma_start(out=v_view[g][:, :, h], in_=kv[g][:, :, 2 + h, 0:DH])
+        def store_k(s, lo, n):
+            first = 2 * (s % 2) + lo
+            nc.sync.dma_start(out=k_view[s // 2][:, first:first + n], in_=kv[s][:, 0, lo:lo + n].rearrange("p i h f -> p i (h f)"))
 
-        def store_k(g, lo, n):
-            nc.sync.dma_start(out=k_view[g][:, lo:lo + n], in_=kv[g][:, lo:lo + n, 0:2, :].rearrange("p i h f -> p i (h f)"))
-
-        for it in range(-2, STEPS + 4):
-            wide, now, mid, lat_q, old, mul = it + 2, it, it - 1, it - 3, it - 4, it - 5
-            if it == 1:
-                quant_down(1)
-            if 0 <= now < STEPS:
-                turn(now, 0)
-            if 0 <= lat_q < STEPS:
-                quant_lat(lat_q)
-            if 0 <= old < STEPS:
-                expand(old, 0)
-                expand(old, 1)
-            if 0 <= now < STEPS:
-                turn(now, 1)
-            if 0 <= mid < STEPS:
-                quant_x(mid)
-                down(mid, 0)
-                down(mid, 1)
-            if 0 <= mul < STEPS - 1 and mul % 2:
-                rope_mul(mul // 2, 0, GROUP)
-                rope_add_beside(mul // 2)
-            if 0 <= now < STEPS:
-                empty_turn(now, 0)
-                empty_turn(now, 1)
-            if it == 2:
-                quant_up()
-            if 0 <= old < STEPS:
-                empty_main(old, 0)
-                empty_main(old, 1)
-                if old % 2:
-                    store_v(old // 2)
+        widen(0, 0, 1)
+        widen(0, 1, 1)
+        group_down(0, pool_copy)
+        group_down(1, pool_copy)
+        widen(1, 0, 2)
+        table_args()
+        widen(2, 0, 2)
+        table_cos()
+        table_sin()
+        widen(3, 0, 2)
+        group_up(nc.scalar.copy)
+        turn(0, 0)
+        turn(0, 1)
+        for s in range(2):
+            for i in range(2):
+                empty_turn(s, i)
+                turn(s + 1, i)
+        empty_turn(2, 0)
+        turn(3, 0)
+        quant_down(0)
+        quant_x(0, 0, 2)
+        quant_down(1)
+        quant_x(1, 0, 2)
+        empty_turn(2, 1)
+        down(0, 0)
+        down(0, 1)
+        turn(3, 1)
+        quant_up()
+        quant_x(2, 0, 2)
+        widen(4, 0, 2)
+        empty_down(0, 0)
+        empty_down(0, 1)
+        down(1, 0)
+        down(1, 1)
+        empty_down(1, 0)
+        empty_down(1, 1)
+        empty_turn(3, 0)
+        quant_lat(0, 0, 2)
+        empty_turn(3, 1)
+        down(2, 0)
+        down(2, 1)
+        expand_rope(0, 0)
+        expand_rope(0, 1)
+        expand_main(0, 0)
+        expand_main(0, 1)
+        turn(4, 0)
+        turn(4, 1)
+        empty_down(2, 0)
+        empty_down(2, 1)
+        empty_main(0, 0)
+        empty_main(0, 1)
+        store_v(0, 0, 2)
+        widen(5, 0, 2)
+        quant_lat(1, 0, 2)
+        quant_x(3, 0, 2)
+        quant_lat(2, 0, 2)
+        rope_mul(0, 0, 2)
+        rope_add(0, 0, 2, nc.gpsimd)
+        store_k(0, 0, 2)
+        expand_rope(1, 0)
+        expand_rope(1, 1)
+        expand_main(1, 0)
+        expand_main(1, 1)
+        empty_main(1, 0)
+        empty_main(1, 1)
+        store_v(1, 0, 2)
+        last = STEPS - 1
+        for it in range(4, last):
+            nxt, wide, mid, old = it + 1, it + 2, it - 1, it - 2
+            empty_turn(it, 0)
+            if it == 4:
+                rope_mul(1, 0, 2)
+                rope_add(1, 0, 2, nc.gpsimd)
+                store_k(1, 0, 2)
+            empty_turn(it, 1)
+            down(mid, 0)
+            down(mid, 1)
+            empty_down(mid, 0)
+            empty_down(mid, 1)
+            expand_main(old, 0)
+            expand_rope(old, 0)
+            expand_rope(old, 1)
+            empty_main(old, 0)
+            turn(nxt, 0)
+            turn(nxt, 1)
+            expand_main(old, 1)
             if wide < STEPS:
-                widen(wide, 0)
-            if 0 <= mid < STEPS:
-                empty_down(mid, 0)
-                empty_down(mid, 1)
-            if wide < STEPS:
-                widen(wide, 1)
-            if it == -2:
-                group_down(1, nc.scalar.copy)
-            if it == 0:
-                group_up()
-            if it == 3:
-                tables()
-            if 0 <= mul < STEPS - 1 and mul % 2:
-                store_k(mul // 2, 0, GROUP)
-        last = N_GROUPS - 1
+                widen(wide, 0, 2)
+            empty_main(old, 1)
+            store_v(old, 0, 2)
+            quant_lat(mid, 0, 2)
+            quant_x(it, 0, 2)
+            rope_mul(old, 0, 2)
+            rope_add(old, 0, 2, nc.gpsimd)
+            store_k(old, 0, 2)
+        empty_turn(last, 0)
+        down(last - 1, 0)
+        down(last - 1, 1)
+        empty_down(last - 1, 0)
+        empty_down(last - 1, 1)
+        for i in range(2):
+            expand_rope(last - 2, i)
+            expand_main(last - 2, i)
+            empty_main(last - 2, i)
+        store_v(last - 2, 0, 2)
+        empty_turn(last, 1)
+        quant_x(last, 0, 1)
+        quant_lat(last - 1, 0, 2)
+        quant_x(last, 1, 1)
+        rope_mul(last - 2, 0, 2)
+        rope_add(last - 2, 0, 2, nc.vector)
+        store_k(last - 2, 0, 2)
+        down(last, 0)
+        for i in range(2):
+            expand_main(last - 1, i)
+        down(last, 1)
+        for i in range(2):
+            expand_rope(last - 1, i)
+        empty_down(last, 0)
+        empty_main(last - 1, 0)
+        empty_down(last, 1)
+        empty_main(last - 1, 1)
+        store_v(last - 1, 0, 2)
+        quant_lat(last, 0, 1)
+        rope_mul(last - 1, 0, 2)
+        quant_lat(last, 1, 1)
+        rope_add(last - 1, 0, 2, nc.vector)
+        store_k(last - 1, 0, 2)
+        for i in range(2):
+            expand_rope(last, i, "xt", 3)
+            expand_main(last, i, "xt", 3)
+            empty_main(last, i)
+            store_v(last, i, 1)
         rope_mul(last, 0, 2)
-        rope_mul(last, 2, 2)
-        for lo in (0, 2):
-            rope_add(last, lo, 2)
-            store_k(last, lo, 2)
+        rope_add(last, 0, 2, nc.vector)
+        store_k(last, 0, 2)

@@ -2,7 +2,6 @@ import math
 from contextlib import ExitStack
 
 import concourse.mybir as mybir
-from concourse.masks import make_identity
 
 F32 = mybir.dt.float32
 BF16 = mybir.dt.bfloat16
@@ -24,7 +23,6 @@ HALF = DR // 2
 N_GROUPS = B * S // (P * GROUP)
 POS_GROUPS = S // (P * GROUP)
 STEPS = N_GROUPS * 2
-AHEAD = 5
 
 
 def tile_multilatentattention_pa_t_kernel(tc, x_bytes, x_scale, w_down, w_up, out_k, out_v):
@@ -61,32 +59,31 @@ def tile_multilatentattention_pa_t_kernel(tc, x_bytes, x_scale, w_down, w_up, ou
         warm = const.tile([P, 1], F32)
         nc.vector.memset(warm[:], 0.0)
         nc.scalar.activation(out=warm[:], in_=warm[:], func=ACT.Sin)
-        ident = const.tile([P, P], F32)
+        n_pos = POS_GROUPS * GROUP
         pos = const.tile([P, POS_GROUPS, GROUP], F32)
         nc.gpsimd.iota(pos[:], pattern=[[P * GROUP, POS_GROUPS], [1, GROUP]], base=0, channel_multiplier=GROUP, allow_small_or_imprecise_dtypes=True)
-        make_identity(nc, ident[:])
-        ones = const.tile([P, 1], F32)
-        nc.vector.memset(ones[:], 1.0)
-        freq = const.tile([P, HALF // 4, 4], F32)
+        offset = const.tile([P, P], F32)
+        nc.gpsimd.iota(offset[:], pattern=[[1, P]], base=0, channel_multiplier=-1, allow_small_or_imprecise_dtypes=True)
+        low = const.tile([P, 4, n_pos], F32)
         for a in range(4):
-            nc.vector.tensor_scalar(out=freq[:, 0, a:a + 1], in0=ones[:], scalar1=10000.0 ** (-a / HALF) / (2 * math.pi), scalar2=None, op0=ALU.mult)
-        for b in range(1, HALF // 4):
-            nc.vector.tensor_scalar(out=freq[:, b], in0=freq[:, 0], scalar1=10000.0 ** (-4 * b / HALF), scalar2=None, op0=ALU.mult)
-        n_pos = POS_GROUPS * GROUP
-        turns = const.tile([P, n_pos, HALF], F32)
-        whole = const.tile([P, n_pos, HALF], I32)
-        frac = const.tile([P, n_pos, HALF], F32)
-        mag = const.tile([P, 2, n_pos, HALF], F32)
-        trig = const.tile([P, n_pos, 3, HALF], F32)
-        halves = [slice(0, n_pos // 2), slice(n_pos // 2, n_pos)]
-        shape = [P, n_pos // 2, HALF]
-        for h in halves:
-            nc.vector.tensor_tensor(
-                out=turns[:, h],
-                in0=pos[:].rearrange("p a b -> p (a b)")[:, h].unsqueeze(2).to_broadcast(shape),
-                in1=freq[:].rearrange("p a b -> p (a b)").unsqueeze(1).to_broadcast(shape),
-                op=ALU.mult,
+            nc.vector.tensor_scalar(
+                out=low[:, a], in0=pos[:].rearrange("p a b -> p (a b)"),
+                scalar1=10000.0 ** (-a / HALF) / (2 * math.pi), scalar2=None, op0=ALU.mult,
             )
+        ident = const.tile([P, P], F32)
+        nc.vector.tensor_scalar(out=ident[:], in0=offset[:], scalar1=0.0, scalar2=None, op0=ALU.is_equal)
+        shape = [P, HALF // 4, n_pos, 4]
+        turns = const.tile(shape, F32)
+        for b in range(HALF // 4):
+            nc.vector.tensor_scalar(
+                out=turns[:, b], in0=low[:].rearrange("p a n -> p n a"),
+                scalar1=10000.0 ** (-4 * b / HALF), scalar2=None, op0=ALU.mult,
+            )
+        whole = const.tile(shape, I32, name="whole_then_wd", align_bytes=64)
+        frac = const.tile(shape, F32)
+        mag = const.tile([P, 2] + shape[1:], F32)
+        trig = const.tile([P, n_pos, 3, HALF], F32)
+        halves = [slice(0, HALF // 8), slice(HALF // 8, HALF // 4)]
         for h in halves:
             nc.vector.tensor_scalar(out=whole[:, h], in0=turns[:, h], scalar1=-0.125, scalar2=None, op0=ALU.add)
         for h in halves:
@@ -96,14 +93,21 @@ def tile_multilatentattention_pa_t_kernel(tc, x_bytes, x_scale, w_down, w_up, ou
             nc.scalar.activation(out=mag[:, 0], in_=frac[:], func=ACT.Abs, scale=2 * math.pi)
             nc.scalar.activation(out=mag[:, 1], in_=frac[:], func=ACT.Abs, scale=2 * math.pi, bias=-math.pi / 2)
 
+        def table(c, arg, sign):
+            nc.scalar.activation(
+                out=trig[:, :, c].rearrange("p n (b a) -> p n b a", a=4),
+                in_=mag[:, arg].rearrange("p b n a -> p n b a"),
+                func=ACT.Sin, scale=-sign, bias=sign * math.pi / 2,
+            )
+
         def table_cos():
-            nc.scalar.activation(out=trig[:, :, 0], in_=mag[:, 0], func=ACT.Sin, scale=-1.0, bias=math.pi / 2)
+            table(0, 0, 1.0)
 
         def table_sin():
-            nc.scalar.activation(out=trig[:, :, 1], in_=mag[:, 1], func=ACT.Sin, scale=1.0, bias=-math.pi / 2)
-            nc.scalar.activation(out=trig[:, :, 2], in_=mag[:, 1], func=ACT.Sin, scale=-1.0, bias=math.pi / 2)
+            table(1, 1, -1.0)
+            table(2, 1, 1.0)
 
-        wd_grp = [const.tile([P, DL * 4], BF16, align_bytes=64, name="wd_grp%d" % g) for g in range(2)]
+        wd_grp = [const.tile([P, DL * 4], BF16, align_bytes=64, name=name) for name in ("whole_then_wd", "wd_grp1")]
         wd_codes = const.tile([P, 2, DL], U32, align_bytes=64)
         wd_scales = const.tile([P, 2, DL], U8, align_bytes=64)
         wu_main_grp = const.tile([P, 2, H, DH, 4], BF16, align_bytes=64)
@@ -153,7 +157,7 @@ def tile_multilatentattention_pa_t_kernel(tc, x_bytes, x_scale, w_down, w_up, ou
 
         def widen(s, lo, n):
             if lo == 0:
-                xbf[s] = work.tile([P, 2, D], BF16, name="xbf", bufs=4)
+                xbf[s] = work.tile([P, 2, D], BF16, name="xbf", bufs=6)
             first = 2 * (s % 2) + lo
             nc.scalar.copy(
                 out=xbf[s][:, lo:lo + n].rearrange("p i d -> p (i d)"),
@@ -170,7 +174,7 @@ def tile_multilatentattention_pa_t_kernel(tc, x_bytes, x_scale, w_down, w_up, ou
 
         def empty_turn(s, i):
             if i == 0:
-                xg[s] = work.tile([P, 2, 2, P * 4], BF16, name="xg", align_bytes=64, bufs=4)
+                xg[s] = work.tile([P, 2, 2, P * 4], BF16, name="xg", align_bytes=64, bufs=5)
             nc.vector.tensor_tensor(
                 out=xg[s][:, i].rearrange("p g (r u e) -> p g r u e", u=2, e=2),
                 in0=xt[s, i][:].bitcast(BF16).rearrange("p u g (r e) -> p g r u e", e=2),
@@ -180,8 +184,8 @@ def tile_multilatentattention_pa_t_kernel(tc, x_bytes, x_scale, w_down, w_up, ou
 
         def quant_x(s, lo, n):
             if lo == 0:
-                codes = work.tile([P, 2, 2, P], U32, name="xcodes", align_bytes=64, bufs=4)
-                scales = work.tile([P, 2, 2, P], U8, name="xscales", align_bytes=64, bufs=4)
+                codes = work.tile([P, 2, 2, P], U32, name="xcodes", align_bytes=64, bufs=5)
+                scales = work.tile([P, 2, 2, P], U8, name="xscales", align_bytes=64, bufs=5)
                 xc[s] = (codes, scales)
             codes, scales = xc[s]
             nc.vector.quantize_mx(
@@ -238,12 +242,16 @@ def tile_multilatentattention_pa_t_kernel(tc, x_bytes, x_scale, w_down, w_up, ou
 
         def expand_rope(s, i, tag="rope", bufs=1):
             if i == 0:
-                kv[s] = outp.tile([P, 2, 2, H, DH + DR], F32, name="kv")
                 rope[s] = psum.tile([P, 2, H, 2, HALF], F32, name=tag, bufs=bufs)
             expand(rope[s][:, i].rearrange("p h a f -> p (h a f)"), s, i, wu_rope_codes, wu_rope_scales)
 
+        def out_tile(s):
+            if s not in kv:
+                kv[s] = outp.tile([P, 2, 2, H, DH + DR], F32, name="kv")
+            return kv[s]
+
         def empty_main(s, i):
-            nc.scalar.copy(out=kv[s][:, :, i, :, 0:DH], in_=main[s, i][:].rearrange("p (a h) f -> p a h f", h=H))
+            nc.scalar.copy(out=out_tile(s)[:, :, i, :, 0:DH], in_=main[s, i][:].rearrange("p (a h) f -> p a h f", h=H))
 
         def rope_mul(s, lo, n):
             prod = work.tile([P, 2, n, H, 2, HALF], F32, name="prod", bufs=3)
@@ -266,7 +274,7 @@ def tile_multilatentattention_pa_t_kernel(tc, x_bytes, x_scale, w_down, w_up, ou
         def rope_add(s, lo, n, engine):
             prod = rot[s, lo]
             engine.tensor_tensor(
-                out=kv[s][:, 0, lo:lo + n, :, DH:],
+                out=out_tile(s)[:, 0, lo:lo + n, :, DH:],
                 in0=prod[:, 0].rearrange("p i h a f -> p i h (a f)"),
                 in1=prod[:, 1].rearrange("p i h a f -> p i h (a f)"),
                 op=ALU.add,
@@ -291,6 +299,7 @@ def tile_multilatentattention_pa_t_kernel(tc, x_bytes, x_scale, w_down, w_up, ou
         table_sin()
         widen(3, 0, 2)
         group_up(nc.scalar.copy)
+        widen(4, 0, 2)
         turn(0, 0)
         turn(0, 1)
         for s in range(2):
@@ -309,110 +318,105 @@ def tile_multilatentattention_pa_t_kernel(tc, x_bytes, x_scale, w_down, w_up, ou
         turn(3, 1)
         quant_up()
         quant_x(2, 0, 2)
-        widen(4, 0, 2)
-        empty_down(0, 0)
-        empty_down(0, 1)
-        down(1, 0)
-        down(1, 1)
-        empty_down(1, 0)
-        empty_down(1, 1)
-        empty_turn(3, 0)
-        quant_lat(0, 0, 2)
-        empty_turn(3, 1)
-        down(2, 0)
-        down(2, 1)
-        expand_rope(0, 0)
-        expand_rope(0, 1)
-        expand_main(0, 0)
-        expand_main(0, 1)
-        turn(4, 0)
-        turn(4, 1)
-        empty_down(2, 0)
-        empty_down(2, 1)
-        empty_main(0, 0)
-        empty_main(0, 1)
-        store_v(0, 0, 2)
-        widen(5, 0, 2)
-        quant_lat(1, 0, 2)
-        quant_x(3, 0, 2)
-        quant_lat(2, 0, 2)
-        rope_mul(0, 0, 2)
-        rope_add(0, 0, 2, nc.gpsimd)
-        store_k(0, 0, 2)
-        expand_rope(1, 0)
-        expand_rope(1, 1)
-        expand_main(1, 0)
-        expand_main(1, 1)
-        empty_main(1, 0)
-        empty_main(1, 1)
-        store_v(1, 0, 2)
+        for i in range(2):
+            empty_down(0, i)
+            down(1, i)
+        for i in range(2):
+            empty_down(1, i)
         last = STEPS - 1
-        for it in range(4, last):
-            nxt, wide, mid, old = it + 1, it + 2, it - 1, it - 2
+        for it in range(3, last - 1):
+            nxt, wide, mid, old, mul = it + 1, it + 2, it - 1, it - 2, it - 3
             empty_turn(it, 0)
-            if it == 4:
-                rope_mul(1, 0, 2)
-                rope_add(1, 0, 2, nc.gpsimd)
-                store_k(1, 0, 2)
+            if it == 3:
+                quant_lat(0, 0, 2)
+                for i in range(2):
+                    expand_rope(0, i)
+                    expand_main(0, i)
+                    empty_main(0, i)
+                store_v(0, 0, 2)
             empty_turn(it, 1)
-            down(mid, 0)
-            down(mid, 1)
-            empty_down(mid, 0)
-            empty_down(mid, 1)
-            expand_main(old, 0)
-            expand_rope(old, 0)
-            expand_rope(old, 1)
-            empty_main(old, 0)
             turn(nxt, 0)
             turn(nxt, 1)
-            expand_main(old, 1)
-            if wide < STEPS:
-                widen(wide, 0, 2)
+            quant_lat(old, 0, 2)
+            quant_x(it, 0, 2)
+            rope_mul(mul, 0, 2)
+            rope_add(mul, 0, 2, nc.gpsimd)
+            store_k(mul, 0, 2)
+            down(mid, 0)
+            down(mid, 1)
+            for i in range(2):
+                expand_main(old, i)
+            for i in range(2):
+                expand_rope(old, i)
+            widen(wide, 0, 2)
+            empty_down(mid, 0)
+            empty_down(mid, 1)
+            empty_main(old, 0)
             empty_main(old, 1)
             store_v(old, 0, 2)
-            quant_lat(mid, 0, 2)
-            quant_x(it, 0, 2)
-            rope_mul(old, 0, 2)
-            rope_add(old, 0, 2, nc.gpsimd)
-            store_k(old, 0, 2)
-        empty_turn(last, 0)
-        down(last - 1, 0)
-        down(last - 1, 1)
-        empty_down(last - 1, 0)
-        empty_down(last - 1, 1)
+        a, b, c, d, e = range(last - 4, last + 1)
+        empty_turn(d, 0)
+        empty_turn(d, 1)
         for i in range(2):
-            expand_rope(last - 2, i)
-            expand_main(last - 2, i)
-            empty_main(last - 2, i)
-        store_v(last - 2, 0, 2)
-        empty_turn(last, 1)
-        quant_x(last, 0, 1)
-        quant_lat(last - 1, 0, 2)
-        quant_x(last, 1, 1)
-        rope_mul(last - 2, 0, 2)
-        rope_add(last - 2, 0, 2, nc.vector)
-        store_k(last - 2, 0, 2)
-        down(last, 0)
+            down(c, i)
+            empty_down(c, i)
+        turn(e, 0)
+        turn(e, 1)
+        quant_lat(b, 0, 2)
+        quant_x(d, 0, 2)
+        quant_lat(c, 0, 2)
+        rope_mul(a, 0, 2)
+        rope_add(a, 0, 2, nc.gpsimd)
+        store_k(a, 0, 2)
         for i in range(2):
-            expand_main(last - 1, i)
-        down(last, 1)
+            expand_main(b, i)
+            empty_main(b, i)
         for i in range(2):
-            expand_rope(last - 1, i)
-        empty_down(last, 0)
-        empty_main(last - 1, 0)
-        empty_down(last, 1)
-        empty_main(last - 1, 1)
-        store_v(last - 1, 0, 2)
-        quant_lat(last, 0, 1)
-        rope_mul(last - 1, 0, 2)
-        quant_lat(last, 1, 1)
-        rope_add(last - 1, 0, 2, nc.vector)
-        store_k(last - 1, 0, 2)
+            expand_rope(b, i)
+        store_v(b, 0, 2)
         for i in range(2):
-            expand_rope(last, i, "xt", 3)
-            expand_main(last, i, "xt", 3)
-            empty_main(last, i)
-            store_v(last, i, 1)
-        rope_mul(last, 0, 2)
-        rope_add(last, 0, 2, nc.vector)
-        store_k(last, 0, 2)
+            down(d, i)
+            empty_down(d, i)
+        for i in range(2):
+            expand_rope(c, i, "xt", 3)
+            expand_main(c, i)
+            empty_main(c, i)
+        store_v(c, 0, 2)
+        empty_turn(e, 0)
+        rope_mul(b, 0, 2)
+        rope_add(b, 0, 2, nc.gpsimd)
+        store_k(b, 0, 2)
+        empty_turn(e, 1)
+        quant_x(e, 0, 1)
+        quant_lat(d, 0, 2)
+        quant_x(e, 1, 1)
+
+        rope_mul(c, 0, 2)
+        rope_add(c, 0, 2, nc.vector)
+        store_k(c, 0, 2)
+        down(e, 0)
+        for i in range(2):
+            expand_main(d, i)
+        down(e, 1)
+        for i in range(2):
+            expand_rope(d, i)
+        empty_down(e, 0)
+        empty_main(d, 0)
+        empty_down(e, 1)
+        empty_main(d, 1)
+        store_v(d, 0, 2)
+        quant_lat(e, 0, 1)
+        rope_mul(d, 0, 2)
+        quant_lat(e, 1, 1)
+        rope_add(d, 0, 2, nc.vector)
+        store_k(d, 0, 2)
+        for i in range(2):
+            expand_rope(e, i, "xt", 3)
+            expand_main(e, i, "xt" if i == 0 else "main", 3 if i == 0 else 2)
+            empty_main(e, i)
+            store_v(e, i, 1)
+        for i in range(2):
+            rope_mul(e, i, 1)
+        for i in range(2):
+            rope_add(e, i, 1, nc.vector)
+            store_k(e, i, 1)

@@ -23,6 +23,8 @@ HALF = DR // 2
 N_GROUPS = B * S // (P * GROUP)
 POS_GROUPS = S // (P * GROUP)
 STEPS = N_GROUPS * 2
+K_PASS = 4 * P
+PERIOD = 3
 
 
 def tile_multilatentattention_pa_t_kernel(tc, x_bytes, x_scale, w_down, w_up, out_k, out_v):
@@ -107,7 +109,7 @@ def tile_multilatentattention_pa_t_kernel(tc, x_bytes, x_scale, w_down, w_up, ou
             table(1, 1, -1.0)
             table(2, 1, 1.0)
 
-        wd_grp = [const.tile([P, DL * 4], BF16, align_bytes=64, name=name) for name in ("whole_then_wd", "wd_grp1")]
+        wd_grp = const.tile([P, 2, DL * 4], BF16, align_bytes=64, name="whole_then_wd")
         wd_codes = const.tile([P, 2, DL], U32, align_bytes=64)
         wd_scales = const.tile([P, 2, DL], U8, align_bytes=64)
         wu_main_grp = const.tile([P, 2, H, DH, 4], BF16, align_bytes=64)
@@ -122,12 +124,16 @@ def tile_multilatentattention_pa_t_kernel(tc, x_bytes, x_scale, w_down, w_up, ou
 
         def group_down(g, copy):
             copy(
-                out=wd_grp[g][:].rearrange("p (t m j) -> p t m j", t=4, j=4),
+                out=wd_grp[:, g].rearrange("p (t m j) -> p t m j", t=4, j=4),
                 in_=wd_raw[g][:].rearrange("p j (m t) -> p t m j", t=4),
             )
 
-        def quant_down(g):
-            nc.vector.quantize_mx(out=wd_codes[:, g].bitcast(FP8X4), scales=wd_scales[:, g], in_=wd_grp[g][:])
+        def quant_down():
+            nc.vector.quantize_mx(
+                out=wd_codes[:].rearrange("p g c -> p (g c)").bitcast(FP8X4),
+                scales=wd_scales[:].rearrange("p g c -> p (g c)"),
+                in_=wd_grp[:].rearrange("p g c -> p (g c)"),
+            )
 
         up = wu_raw[:].rearrange("p j (h f) -> p h f j", h=H)
 
@@ -144,6 +150,7 @@ def tile_multilatentattention_pa_t_kernel(tc, x_bytes, x_scale, w_down, w_up, ou
             nc.vector.quantize_mx(out=wu_rope_codes[:].bitcast(FP8X4), scales=wu_rope_scales[:], in_=wu_rope_grp[:].rearrange("p h f j -> p (h f j)"))
 
         xbf = {}
+        aside = {}
         xt = {}
         xg = {}
         xc = {}
@@ -153,24 +160,32 @@ def tile_multilatentattention_pa_t_kernel(tc, x_bytes, x_scale, w_down, w_up, ou
         main = {}
         rope = {}
         kv = {}
-        rot = {}
+        spill = {}
+        by_cos = {}
+        by_sin = {}
 
-        def widen(s, lo, n):
+        def x_bytes_of(s):
+            return x_tiles[s // 2][:, 2 * (s % 2):2 * (s % 2) + 2].rearrange("p i d -> p (i d)").bitcast(FP8)
+
+        def widen(s, lo, hi):
             if lo == 0:
-                xbf[s] = work.tile([P, 2, D], BF16, name="xbf", bufs=6)
-            first = 2 * (s % 2) + lo
-            nc.scalar.copy(
-                out=xbf[s][:, lo:lo + n].rearrange("p i d -> p (i d)"),
-                in_=x_tiles[s // 2][:, first:first + n].rearrange("p i d -> p (i d)").bitcast(FP8),
-            )
+                xbf[s] = work.tile([P, 2 * D], BF16, name="xbf", bufs=6)
+            nc.scalar.copy(out=xbf[s][:, lo:hi], in_=x_bytes_of(s)[:, lo:hi])
+
+        def widen_aside(s, spent):
+            aside[s] = xg[spent][:, 0, 0]
+            nc.gpsimd.tensor_copy(out=aside[s], in_=x_bytes_of(s)[:, 2 * D - K_PASS:])
 
         def turn(s, i):
             bank = psum.tile([P, 2, 2, P], F32, name="xt", bufs=3)
             xt[s, i] = bank
-            words = xbf[s][:, i].bitcast(F32)
             for g in range(2):
+                if s in aside and i == 1 and g == 1:
+                    values = aside[s]
+                else:
+                    values = xbf[s][:, i * D + g * K_PASS:i * D + (g + 1) * K_PASS]
                 for u in range(2):
-                    nc.tensor.transpose(bank[:, u, g, :], words[:, 256 * g + u:256 * (g + 1):2], ident[:])
+                    nc.tensor.transpose(bank[:, u, g, :], values.bitcast(F32)[:, u::2], ident[:])
 
         def empty_turn(s, i):
             if i == 0:
@@ -253,30 +268,45 @@ def tile_multilatentattention_pa_t_kernel(tc, x_bytes, x_scale, w_down, w_up, ou
         def empty_main(s, i):
             nc.scalar.copy(out=out_tile(s)[:, :, i, :, 0:DH], in_=main[s, i][:].rearrange("p (a h) f -> p a h f", h=H))
 
-        def rope_mul(s, lo, n):
-            prod = work.tile([P, 2, n, H, 2, HALF], F32, name="prod", bufs=3)
-            rot[s, lo] = prod
+        def cos_of(s, lo, n):
             first = (2 * s) % n_pos + lo
-            bank = rope[s][:, lo:lo + n]
+            return trig[:, first:first + n, 0].unsqueeze(2).to_broadcast([P, n, 2 * H, HALF])
+
+        def spill_rope(s):
+            spill[s] = work.tile([P, 2, 2 * H, HALF], F32, name="spill")
+            nc.scalar.copy(out=spill[s][:], in_=rope[s][:].rearrange("p i h a f -> p i (h a) f"))
+
+        def rope_cos_beside(s, spent):
+            by_cos[s, 0] = spent.bitcast(F32).rearrange("p (i c f) -> p i c f", i=2, f=HALF)
+            nc.gpsimd.tensor_tensor(out=by_cos[s, 0], in0=spill[s][:], in1=cos_of(s, 0, 2), op=ALU.mult)
+
+        def rope_cos(s, lo, n):
+            product = work.tile([P, n, 2 * H, HALF], F32, name="by_cos")
+            by_cos[s, lo] = product[:]
             nc.vector.tensor_tensor(
-                out=prod[:, 0].rearrange("p i h a f -> p i (h a) f"),
-                in0=bank.rearrange("p i h a f -> p i (h a) f"),
-                in1=trig[:, first:first + n, 0].unsqueeze(2).to_broadcast([P, n, 2 * H, HALF]),
-                op=ALU.mult,
+                out=by_cos[s, lo], in0=rope[s][:, lo:lo + n].rearrange("p i h a f -> p i (h a) f"),
+                in1=cos_of(s, lo, n), op=ALU.mult,
             )
+
+        def rope_sin(s, lo, n):
+            by_sin[s, lo] = work.tile([P, n, H, 2, HALF], F32, name="by_sin")
+            first = (2 * s) % n_pos + lo
             nc.vector.tensor_tensor(
-                out=prod[:, 1],
-                in0=bank[:, :, :, ::-1, :],
+                out=by_sin[s, lo][:],
+                in0=rope[s][:, lo:lo + n, :, ::-1, :],
                 in1=trig[:, first:first + n, 1:3].unsqueeze(2).to_broadcast([P, n, H, 2, HALF]),
                 op=ALU.mult,
             )
 
+        def rope_mul(s, lo, n):
+            rope_cos(s, lo, n)
+            rope_sin(s, lo, n)
+
         def rope_add(s, lo, n, engine):
-            prod = rot[s, lo]
             engine.tensor_tensor(
                 out=out_tile(s)[:, 0, lo:lo + n, :, DH:],
-                in0=prod[:, 0].rearrange("p i h a f -> p i h (a f)"),
-                in1=prod[:, 1].rearrange("p i h a f -> p i h (a f)"),
+                in0=by_cos[s, lo].rearrange("p i (h a) f -> p i h (a f)", h=H),
+                in1=by_sin[s, lo][:].rearrange("p i h a f -> p i h (a f)"),
                 op=ALU.add,
             )
 
@@ -288,18 +318,18 @@ def tile_multilatentattention_pa_t_kernel(tc, x_bytes, x_scale, w_down, w_up, ou
             first = 2 * (s % 2) + lo
             nc.sync.dma_start(out=k_view[s // 2][:, first:first + n], in_=kv[s][:, 0, lo:lo + n].rearrange("p i h f -> p i (h f)"))
 
-        widen(0, 0, 1)
-        widen(0, 1, 1)
+        widen(0, 0, D)
+        widen(0, D, 2 * D)
         group_down(0, pool_copy)
         group_down(1, pool_copy)
-        widen(1, 0, 2)
+        widen(1, 0, 2 * D)
         table_args()
-        widen(2, 0, 2)
+        widen(2, 0, 2 * D)
         table_cos()
         table_sin()
-        widen(3, 0, 2)
+        widen(3, 0, 2 * D)
         group_up(nc.scalar.copy)
-        widen(4, 0, 2)
+        widen(4, 0, 2 * D)
         turn(0, 0)
         turn(0, 1)
         for s in range(2):
@@ -308,9 +338,8 @@ def tile_multilatentattention_pa_t_kernel(tc, x_bytes, x_scale, w_down, w_up, ou
                 turn(s + 1, i)
         empty_turn(2, 0)
         turn(3, 0)
-        quant_down(0)
+        quant_down()
         quant_x(0, 0, 2)
-        quant_down(1)
         quant_x(1, 0, 2)
         empty_turn(2, 1)
         down(0, 0)
@@ -324,6 +353,10 @@ def tile_multilatentattention_pa_t_kernel(tc, x_bytes, x_scale, w_down, w_up, ou
         for i in range(2):
             empty_down(1, i)
         last = STEPS - 1
+
+        def spilled(s):
+            return s % PERIOD != 0 and s < last - 4
+
         for it in range(3, last - 1):
             nxt, wide, mid, old, mul = it + 1, it + 2, it - 1, it - 2, it - 3
             empty_turn(it, 0)
@@ -339,7 +372,12 @@ def tile_multilatentattention_pa_t_kernel(tc, x_bytes, x_scale, w_down, w_up, ou
             turn(nxt, 1)
             quant_lat(old, 0, 2)
             quant_x(it, 0, 2)
-            rope_mul(mul, 0, 2)
+            if spilled(mul):
+                rope_cos_beside(mul, xg[it][:, 0, 0])
+                rope_sin(mul, 0, 2)
+            else:
+                widen_aside(wide, it)
+                rope_mul(mul, 0, 2)
             rope_add(mul, 0, 2, nc.gpsimd)
             store_k(mul, 0, 2)
             down(mid, 0)
@@ -348,10 +386,13 @@ def tile_multilatentattention_pa_t_kernel(tc, x_bytes, x_scale, w_down, w_up, ou
                 expand_main(old, i)
             for i in range(2):
                 expand_rope(old, i)
-            widen(wide, 0, 2)
+            widen(wide, 0, 2 * D - (K_PASS if wide in aside else 0))
             empty_down(mid, 0)
             empty_down(mid, 1)
             empty_main(old, 0)
+            if spilled(old):
+                spill_rope(old)
+
             empty_main(old, 1)
             store_v(old, 0, 2)
         a, b, c, d, e = range(last - 4, last + 1)
@@ -415,8 +456,6 @@ def tile_multilatentattention_pa_t_kernel(tc, x_bytes, x_scale, w_down, w_up, ou
             expand_main(e, i, "xt" if i == 0 else "main", 3 if i == 0 else 2)
             empty_main(e, i)
             store_v(e, i, 1)
-        for i in range(2):
-            rope_mul(e, i, 1)
-        for i in range(2):
-            rope_add(e, i, 1, nc.vector)
-            store_k(e, i, 1)
+        rope_mul(e, 0, 2)
+        rope_add(e, 0, 2, nc.vector)
+        store_k(e, 0, 2)

@@ -24,7 +24,7 @@ N_GROUPS = B * S // (P * GROUP)
 POS_GROUPS = S // (P * GROUP)
 STEPS = N_GROUPS * 2
 K_PASS = 4 * P
-PERIOD = 3
+PERIOD = 5
 
 
 def tile_multilatentattention_pa_t_kernel(tc, x_bytes, x_scale, w_down, w_up, out_k, out_v):
@@ -173,27 +173,28 @@ def tile_multilatentattention_pa_t_kernel(tc, x_bytes, x_scale, w_down, w_up, ou
             nc.scalar.copy(out=xbf[s][:, lo:hi], in_=x_bytes_of(s)[:, lo:hi])
 
         def widen_aside(s, spent):
-            aside[s] = xg[spent][:, 0, 0]
-            nc.gpsimd.tensor_copy(out=aside[s], in_=x_bytes_of(s)[:, 2 * D - K_PASS:])
+            aside[s] = xg[spent][:, 0].rearrange("p g c -> p (g c)")
+            nc.gpsimd.tensor_copy(out=aside[s], in_=x_bytes_of(s)[:, D:])
 
-        def turn(s, i):
+        def turn(s, i, passes=(0, 1)):
             bank = psum.tile([P, 2, 2, P], F32, name="xt", bufs=3)
-            xt[s, i] = bank
-            for g in range(2):
-                if s in aside and i == 1 and g == 1:
-                    values = aside[s]
+            xt[s, i, passes[0]] = bank
+            for g in passes:
+                if s in aside and i == 1:
+                    values = aside[s][:, g * K_PASS:(g + 1) * K_PASS]
                 else:
                     values = xbf[s][:, i * D + g * K_PASS:i * D + (g + 1) * K_PASS]
                 for u in range(2):
                     nc.tensor.transpose(bank[:, u, g, :], values.bitcast(F32)[:, u::2], ident[:])
 
-        def empty_turn(s, i):
-            if i == 0:
+        def empty_turn(s, i, passes=(0, 1)):
+            if i == 0 and passes[0] == 0:
                 xg[s] = work.tile([P, 2, 2, P * 4], BF16, name="xg", align_bytes=64, bufs=5)
+            gs = slice(passes[0], passes[-1] + 1)
             nc.vector.tensor_tensor(
-                out=xg[s][:, i].rearrange("p g (r u e) -> p g r u e", u=2, e=2),
-                in0=xt[s, i][:].bitcast(BF16).rearrange("p u g (r e) -> p g r u e", e=2),
-                in1=scale_cols[:].rearrange("p g (u e) -> p g u e", u=2).unsqueeze(2).to_broadcast([P, 2, P, 2, 2]),
+                out=xg[s][:, i, gs].rearrange("p g (r u e) -> p g r u e", u=2, e=2),
+                in0=xt[s, i, passes[0]][:, :, gs].bitcast(BF16).rearrange("p u g (r e) -> p g r u e", e=2),
+                in1=scale_cols[:, gs].rearrange("p g (u e) -> p g u e", u=2).unsqueeze(2).to_broadcast([P, len(passes), P, 2, 2]),
                 op=ALU.mult,
             )
 
@@ -318,7 +319,8 @@ def tile_multilatentattention_pa_t_kernel(tc, x_bytes, x_scale, w_down, w_up, ou
             first = 2 * (s % 2) + lo
             nc.sync.dma_start(out=k_view[s // 2][:, first:first + n], in_=kv[s][:, 0, lo:lo + n].rearrange("p i h f -> p i (h f)"))
 
-        widen(0, 0, D)
+        widen(0, 0, K_PASS)
+        widen(0, K_PASS, D)
         widen(0, D, 2 * D)
         group_down(0, pool_copy)
         group_down(1, pool_copy)
@@ -330,21 +332,25 @@ def tile_multilatentattention_pa_t_kernel(tc, x_bytes, x_scale, w_down, w_up, ou
         widen(3, 0, 2 * D)
         group_up(nc.scalar.copy)
         widen(4, 0, 2 * D)
-        turn(0, 0)
+        turn(0, 0, (0,))
+        turn(0, 0, (1,))
         turn(0, 1)
-        for s in range(2):
-            for i in range(2):
-                empty_turn(s, i)
-                turn(s + 1, i)
-        empty_turn(2, 0)
-        turn(3, 0)
+        empty_turn(0, 0, (0,))
+        empty_turn(0, 0, (1,))
+        turn(1, 0)
+        empty_turn(0, 1)
+        turn(1, 1)
+        for i in range(2):
+            empty_turn(1, i)
+            turn(2, i)
+        for i in range(2):
+            empty_turn(2, i)
+            turn(3, i)
         quant_down()
         quant_x(0, 0, 2)
         quant_x(1, 0, 2)
-        empty_turn(2, 1)
         down(0, 0)
         down(0, 1)
-        turn(3, 1)
         quant_up()
         quant_x(2, 0, 2)
         for i in range(2):
@@ -386,7 +392,7 @@ def tile_multilatentattention_pa_t_kernel(tc, x_bytes, x_scale, w_down, w_up, ou
                 expand_main(old, i)
             for i in range(2):
                 expand_rope(old, i)
-            widen(wide, 0, 2 * D - (K_PASS if wide in aside else 0))
+            widen(wide, 0, 2 * D - (D if wide in aside else 0))
             empty_down(mid, 0)
             empty_down(mid, 1)
             empty_main(old, 0)
@@ -443,9 +449,10 @@ def tile_multilatentattention_pa_t_kernel(tc, x_bytes, x_scale, w_down, w_up, ou
             expand_rope(d, i)
         empty_down(e, 0)
         empty_main(d, 0)
+        store_v(d, 0, 1)
         empty_down(e, 1)
         empty_main(d, 1)
-        store_v(d, 0, 2)
+        store_v(d, 1, 1)
         quant_lat(e, 0, 1)
         rope_mul(d, 0, 2)
         quant_lat(e, 1, 1)

@@ -16,15 +16,18 @@ ACT = mybir.ActivationFunctionType
 B, S, D, H, DH, DL, DR = 2, 2048, 1024, 2, 128, 512, 64
 N_UP = H * (2 * DH + DR)
 FLOPS = 2 * B * S * D * DL + 2 * B * S * DL * N_UP
+ROPE_BASE = 10000.0
 
 P = 128
+K_PASS = 4 * P
 GROUP = 4
 HALF = DR // 2
 N_GROUPS = B * S // (P * GROUP)
 POS_GROUPS = S // (P * GROUP)
-STEPS = N_GROUPS * 2
-K_PASS = 4 * P
-PERIOD = 5
+N_POS = POS_GROUPS * GROUP
+PAIRS = N_GROUPS * 2
+TURN_BANKS = 3
+SHARE_PERIOD = 5
 
 
 def tile_multilatentattention_pa_t_kernel(tc, x_bytes, x_scale, w_down, w_up, out_k, out_v):
@@ -61,30 +64,30 @@ def tile_multilatentattention_pa_t_kernel(tc, x_bytes, x_scale, w_down, w_up, ou
         warm = const.tile([P, 1], F32)
         nc.vector.memset(warm[:], 0.0)
         nc.scalar.activation(out=warm[:], in_=warm[:], func=ACT.Sin)
-        n_pos = POS_GROUPS * GROUP
+
         pos = const.tile([P, POS_GROUPS, GROUP], F32)
         nc.gpsimd.iota(pos[:], pattern=[[P * GROUP, POS_GROUPS], [1, GROUP]], base=0, channel_multiplier=GROUP, allow_small_or_imprecise_dtypes=True)
         offset = const.tile([P, P], F32)
         nc.gpsimd.iota(offset[:], pattern=[[1, P]], base=0, channel_multiplier=-1, allow_small_or_imprecise_dtypes=True)
-        low = const.tile([P, 4, n_pos], F32)
+        low = const.tile([P, 4, N_POS], F32)
         for a in range(4):
             nc.vector.tensor_scalar(
                 out=low[:, a], in0=pos[:].rearrange("p a b -> p (a b)"),
-                scalar1=10000.0 ** (-a / HALF) / (2 * math.pi), scalar2=None, op0=ALU.mult,
+                scalar1=ROPE_BASE ** (-a / HALF) / (2 * math.pi), scalar2=None, op0=ALU.mult,
             )
         ident = const.tile([P, P], F32)
         nc.vector.tensor_scalar(out=ident[:], in0=offset[:], scalar1=0.0, scalar2=None, op0=ALU.is_equal)
-        shape = [P, HALF // 4, n_pos, 4]
+        shape = [P, HALF // 4, N_POS, 4]
         turns = const.tile(shape, F32)
         for b in range(HALF // 4):
             nc.vector.tensor_scalar(
                 out=turns[:, b], in0=low[:].rearrange("p a n -> p n a"),
-                scalar1=10000.0 ** (-4 * b / HALF), scalar2=None, op0=ALU.mult,
+                scalar1=ROPE_BASE ** (-4 * b / HALF), scalar2=None, op0=ALU.mult,
             )
         whole = const.tile(shape, I32, name="whole_then_wd", align_bytes=64)
         frac = const.tile(shape, F32)
         mag = const.tile([P, 2] + shape[1:], F32)
-        trig = const.tile([P, n_pos, 3, HALF], F32)
+        trig = const.tile([P, N_POS, 3, HALF], F32)
         halves = [slice(0, HALF // 8), slice(HALF // 8, HALF // 4)]
         for h in halves:
             nc.vector.tensor_scalar(out=whole[:, h], in0=turns[:, h], scalar1=-0.125, scalar2=None, op0=ALU.add)
@@ -95,19 +98,13 @@ def tile_multilatentattention_pa_t_kernel(tc, x_bytes, x_scale, w_down, w_up, ou
             nc.scalar.activation(out=mag[:, 0], in_=frac[:], func=ACT.Abs, scale=2 * math.pi)
             nc.scalar.activation(out=mag[:, 1], in_=frac[:], func=ACT.Abs, scale=2 * math.pi, bias=-math.pi / 2)
 
-        def table(c, arg, sign):
-            nc.scalar.activation(
-                out=trig[:, :, c].rearrange("p n (b a) -> p n b a", a=4),
-                in_=mag[:, arg].rearrange("p b n a -> p n b a"),
-                func=ACT.Sin, scale=-sign, bias=sign * math.pi / 2,
-            )
-
-        def table_cos():
-            table(0, 0, 1.0)
-
-        def table_sin():
-            table(1, 1, -1.0)
-            table(2, 1, 1.0)
+        def tables():
+            for c, arg, sign in ((0, 0, 1.0), (1, 1, -1.0), (2, 1, 1.0)):
+                nc.scalar.activation(
+                    out=trig[:, :, c].rearrange("p n (b a) -> p n b a", a=4),
+                    in_=mag[:, arg].rearrange("p b n a -> p n b a"),
+                    func=ACT.Sin, scale=-sign, bias=sign * math.pi / 2,
+                )
 
         wd_grp = const.tile([P, 2, DL * 4], BF16, align_bytes=64, name="whole_then_wd")
         wd_codes = const.tile([P, 2, DL], U32, align_bytes=64)
@@ -119,13 +116,11 @@ def tile_multilatentattention_pa_t_kernel(tc, x_bytes, x_scale, w_down, w_up, ou
         wu_rope_codes = const.tile([P, H * DR], U32, align_bytes=64)
         wu_rope_scales = const.tile([P, H * DR], U8, align_bytes=64)
 
-        def pool_copy(out, in_):
-            nc.gpsimd.tensor_scalar(out=out, in0=in_, scalar1=1.0, scalar2=0.0, op0=ALU.mult, op1=ALU.add)
-
-        def group_down(g, copy):
-            copy(
+        def group_down(g):
+            nc.gpsimd.tensor_scalar(
                 out=wd_grp[:, g].rearrange("p (t m j) -> p t m j", t=4, j=4),
-                in_=wd_raw[g][:].rearrange("p j (m t) -> p t m j", t=4),
+                in0=wd_raw[g][:].rearrange("p j (m t) -> p t m j", t=4),
+                scalar1=1.0, scalar2=0.0, op0=ALU.mult, op1=ALU.add,
             )
 
         def quant_down():
@@ -135,15 +130,14 @@ def tile_multilatentattention_pa_t_kernel(tc, x_bytes, x_scale, w_down, w_up, ou
                 in_=wd_grp[:].rearrange("p g c -> p (g c)"),
             )
 
-        up = wu_raw[:].rearrange("p j (h f) -> p h f j", h=H)
-
-        def group_up(copy):
+        def group_up():
+            up = wu_raw[:].rearrange("p j (h f) -> p h f j", h=H)
             for dst, src in (
                 (wu_main_grp[:, 0], up[:, :, 0:DH, :]),
                 (wu_main_grp[:, 1], up[:, :, DH + DR:, :]),
                 (wu_rope_grp[:], up[:, :, DH:DH + DR, :]),
             ):
-                copy(out=dst, in_=src)
+                nc.scalar.copy(out=dst, in_=src)
 
         def quant_up():
             nc.vector.quantize_mx(out=wu_main_codes[:].bitcast(FP8X4), scales=wu_main_scales[:], in_=wu_main_grp[:].rearrange("p a h f j -> p (a h f j)"))
@@ -177,7 +171,7 @@ def tile_multilatentattention_pa_t_kernel(tc, x_bytes, x_scale, w_down, w_up, ou
             nc.gpsimd.tensor_copy(out=aside[s], in_=x_bytes_of(s)[:, D:])
 
         def turn(s, i, passes=(0, 1)):
-            bank = psum.tile([P, 2, 2, P], F32, name="xt", bufs=3)
+            bank = psum.tile([P, 2, 2, P], F32, name="xt", bufs=TURN_BANKS)
             xt[s, i, passes[0]] = bank
             for g in passes:
                 if s in aside and i == 1:
@@ -198,7 +192,7 @@ def tile_multilatentattention_pa_t_kernel(tc, x_bytes, x_scale, w_down, w_up, ou
                 op=ALU.mult,
             )
 
-        def quant_x(s, lo, n):
+        def quant_x(s, lo=0, n=2):
             if lo == 0:
                 codes = work.tile([P, 2, 2, P], U32, name="xcodes", align_bytes=64, bufs=5)
                 scales = work.tile([P, 2, 2, P], U8, name="xscales", align_bytes=64, bufs=5)
@@ -231,7 +225,7 @@ def tile_multilatentattention_pa_t_kernel(tc, x_bytes, x_scale, w_down, w_up, ou
                 lg[s] = work.tile([P, 2, P, 4], BF16, name="lg", align_bytes=64, bufs=4)
             nc.scalar.copy(out=lg[s][:, i], in_=lat[s, i][:].rearrange("p t r -> p r t"))
 
-        def quant_lat(s, lo, n):
+        def quant_lat(s, lo=0, n=2):
             if lo == 0:
                 codes = work.tile([P, 2, P], U32, name="lcodes", align_bytes=64, bufs=4)
                 scales = work.tile([P, 2, P], U8, name="lscales", align_bytes=64, bufs=4)
@@ -269,68 +263,61 @@ def tile_multilatentattention_pa_t_kernel(tc, x_bytes, x_scale, w_down, w_up, ou
         def empty_main(s, i):
             nc.scalar.copy(out=out_tile(s)[:, :, i, :, 0:DH], in_=main[s, i][:].rearrange("p (a h) f -> p a h f", h=H))
 
-        def cos_of(s, lo, n):
-            first = (2 * s) % n_pos + lo
-            return trig[:, first:first + n, 0].unsqueeze(2).to_broadcast([P, n, 2 * H, HALF])
+        def trig_of(s):
+            return trig[:, (2 * s) % N_POS:(2 * s) % N_POS + 2]
+
+        def cos_of(s):
+            return trig_of(s)[:, :, 0].unsqueeze(2).to_broadcast([P, 2, 2 * H, HALF])
 
         def spill_rope(s):
             spill[s] = work.tile([P, 2, 2 * H, HALF], F32, name="spill")
             nc.scalar.copy(out=spill[s][:], in_=rope[s][:].rearrange("p i h a f -> p i (h a) f"))
 
         def rope_cos_beside(s, spent):
-            by_cos[s, 0] = spent.bitcast(F32).rearrange("p (i c f) -> p i c f", i=2, f=HALF)
-            nc.gpsimd.tensor_tensor(out=by_cos[s, 0], in0=spill[s][:], in1=cos_of(s, 0, 2), op=ALU.mult)
+            by_cos[s] = xg[spent][:, 0, 0].bitcast(F32).rearrange("p (i c f) -> p i c f", i=2, f=HALF)
+            nc.gpsimd.tensor_tensor(out=by_cos[s], in0=spill[s][:], in1=cos_of(s), op=ALU.mult)
 
-        def rope_cos(s, lo, n):
-            product = work.tile([P, n, 2 * H, HALF], F32, name="by_cos")
-            by_cos[s, lo] = product[:]
-            nc.vector.tensor_tensor(
-                out=by_cos[s, lo], in0=rope[s][:, lo:lo + n].rearrange("p i h a f -> p i (h a) f"),
-                in1=cos_of(s, lo, n), op=ALU.mult,
-            )
+        def rope_cos(s):
+            product = work.tile([P, 2, 2 * H, HALF], F32, name="by_cos")
+            by_cos[s] = product[:]
+            nc.vector.tensor_tensor(out=by_cos[s], in0=rope[s][:].rearrange("p i h a f -> p i (h a) f"), in1=cos_of(s), op=ALU.mult)
 
-        def rope_sin(s, lo, n):
-            by_sin[s, lo] = work.tile([P, n, H, 2, HALF], F32, name="by_sin")
-            first = (2 * s) % n_pos + lo
+        def rope_sin(s):
+            by_sin[s] = work.tile([P, 2, H, 2, HALF], F32, name="by_sin")
             nc.vector.tensor_tensor(
-                out=by_sin[s, lo][:],
-                in0=rope[s][:, lo:lo + n, :, ::-1, :],
-                in1=trig[:, first:first + n, 1:3].unsqueeze(2).to_broadcast([P, n, H, 2, HALF]),
+                out=by_sin[s][:],
+                in0=rope[s][:, :, :, ::-1, :],
+                in1=trig_of(s)[:, :, 1:3].unsqueeze(2).to_broadcast([P, 2, H, 2, HALF]),
                 op=ALU.mult,
             )
 
-        def rope_mul(s, lo, n):
-            rope_cos(s, lo, n)
-            rope_sin(s, lo, n)
-
-        def rope_add(s, lo, n, engine):
+        def rope_add(s, engine):
             engine.tensor_tensor(
-                out=out_tile(s)[:, 0, lo:lo + n, :, DH:],
-                in0=by_cos[s, lo].rearrange("p i (h a) f -> p i h (a f)", h=H),
-                in1=by_sin[s, lo][:].rearrange("p i h a f -> p i h (a f)"),
+                out=out_tile(s)[:, 0, :, :, DH:],
+                in0=by_cos[s].rearrange("p i (h a) f -> p i h (a f)", h=H),
+                in1=by_sin[s][:].rearrange("p i h a f -> p i h (a f)"),
                 op=ALU.add,
             )
 
-        def store_v(s, lo, n):
+        def store_v(s, lo=0, n=2):
             first = 2 * (s % 2) + lo
             nc.sync.dma_start(out=v_view[s // 2][:, H * first:H * (first + n)], in_=kv[s][:, 1, lo:lo + n, :, 0:DH].rearrange("p i h f -> p (i h) f"))
 
-        def store_k(s, lo, n):
-            first = 2 * (s % 2) + lo
-            nc.sync.dma_start(out=k_view[s // 2][:, first:first + n], in_=kv[s][:, 0, lo:lo + n].rearrange("p i h f -> p i (h f)"))
+        def store_k(s):
+            first = 2 * (s % 2)
+            nc.sync.dma_start(out=k_view[s // 2][:, first:first + 2], in_=kv[s][:, 0].rearrange("p i h f -> p i (h f)"))
 
         widen(0, 0, K_PASS)
         widen(0, K_PASS, D)
         widen(0, D, 2 * D)
-        group_down(0, pool_copy)
-        group_down(1, pool_copy)
+        group_down(0)
+        group_down(1)
         widen(1, 0, 2 * D)
         table_args()
         widen(2, 0, 2 * D)
-        table_cos()
-        table_sin()
+        tables()
         widen(3, 0, 2 * D)
-        group_up(nc.scalar.copy)
+        group_up()
         widen(4, 0, 2 * D)
         turn(0, 0, (0,))
         turn(0, 0, (1,))
@@ -340,68 +327,67 @@ def tile_multilatentattention_pa_t_kernel(tc, x_bytes, x_scale, w_down, w_up, ou
         turn(1, 0)
         empty_turn(0, 1)
         turn(1, 1)
-        for i in range(2):
-            empty_turn(1, i)
-            turn(2, i)
-        for i in range(2):
-            empty_turn(2, i)
-            turn(3, i)
+        for s in (1, 2):
+            for i in range(2):
+                empty_turn(s, i)
+                turn(s + 1, i)
         quant_down()
-        quant_x(0, 0, 2)
-        quant_x(1, 0, 2)
+        quant_x(0)
+        quant_x(1)
         down(0, 0)
         down(0, 1)
         quant_up()
-        quant_x(2, 0, 2)
+        quant_x(2)
         for i in range(2):
             empty_down(0, i)
             down(1, i)
         for i in range(2):
             empty_down(1, i)
-        last = STEPS - 1
+
+        first_round, tail = 3, PAIRS - 5
 
         def spilled(s):
-            return s % PERIOD != 0 and s < last - 4
+            return s % SHARE_PERIOD != 0 and s < tail
 
-        for it in range(3, last - 1):
-            nxt, wide, mid, old, mul = it + 1, it + 2, it - 1, it - 2, it - 3
-            empty_turn(it, 0)
-            if it == 3:
-                quant_lat(0, 0, 2)
+        for now in range(first_round, PAIRS - 2):
+            wide, mid, old, done = now + 2, now - 1, now - 2, now - 3
+            empty_turn(now, 0)
+            if now == first_round:
+                quant_lat(0)
                 for i in range(2):
                     expand_rope(0, i)
                     expand_main(0, i)
                     empty_main(0, i)
-                store_v(0, 0, 2)
-            empty_turn(it, 1)
-            turn(nxt, 0)
-            turn(nxt, 1)
-            quant_lat(old, 0, 2)
-            quant_x(it, 0, 2)
-            if spilled(mul):
-                rope_cos_beside(mul, xg[it][:, 0, 0])
-                rope_sin(mul, 0, 2)
+                store_v(0)
+            empty_turn(now, 1)
+            turn(now + 1, 0)
+            turn(now + 1, 1)
+            quant_lat(old)
+            quant_x(now)
+            if spilled(done):
+                rope_cos_beside(done, now)
             else:
-                widen_aside(wide, it)
-                rope_mul(mul, 0, 2)
-            rope_add(mul, 0, 2, nc.gpsimd)
-            store_k(mul, 0, 2)
+                widen_aside(wide, now)
+                rope_cos(done)
+            rope_sin(done)
+            rope_add(done, nc.gpsimd)
+            store_k(done)
             down(mid, 0)
             down(mid, 1)
             for i in range(2):
                 expand_main(old, i)
             for i in range(2):
                 expand_rope(old, i)
-            widen(wide, 0, 2 * D - (D if wide in aside else 0))
+            widen(wide, 0, D if wide in aside else 2 * D)
             empty_down(mid, 0)
             empty_down(mid, 1)
             empty_main(old, 0)
             if spilled(old):
                 spill_rope(old)
-
             empty_main(old, 1)
-            store_v(old, 0, 2)
-        a, b, c, d, e = range(last - 4, last + 1)
+            store_v(old)
+
+        a, b, c, d, e = range(tail, PAIRS)
         empty_turn(d, 0)
         empty_turn(d, 1)
         for i in range(2):
@@ -409,60 +395,69 @@ def tile_multilatentattention_pa_t_kernel(tc, x_bytes, x_scale, w_down, w_up, ou
             empty_down(c, i)
         turn(e, 0)
         turn(e, 1)
-        quant_lat(b, 0, 2)
-        quant_x(d, 0, 2)
-        quant_lat(c, 0, 2)
-        rope_mul(a, 0, 2)
-        rope_add(a, 0, 2, nc.gpsimd)
-        store_k(a, 0, 2)
+        quant_lat(b)
+        quant_x(d)
+        quant_lat(c)
+        rope_cos(a)
+        rope_sin(a)
+        rope_add(a, nc.gpsimd)
         for i in range(2):
             expand_main(b, i)
             empty_main(b, i)
         for i in range(2):
             expand_rope(b, i)
-        store_v(b, 0, 2)
+        store_v(b)
+        store_k(a)
         for i in range(2):
             down(d, i)
             empty_down(d, i)
         for i in range(2):
-            expand_rope(c, i, "xt", 3)
+            expand_rope(c, i, "xt", TURN_BANKS)
             expand_main(c, i)
-            empty_main(c, i)
-        store_v(c, 0, 2)
         empty_turn(e, 0)
-        rope_mul(b, 0, 2)
-        rope_add(b, 0, 2, nc.gpsimd)
-        store_k(b, 0, 2)
-        empty_turn(e, 1)
+        rope_cos(b)
         quant_x(e, 0, 1)
-        quant_lat(d, 0, 2)
-        quant_x(e, 1, 1)
-
-        rope_mul(c, 0, 2)
-        rope_add(c, 0, 2, nc.vector)
-        store_k(c, 0, 2)
+        rope_sin(b)
+        rope_add(b, nc.gpsimd)
         down(e, 0)
-        for i in range(2):
-            expand_main(d, i)
-        down(e, 1)
+        empty_main(c, 0)
+        store_v(c, 0, 1)
+        store_k(b)
+        empty_down(e, 0)
+        empty_main(c, 1)
+        store_v(c, 1, 1)
+        empty_turn(e, 1)
+        quant_lat(d)
+        quant_x(e, 1, 1)
+        quant_lat(e, 0, 1)
+        rope_cos(c)
+        rope_sin(c)
+        rope_add(c, nc.vector)
         for i in range(2):
             expand_rope(d, i)
-        empty_down(e, 0)
+        expand_main(d, 0)
+        down(e, 1)
+        expand_main(d, 1)
         empty_main(d, 0)
         store_v(d, 0, 1)
+        store_k(c)
         empty_down(e, 1)
+        expand_rope(e, 0, "xt", TURN_BANKS)
+        expand_main(e, 0, "xt", TURN_BANKS)
+        rope_cos(d)
+        rope_sin(d)
+        quant_lat(e, 1, 1)
+        rope_add(d, nc.vector)
         empty_main(d, 1)
         store_v(d, 1, 1)
-        quant_lat(e, 0, 1)
-        rope_mul(d, 0, 2)
-        quant_lat(e, 1, 1)
-        rope_add(d, 0, 2, nc.vector)
-        store_k(d, 0, 2)
-        for i in range(2):
-            expand_rope(e, i, "xt", 3)
-            expand_main(e, i, "xt" if i == 0 else "main", 3 if i == 0 else 2)
-            empty_main(e, i)
-            store_v(e, i, 1)
-        rope_mul(e, 0, 2)
-        rope_add(e, 0, 2, nc.vector)
-        store_k(e, 0, 2)
+        store_k(d)
+        empty_main(e, 0)
+        store_v(e, 0, 1)
+        expand_rope(e, 1)
+        expand_main(e, 1)
+        empty_main(e, 1)
+        store_v(e, 1, 1)
+        rope_cos(e)
+        rope_sin(e)
+        rope_add(e, nc.vector)
+        store_k(e)

@@ -25,9 +25,9 @@ HALF = DR // 2
 N_GROUPS = B * S // (P * GROUP)
 POS_GROUPS = S // (P * GROUP)
 N_POS = POS_GROUPS * GROUP
-PAIRS = N_GROUPS * 2
-TURN_BANKS = 3
-SHARE_PERIOD = 5
+N_TILES = N_GROUPS * GROUP
+TURN_BANKS = 4
+PRODUCT_BANKS = 4
 
 
 def tile_multilatentattention_pa_t_kernel(tc, x_bytes, x_scale, w_down, w_up, out_k, out_v):
@@ -41,8 +41,8 @@ def tile_multilatentattention_pa_t_kernel(tc, x_bytes, x_scale, w_down, w_up, ou
         const = ctx.enter_context(tc.tile_pool(name="const", bufs=1))
         xin = ctx.enter_context(tc.tile_pool(name="xin", bufs=N_GROUPS))
         work = ctx.enter_context(tc.tile_pool(name="work", bufs=3))
-        outp = ctx.enter_context(tc.tile_pool(name="outp", bufs=6))
-        psum = ctx.enter_context(tc.psum_pool(name="psum", bufs=2))
+        outp = ctx.enter_context(tc.tile_pool(name="outp", bufs=3))
+        psum = ctx.enter_context(tc.psum_pool(name="psum", bufs=PRODUCT_BANKS))
         ctx.enter_context(tc.manual_schedule())
 
         wd_raw = [const.tile([P, 4, DL], BF16, name="wd_raw%d" % g) for g in range(2)]
@@ -57,13 +57,16 @@ def tile_multilatentattention_pa_t_kernel(tc, x_bytes, x_scale, w_down, w_up, ou
         nc.sync.dma_start(out=x_tiles[1][:], in_=x_view[1])
         nc.sync.dma_start(out=wd_raw[1][:], in_=wd_view[1])
         nc.sync.dma_start(out=x_tiles[2][:], in_=x_view[2])
+        nc.sync.dma_start(out=x_tiles[3][:], in_=x_view[3])
         nc.sync.dma_start(out=wu_raw[:], in_=w_up.rearrange("(p j) n -> p j n", j=4))
-        for g in range(3, N_GROUPS):
+        for g in range(4, N_GROUPS):
             nc.sync.dma_start(out=x_tiles[g][:], in_=x_view[g])
 
         warm = const.tile([P, 1], F32)
         nc.vector.memset(warm[:], 0.0)
         nc.scalar.activation(out=warm[:], in_=warm[:], func=ACT.Sin)
+        zeros = const.tile([P, K_PASS], BF16)
+        nc.vector.memset(zeros[:], 0.0)
 
         pos = const.tile([P, POS_GROUPS, GROUP], F32)
         nc.gpsimd.iota(pos[:], pattern=[[P * GROUP, POS_GROUPS], [1, GROUP]], base=0, channel_multiplier=GROUP, allow_small_or_imprecise_dtypes=True)
@@ -87,19 +90,18 @@ def tile_multilatentattention_pa_t_kernel(tc, x_bytes, x_scale, w_down, w_up, ou
         whole = const.tile(shape, I32, name="whole_then_wd", align_bytes=64)
         frac = const.tile(shape, F32)
         mag = const.tile([P, 2] + shape[1:], F32)
-        trig = const.tile([P, N_POS, 3, HALF], F32)
+        trig = const.tile([P, N_POS, 4, HALF], F32)
         halves = [slice(0, HALF // 8), slice(HALF // 8, HALF // 4)]
         for h in halves:
             nc.vector.tensor_scalar(out=whole[:, h], in0=turns[:, h], scalar1=-0.125, scalar2=None, op0=ALU.add)
         for h in halves:
             nc.vector.tensor_tensor(out=frac[:, h], in0=turns[:, h], in1=whole[:, h], op=ALU.subtract)
 
-        def table_args():
-            nc.scalar.activation(out=mag[:, 0], in_=frac[:], func=ACT.Abs, scale=2 * math.pi)
-            nc.scalar.activation(out=mag[:, 1], in_=frac[:], func=ACT.Abs, scale=2 * math.pi, bias=-math.pi / 2)
+        def table_arg(c):
+            nc.scalar.activation(out=mag[:, c], in_=frac[:], func=ACT.Abs, scale=2 * math.pi, bias=-c * math.pi / 2)
 
         def tables():
-            for c, arg, sign in ((0, 0, 1.0), (1, 1, -1.0), (2, 1, 1.0)):
+            for c, arg, sign in ((0, 0, 1.0), (1, 1, 1.0), (2, 1, -1.0), (3, 0, 1.0)):
                 nc.scalar.activation(
                     out=trig[:, :, c].rearrange("p n (b a) -> p n b a", a=4),
                     in_=mag[:, arg].rearrange("p b n a -> p n b a"),
@@ -109,19 +111,17 @@ def tile_multilatentattention_pa_t_kernel(tc, x_bytes, x_scale, w_down, w_up, ou
         wd_grp = const.tile([P, 2, DL * 4], BF16, align_bytes=64, name="whole_then_wd")
         wd_codes = const.tile([P, 2, DL], U32, align_bytes=64)
         wd_scales = const.tile([P, 2, DL], U8, align_bytes=64)
-        wu_main_grp = const.tile([P, 2, H, DH, 4], BF16, align_bytes=64)
-        wu_rope_grp = const.tile([P, H, DR, 4], BF16, align_bytes=64)
         wu_main_codes = const.tile([P, 4 * DH], U32, align_bytes=64)
         wu_main_scales = const.tile([P, 4 * DH], U8, align_bytes=64)
         wu_rope_codes = const.tile([P, H * DR], U32, align_bytes=64)
         wu_rope_scales = const.tile([P, H * DR], U8, align_bytes=64)
+        wu_grp = {}
+
+        def group(out, in0):
+            nc.gpsimd.tensor_scalar(out=out, in0=in0, scalar1=1.0, scalar2=0.0, op0=ALU.mult, op1=ALU.add)
 
         def group_down(g):
-            nc.gpsimd.tensor_scalar(
-                out=wd_grp[:, g].rearrange("p (t m j) -> p t m j", t=4, j=4),
-                in0=wd_raw[g][:].rearrange("p j (m t) -> p t m j", t=4),
-                scalar1=1.0, scalar2=0.0, op0=ALU.mult, op1=ALU.add,
-            )
+            group(wd_grp[:, g].rearrange("p (t m j) -> p t m j", t=4, j=4), wd_raw[g][:].rearrange("p j (m t) -> p t m j", t=4))
 
         def quant_down():
             nc.vector.quantize_mx(
@@ -130,21 +130,29 @@ def tile_multilatentattention_pa_t_kernel(tc, x_bytes, x_scale, w_down, w_up, ou
                 in_=wd_grp[:].rearrange("p g c -> p (g c)"),
             )
 
-        def group_up():
-            up = wu_raw[:].rearrange("p j (h f) -> p h f j", h=H)
-            for dst, src in (
-                (wu_main_grp[:, 0], up[:, :, 0:DH, :]),
-                (wu_main_grp[:, 1], up[:, :, DH + DR:, :]),
-                (wu_rope_grp[:], up[:, :, DH:DH + DR, :]),
-            ):
-                nc.scalar.copy(out=dst, in_=src)
+        up = wu_raw[:].rearrange("p j (h f) -> p h f j", h=H)
+
+        def spent_room(spent):
+            return xg[spent][0][:].rearrange("p i g c -> p (i g c)")
+
+        def group_up(spent, spent_before):
+            wu_grp[0] = spent_room(spent)[:, 0:16 * DH]
+            wu_grp[1] = spent_room(spent_before)[:, 0:4 * H * DR]
+            main_grp = wu_grp[0].rearrange("p (a h f j) -> p a h f j", a=2, h=H, j=4)
+            group(main_grp[:, 0], up[:, :, 0:DH, :])
+            group(main_grp[:, 1], up[:, :, DH + DR:, :])
+            group(wu_grp[1].rearrange("p (h f j) -> p h f j", h=H, j=4), up[:, :, DH:DH + DR, :])
 
         def quant_up():
-            nc.vector.quantize_mx(out=wu_main_codes[:].bitcast(FP8X4), scales=wu_main_scales[:], in_=wu_main_grp[:].rearrange("p a h f j -> p (a h f j)"))
-            nc.vector.quantize_mx(out=wu_rope_codes[:].bitcast(FP8X4), scales=wu_rope_scales[:], in_=wu_rope_grp[:].rearrange("p h f j -> p (h f j)"))
+            nc.vector.quantize_mx(out=wu_rope_codes[:].bitcast(FP8X4), scales=wu_rope_scales[:], in_=wu_grp[1])
+            nc.vector.quantize_mx(out=wu_main_codes[:].bitcast(FP8X4), scales=wu_main_scales[:], in_=wu_grp[0])
+
+        def warm_up(count):
+            bank = psum.tile([P, K_PASS], F32, name="product")
+            for i in range(count):
+                nc.tensor.matmul(out=bank[:], lhsT=zeros[:, 0:P], rhs=zeros[:], start=True, stop=True)
 
         xbf = {}
-        aside = {}
         xt = {}
         xg = {}
         xc = {}
@@ -155,59 +163,66 @@ def tile_multilatentattention_pa_t_kernel(tc, x_bytes, x_scale, w_down, w_up, ou
         rope = {}
         kv = {}
         spill = {}
-        by_cos = {}
-        by_sin = {}
+        products = {}
 
-        def x_bytes_of(s):
-            return x_tiles[s // 2][:, 2 * (s % 2):2 * (s % 2) + 2].rearrange("p i d -> p (i d)").bitcast(FP8)
+        def x_bytes_of(n, count):
+            return x_tiles[n // GROUP][:, n % GROUP:n % GROUP + count].rearrange("p i d -> p (i d)").bitcast(FP8)
 
-        def widen(s, lo, hi):
-            if lo == 0:
-                xbf[s] = work.tile([P, 2 * D], BF16, name="xbf", bufs=6)
-            nc.scalar.copy(out=xbf[s][:, lo:hi], in_=x_bytes_of(s)[:, lo:hi])
+        def widen(n, count=2, parts=1):
+            wide = work.tile([P, count, D], BF16, name="xbf", bufs=8)
+            width = count * D // parts
+            for part in range(parts):
+                cols = slice(part * width, (part + 1) * width)
+                nc.scalar.copy(out=wide[:].rearrange("p i d -> p (i d)")[:, cols], in_=x_bytes_of(n, count)[:, cols])
+            for i in range(count):
+                xbf[n + i] = wide[:, i]
 
-        def widen_aside(s, spent):
-            aside[s] = xg[spent][:, 0].rearrange("p g c -> p (g c)")
-            nc.gpsimd.tensor_copy(out=aside[s], in_=x_bytes_of(s)[:, D:])
+        def widen_aside(n, count, spent, lo=0):
+            wide = xg[spent][0][:, lo:lo + count].rearrange("p i g c -> p i (g c)")
+            nc.gpsimd.tensor_copy(out=wide.rearrange("p i d -> p (i d)"), in_=x_bytes_of(n, count))
+            for i in range(count):
+                xbf[n + i] = wide[:, i]
 
-        def turn(s, i, passes=(0, 1)):
+        def turn(n, passes=(0, 1)):
             bank = psum.tile([P, 2, 2, P], F32, name="xt", bufs=TURN_BANKS)
-            xt[s, i, passes[0]] = bank
+            xt[n, passes[0]] = bank
             for g in passes:
-                if s in aside and i == 1:
-                    values = aside[s][:, g * K_PASS:(g + 1) * K_PASS]
-                else:
-                    values = xbf[s][:, i * D + g * K_PASS:i * D + (g + 1) * K_PASS]
+                values = xbf[n][:, g * K_PASS:(g + 1) * K_PASS]
                 for u in range(2):
                     nc.tensor.transpose(bank[:, u, g, :], values.bitcast(F32)[:, u::2], ident[:])
 
-        def empty_turn(s, i, passes=(0, 1)):
-            if i == 0 and passes[0] == 0:
-                xg[s] = work.tile([P, 2, 2, P * 4], BF16, name="xg", align_bytes=64, bufs=5)
+        def open_x(lo, count):
+            values = work.tile([P, count, 2, P * 4], BF16, name="xg", align_bytes=64, bufs=4)
+            codes = work.tile([P, count, 2, P], U32, name="xcodes", align_bytes=64)
+            scales = work.tile([P, count, 2, P], U8, name="xscales", align_bytes=64)
+            for i in range(count):
+                xg[lo + i] = (values, i)
+                xc[lo + i] = (codes, scales)
+
+        def scale_x(n, passes=(0, 1)):
+            values, i = xg[n]
             gs = slice(passes[0], passes[-1] + 1)
             nc.vector.tensor_tensor(
-                out=xg[s][:, i, gs].rearrange("p g (r u e) -> p g r u e", u=2, e=2),
-                in0=xt[s, i, passes[0]][:, :, gs].bitcast(BF16).rearrange("p u g (r e) -> p g r u e", e=2),
+                out=values[:, i, gs].rearrange("p g (r u e) -> p g r u e", u=2, e=2),
+                in0=xt[n, passes[0]][:, :, gs].bitcast(BF16).rearrange("p u g (r e) -> p g r u e", e=2),
                 in1=scale_cols[:, gs].rearrange("p g (u e) -> p g u e", u=2).unsqueeze(2).to_broadcast([P, len(passes), P, 2, 2]),
                 op=ALU.mult,
             )
 
-        def quant_x(s, lo=0, n=2):
-            if lo == 0:
-                codes = work.tile([P, 2, 2, P], U32, name="xcodes", align_bytes=64, bufs=5)
-                scales = work.tile([P, 2, 2, P], U8, name="xscales", align_bytes=64, bufs=5)
-                xc[s] = (codes, scales)
-            codes, scales = xc[s]
+        def quant_x(n, count):
+            values, i = xg[n]
+            codes, scales = xc[n]
             nc.vector.quantize_mx(
-                out=codes[:, lo:lo + n].rearrange("p i g r -> p (i g r)").bitcast(FP8X4),
-                scales=scales[:, lo:lo + n].rearrange("p i g r -> p (i g r)"),
-                in_=xg[s][:, lo:lo + n].rearrange("p i g c -> p (i g c)"),
+                out=codes[:, i:i + count].rearrange("p i g r -> p (i g r)").bitcast(FP8X4),
+                scales=scales[:, i:i + count].rearrange("p i g r -> p (i g r)"),
+                in_=values[:, i:i + count].rearrange("p i g c -> p (i g c)"),
             )
 
-        def down(s, i):
-            bank = psum.tile([P, 4, P], F32, name="lat")
-            lat[s, i] = bank
-            codes, scales = xc[s]
+        def down(n):
+            bank = psum.tile([P, 4, P], F32, name="product")
+            lat[n] = bank
+            codes, scales = xc[n]
+            i = xg[n][1]
             for t in range(4):
                 for g in range(2):
                     nc.tensor.matmul_mx(
@@ -220,25 +235,28 @@ def tile_multilatentattention_pa_t_kernel(tc, x_bytes, x_scale, w_down, w_up, ou
                         stop=(g == 1),
                     )
 
-        def empty_down(s, i):
+        def empty_down(n, engine=None):
+            g, i = divmod(n, GROUP)
             if i == 0:
-                lg[s] = work.tile([P, 2, P, 4], BF16, name="lg", align_bytes=64, bufs=4)
-            nc.scalar.copy(out=lg[s][:, i], in_=lat[s, i][:].rearrange("p t r -> p r t"))
+                lg[g] = work.tile([P, GROUP, P, 4], BF16, name="lg", align_bytes=64)
+            nc.scalar.copy(out=lg[g][:, i], in_=lat[n][:].rearrange("p t r -> p r t"))
 
-        def quant_lat(s, lo=0, n=2):
-            if lo == 0:
-                codes = work.tile([P, 2, P], U32, name="lcodes", align_bytes=64, bufs=4)
-                scales = work.tile([P, 2, P], U8, name="lscales", align_bytes=64, bufs=4)
-                lc[s] = (codes, scales)
-            codes, scales = lc[s]
+        def quant_lat(n, count):
+            g, i = divmod(n, GROUP)
+            if i == 0:
+                codes = work.tile([P, GROUP, P], U32, name="lcodes", align_bytes=64)
+                scales = work.tile([P, GROUP, P], U8, name="lscales", align_bytes=64)
+                lc[g] = (codes, scales)
+            codes, scales = lc[g]
             nc.vector.quantize_mx(
-                out=codes[:, lo:lo + n].rearrange("p i r -> p (i r)").bitcast(FP8X4),
-                scales=scales[:, lo:lo + n].rearrange("p i r -> p (i r)"),
-                in_=lg[s][:, lo:lo + n].rearrange("p i r t -> p (i r t)"),
+                out=codes[:, i:i + count].rearrange("p i r -> p (i r)").bitcast(FP8X4),
+                scales=scales[:, i:i + count].rearrange("p i r -> p (i r)"),
+                in_=lg[g][:, i:i + count].rearrange("p i r t -> p (i r t)"),
             )
 
-        def expand(out, s, i, w_codes, w_scales):
-            codes, scales = lc[s]
+        def expand(out, n, w_codes, w_scales):
+            g, i = divmod(n, GROUP)
+            codes, scales = lc[g]
             nc.tensor.matmul_mx(
                 out=out,
                 lhsT=codes[:, i].bitcast(FP8X4), lhsT_scale=scales[:, i],
@@ -246,218 +264,229 @@ def tile_multilatentattention_pa_t_kernel(tc, x_bytes, x_scale, w_down, w_up, ou
                 start=True, stop=True,
             )
 
-        def expand_main(s, i, tag="main", bufs=2):
-            main[s, i] = psum.tile([P, 4, DH], F32, name=tag, bufs=bufs)
-            expand(main[s, i][:].rearrange("p a f -> p (a f)"), s, i, wu_main_codes, wu_main_scales)
+        def expand_main(n, tag="product"):
+            main[n] = psum.tile([P, 4, DH], F32, name=tag)
+            expand(main[n][:].rearrange("p a f -> p (a f)"), n, wu_main_codes, wu_main_scales)
 
-        def expand_rope(s, i, tag="rope", bufs=1):
-            if i == 0:
-                rope[s] = psum.tile([P, 2, H, 2, HALF], F32, name=tag, bufs=bufs)
-            expand(rope[s][:, i].rearrange("p h a f -> p (h a f)"), s, i, wu_rope_codes, wu_rope_scales)
+        def expand_rope(n, count, tag="product"):
+            rope[n] = psum.tile([P, count, H * DR], F32, name=tag)
+            for i in range(count):
+                expand(rope[n][:, i], n + i, wu_rope_codes, wu_rope_scales)
 
-        def out_tile(s):
-            if s not in kv:
-                kv[s] = outp.tile([P, 2, 2, H, DH + DR], F32, name="kv")
-            return kv[s]
+        def out_tile(g):
+            if g not in kv:
+                kv[g] = outp.tile([P, 2, GROUP, H, DH + DR], F32, name="kv")
+            return kv[g]
 
-        def empty_main(s, i):
-            nc.scalar.copy(out=out_tile(s)[:, :, i, :, 0:DH], in_=main[s, i][:].rearrange("p (a h) f -> p a h f", h=H))
+        def empty_main(n, on_vector=False):
+            g, i = divmod(n, GROUP)
+            out = out_tile(g)[:, :, i, :, 0:DH]
+            bank = main[n][:].rearrange("p (a h) f -> p a h f", h=H)
+            if on_vector:
+                nc.vector.tensor_copy(out=out, in_=bank)
+            else:
+                nc.scalar.copy(out=out, in_=bank)
 
-        def trig_of(s):
-            return trig[:, (2 * s) % N_POS:(2 * s) % N_POS + 2]
+        def spill_rope(n, lo, count):
+            spill[n] = work.tile([P, count, H * DR], F32, name="spill", bufs=2)
+            nc.scalar.copy(out=spill[n][:], in_=rope[n][:, lo:lo + count])
 
-        def cos_of(s):
-            return trig_of(s)[:, :, 0].unsqueeze(2).to_broadcast([P, 2, 2 * H, HALF])
+        def open_products(n, count, spent=None):
+            if spent is None:
+                room = work.tile([P, count * H * 2 * DR], F32, name="products", bufs=2)
+                room = room[:]
+            else:
+                room = spent_room(spent).bitcast(F32)[:, 0:count * H * 2 * DR]
+            products[n] = room.rearrange("p (i h a c f) -> p i h a c f", h=H, a=2, c=2, f=HALF)
 
-        def spill_rope(s):
-            spill[s] = work.tile([P, 2, 2 * H, HALF], F32, name="spill")
-            nc.scalar.copy(out=spill[s][:], in_=rope[s][:].rearrange("p i h a f -> p i (h a) f"))
-
-        def rope_cos_beside(s, spent):
-            by_cos[s] = xg[spent][:, 0, 0].bitcast(F32).rearrange("p (i c f) -> p i c f", i=2, f=HALF)
-            nc.gpsimd.tensor_tensor(out=by_cos[s], in0=spill[s][:], in1=cos_of(s), op=ALU.mult)
-
-        def rope_cos(s):
-            product = work.tile([P, 2, 2 * H, HALF], F32, name="by_cos")
-            by_cos[s] = product[:]
-            nc.vector.tensor_tensor(out=by_cos[s], in0=rope[s][:].rearrange("p i h a f -> p i (h a) f"), in1=cos_of(s), op=ALU.mult)
-
-        def rope_sin(s):
-            by_sin[s] = work.tile([P, 2, H, 2, HALF], F32, name="by_sin")
-            nc.vector.tensor_tensor(
-                out=by_sin[s][:],
-                in0=rope[s][:, :, :, ::-1, :],
-                in1=trig_of(s)[:, :, 1:3].unsqueeze(2).to_broadcast([P, 2, H, 2, HALF]),
+        def rope_products(engine, source, n, lo, count):
+            shape = [P, count, H, 2, 2, HALF]
+            first = (n + lo) % N_POS
+            engine.tensor_tensor(
+                out=products[n][:, lo:lo + count],
+                in0=source.rearrange("p i (h a f) -> p i h a f", h=H, a=2).unsqueeze(4).to_broadcast(shape),
+                in1=trig[:, first:first + count].rearrange("p i (a c) f -> p i a c f", a=2).unsqueeze(2).to_broadcast(shape),
                 op=ALU.mult,
             )
 
-        def rope_add(s, engine):
+        def products_aside(n, lo, count):
+            rope_products(nc.gpsimd, spill[n][:], n, lo, count)
+
+        def products_direct(n, lo, count):
+            rope_products(nc.vector, rope[n][:, lo:lo + count], n, lo, count)
+
+        def rope_add(engine, n, count, lo=0):
+            g, i = divmod(n + lo, GROUP)
             engine.tensor_tensor(
-                out=out_tile(s)[:, 0, :, :, DH:],
-                in0=by_cos[s].rearrange("p i (h a) f -> p i h (a f)", h=H),
-                in1=by_sin[s][:].rearrange("p i h a f -> p i h (a f)"),
+                out=out_tile(g)[:, 0, i:i + count, :, DH:].rearrange("p i h f -> p (i h) f"),
+                in0=products[n][:, lo:lo + count, :, 0].rearrange("p i h c f -> p (i h) (c f)"),
+                in1=products[n][:, lo:lo + count, :, 1].rearrange("p i h c f -> p (i h) (c f)"),
                 op=ALU.add,
             )
 
-        def store_v(s, lo=0, n=2):
-            first = 2 * (s % 2) + lo
-            nc.sync.dma_start(out=v_view[s // 2][:, H * first:H * (first + n)], in_=kv[s][:, 1, lo:lo + n, :, 0:DH].rearrange("p i h f -> p (i h) f"))
+        def store_v(n, count):
+            g, i = divmod(n, GROUP)
+            nc.sync.dma_start(out=v_view[g][:, H * i:H * (i + count)], in_=kv[g][:, 1, i:i + count, :, 0:DH].rearrange("p i h f -> p (i h) f"))
 
-        def store_k(s):
-            first = 2 * (s % 2)
-            nc.sync.dma_start(out=k_view[s // 2][:, first:first + 2], in_=kv[s][:, 0].rearrange("p i h f -> p i (h f)"))
+        def store_k(n, count):
+            g, i = divmod(n, GROUP)
+            nc.sync.dma_start(out=k_view[g][:, i:i + count], in_=kv[g][:, 0, i:i + count].rearrange("p i h f -> p i (h f)"))
 
-        widen(0, 0, K_PASS)
-        widen(0, K_PASS, D)
-        widen(0, D, 2 * D)
+        widen(0, 1, parts=2)
+        widen(1, 1)
         group_down(0)
         group_down(1)
-        widen(1, 0, 2 * D)
-        table_args()
-        widen(2, 0, 2 * D)
+        widen(2)
+        table_arg(0)
+        table_arg(1)
+        widen(4)
+        widen(6)
+        widen(8)
+        widen(10)
         tables()
-        widen(3, 0, 2 * D)
-        group_up()
-        widen(4, 0, 2 * D)
-        turn(0, 0, (0,))
-        turn(0, 0, (1,))
-        turn(0, 1)
-        empty_turn(0, 0, (0,))
-        empty_turn(0, 0, (1,))
-        turn(1, 0)
-        empty_turn(0, 1)
-        turn(1, 1)
-        for s in (1, 2):
-            for i in range(2):
-                empty_turn(s, i)
-                turn(s + 1, i)
+        widen(12)
+        open_x(0, 4)
+        open_x(4, 2)
+        turn(0, (0,))
+        turn(0, (1,))
+        turn(1)
+        turn(2)
+        scale_x(0, (0,))
+        turn(3)
+        scale_x(0, (1,))
+        for n in range(1, 5):
+            turn(n + 3)
+            scale_x(n)
+        warm_up(3)
+        scale_x(5)
+        turn(8)
+        turn(9)
+        widen(14)
+        widen(16)
         quant_down()
-        quant_x(0)
-        quant_x(1)
-        down(0, 0)
-        down(0, 1)
-        quant_up()
-        quant_x(2)
-        for i in range(2):
-            empty_down(0, i)
-            down(1, i)
-        for i in range(2):
-            empty_down(1, i)
+        quant_x(0, 4)
+        quant_x(4, 2)
+        group_up(4, 0)
+        for n in range(2):
+            down(n)
+            empty_down(n)
 
-        first_round, tail = 3, PAIRS - 5
-
-        def spilled(s):
-            return s % SHARE_PERIOD != 0 and s < tail
-
-        for now in range(first_round, PAIRS - 2):
-            wide, mid, old, done = now + 2, now - 1, now - 2, now - 3
-            empty_turn(now, 0)
-            if now == first_round:
-                quant_lat(0)
+        wide = list(range(18, N_TILES))
+        for r in range(1, N_GROUPS - 1):
+            now = GROUP * r + 2
+            mid = now - GROUP
+            old = GROUP * (r - 2)
+            ahead = now + GROUP
+            last = r == N_GROUPS - 2
+            open_x(now, GROUP)
+            if old >= 0:
+                expand_rope(old, GROUP)
+                spill_rope(old, 0, GROUP)
+                open_products(old, GROUP, mid)
+                products_aside(old, 0, GROUP)
+                rope_add(nc.gpsimd, old, GROUP)
+                if old > 0:
+                    empty_main(old - 1)
+                    store_v(old - GROUP, GROUP)
+                    store_k(old - GROUP, GROUP)
                 for i in range(2):
-                    expand_rope(0, i)
-                    expand_main(0, i)
-                    empty_main(0, i)
-                store_v(0)
-            empty_turn(now, 1)
-            turn(now + 1, 0)
-            turn(now + 1, 1)
-            quant_lat(old)
-            quant_x(now)
-            if spilled(done):
-                rope_cos_beside(done, now)
-            else:
-                widen_aside(wide, now)
-                rope_cos(done)
-            rope_sin(done)
-            rope_add(done, nc.gpsimd)
-            store_k(done)
-            down(mid, 0)
-            down(mid, 1)
-            for i in range(2):
-                expand_main(old, i)
-            for i in range(2):
-                expand_rope(old, i)
-            widen(wide, 0, D if wide in aside else 2 * D)
-            empty_down(mid, 0)
-            empty_down(mid, 1)
-            empty_main(old, 0)
-            if spilled(old):
-                spill_rope(old)
-            empty_main(old, 1)
-            store_v(old)
+                    expand_main(old + i)
+                    empty_main(old + i)
+                turn(now + 2)
+                turn(now + 3)
+            if wide and r > 1:
+                widen(wide.pop(0), 1)
+            for n in range(mid, mid + GROUP):
+                down(n)
+                empty_down(n)
+            scale_x(now)
+            scale_x(now + 1)
+            turn(ahead)
+            turn(ahead + 1)
+            for i in range(3 if r == 1 else 2):
+                if wide:
+                    widen(wide.pop(0), 1)
+            if old >= 0:
+                expand_main(old + 2)
+                expand_main(old + 3)
+                empty_main(old + 2)
+            scale_x(now + 2)
+            scale_x(now + 3)
+            quant_lat(old + GROUP, GROUP)
+            if r == 1:
+                quant_up()
+            quant_x(now, GROUP)
+        empty_main(19)
+        store_v(16, GROUP)
+        store_k(16, GROUP)
 
-        a, b, c, d, e = range(tail, PAIRS)
-        empty_turn(d, 0)
-        empty_turn(d, 1)
-        for i in range(2):
-            down(c, i)
-            empty_down(c, i)
-        turn(e, 0)
-        turn(e, 1)
-        quant_lat(b)
-        quant_x(d)
-        quant_lat(c)
-        rope_cos(a)
-        rope_sin(a)
-        rope_add(a, nc.gpsimd)
-        for i in range(2):
-            expand_main(b, i)
-            empty_main(b, i)
-        for i in range(2):
-            expand_rope(b, i)
-        store_v(b)
-        store_k(a)
-        for i in range(2):
-            down(d, i)
-            empty_down(d, i)
-        for i in range(2):
-            expand_rope(c, i, "xt", TURN_BANKS)
-            expand_main(c, i)
-        empty_turn(e, 0)
-        rope_cos(b)
-        quant_x(e, 0, 1)
-        rope_sin(b)
-        rope_add(b, nc.gpsimd)
-        down(e, 0)
-        empty_main(c, 0)
-        store_v(c, 0, 1)
-        store_k(b)
-        empty_down(e, 0)
-        empty_main(c, 1)
-        store_v(c, 1, 1)
-        empty_turn(e, 1)
-        quant_lat(d)
-        quant_x(e, 1, 1)
-        quant_lat(e, 0, 1)
-        rope_cos(c)
-        rope_sin(c)
-        rope_add(c, nc.vector)
-        for i in range(2):
-            expand_rope(d, i)
-        expand_main(d, 0)
-        down(e, 1)
-        expand_main(d, 1)
-        empty_main(d, 0)
-        store_v(d, 0, 1)
-        store_k(c)
-        empty_down(e, 1)
-        expand_rope(e, 0, "xt", TURN_BANKS)
-        expand_main(e, 0, "xt", TURN_BANKS)
-        rope_cos(d)
-        rope_sin(d)
-        quant_lat(e, 1, 1)
-        rope_add(d, nc.vector)
-        empty_main(d, 1)
-        store_v(d, 1, 1)
-        store_k(d)
-        empty_main(e, 0)
-        store_v(e, 0, 1)
-        expand_rope(e, 1)
-        expand_main(e, 1)
-        empty_main(e, 1)
-        store_v(e, 1, 1)
-        rope_cos(e)
-        rope_sin(e)
-        rope_add(e, nc.vector)
-        store_k(e)
+        open_x(30, 2)
+        expand_rope(20, GROUP, "xt")
+        for n in (20, 21):
+            expand_main(n)
+            empty_main(n)
+        down(26)
+        down(27)
+        expand_main(22)
+        expand_main(23)
+        empty_down(26)
+        empty_down(27)
+        empty_main(22)
+        empty_main(23)
+        open_products(20, GROUP)
+        products_direct(20, 0, GROUP)
+        rope_add(nc.gpsimd, 20, GROUP)
+        store_v(20, 2)
+        store_k(20, 2)
+        store_v(22, 2)
+        store_k(22, 2)
+        scale_x(30)
+        scale_x(31)
+        for n in (28, 29):
+            down(n)
+            empty_down(n)
+        quant_lat(24, GROUP)
+        quant_x(30, 2)
+        quant_lat(28, 2)
+        expand_rope(24, GROUP, "xt")
+        for n in (24, 25):
+            expand_main(n)
+            empty_main(n)
+        store_v(24, 2)
+        down(30)
+        down(31)
+        expand_main(26)
+        expand_rope(28, 2, "xt")
+        expand_main(27)
+        expand_main(28, "xt")
+        empty_down(30)
+        empty_down(31)
+        empty_main(26)
+        empty_main(27)
+        expand_main(29)
+        empty_main(29)
+        open_products(24, GROUP)
+        products_direct(24, 0, 2)
+        products_direct(24, 2, 2)
+        rope_add(nc.vector, 24, 2)
+        store_k(24, 2)
+        rope_add(nc.vector, 24, 2, 2)
+        open_products(28, 2)
+        products_direct(28, 0, 2)
+        store_v(26, 2)
+        store_k(26, 2)
+        quant_lat(30, 2)
+        rope_add(nc.vector, 28, 2)
+        empty_main(28, on_vector=True)
+        store_k(28, 2)
+        store_v(28, 2)
+        expand_rope(30, 2, "xt")
+        expand_main(30)
+        expand_main(31)
+        open_products(30, 2)
+        products_direct(30, 0, 2)
+        empty_main(30)
+        empty_main(31)
+        rope_add(nc.vector, 30, 2)
+        store_k(30, 2)
+        store_v(30, 2)

@@ -28,6 +28,8 @@ N_POS = POS_GROUPS * GROUP
 N_TILES = N_GROUPS * GROUP
 TURN_BANKS = 4
 PRODUCT_BANKS = 4
+SCALE_RUN = 32
+DENSE_V = 5
 
 
 def tile_multilatentattention_pa_t_kernel(tc, x_bytes, x_scale, w_down, w_up, out_k, out_v):
@@ -94,6 +96,8 @@ def tile_multilatentattention_pa_t_kernel(tc, x_bytes, x_scale, w_down, w_up, ou
         halves = [slice(0, HALF // 8), slice(HALF // 8, HALF // 4)]
         for h in halves:
             nc.vector.tensor_scalar(out=whole[:, h], in0=turns[:, h], scalar1=-0.125, scalar2=None, op0=ALU.add)
+        scale_run = const.tile([P, 2, SCALE_RUN, 4], F32)
+        nc.vector.tensor_copy(out=scale_run[:], in_=scale_cols[:].unsqueeze(2).to_broadcast([P, 2, SCALE_RUN, 4]))
         for h in halves:
             nc.vector.tensor_tensor(out=frac[:, h], in0=turns[:, h], in1=whole[:, h], op=ALU.subtract)
 
@@ -184,12 +188,12 @@ def tile_multilatentattention_pa_t_kernel(tc, x_bytes, x_scale, w_down, w_up, ou
                 xbf[n + i] = wide[:, i]
 
         def turn(n, passes=(0, 1)):
-            bank = psum.tile([P, 2, 2, P], F32, name="xt", bufs=TURN_BANKS)
+            bank = psum.tile([P, 2, P, 2], F32, name="xt", bufs=TURN_BANKS)
             xt[n, passes[0]] = bank
             for g in passes:
                 values = xbf[n][:, g * K_PASS:(g + 1) * K_PASS]
                 for u in range(2):
-                    nc.tensor.transpose(bank[:, u, g, :], values.bitcast(F32)[:, u::2], ident[:])
+                    nc.tensor.transpose(bank[:, g, :, u], values.bitcast(F32)[:, u::2], ident[:])
 
         def open_x(lo, count):
             values = work.tile([P, count, 2, P * 4], BF16, name="xg", align_bytes=64, bufs=4)
@@ -203,9 +207,9 @@ def tile_multilatentattention_pa_t_kernel(tc, x_bytes, x_scale, w_down, w_up, ou
             values, i = xg[n]
             gs = slice(passes[0], passes[-1] + 1)
             nc.vector.tensor_tensor(
-                out=values[:, i, gs].rearrange("p g (r u e) -> p g r u e", u=2, e=2),
-                in0=xt[n, passes[0]][:, :, gs].bitcast(BF16).rearrange("p u g (r e) -> p g r u e", e=2),
-                in1=scale_cols[:, gs].rearrange("p g (u e) -> p g u e", u=2).unsqueeze(2).to_broadcast([P, len(passes), P, 2, 2]),
+                out=values[:, i, gs].rearrange("p g (a c) -> p g a c", c=4 * SCALE_RUN),
+                in0=xt[n, passes[0]][:, gs].rearrange("p g r u -> p g (r u)").bitcast(BF16).rearrange("p g (a c) -> p g a c", c=4 * SCALE_RUN),
+                in1=scale_run[:, gs].rearrange("p g r t -> p g (r t)").unsqueeze(2).to_broadcast([P, len(passes), P // SCALE_RUN, 4 * SCALE_RUN]),
                 op=ALU.mult,
             )
 
@@ -278,14 +282,23 @@ def tile_multilatentattention_pa_t_kernel(tc, x_bytes, x_scale, w_down, w_up, ou
                 kv[g] = outp.tile([P, 2, GROUP, H, DH + DR], F32, name="kv")
             return kv[g]
 
+        def v_rows(g):
+            if g < DENSE_V:
+                return out_tile(g)[:, 1, :, :, 0:DH]
+            return out_tile(g)[:, 1].rearrange("p i h f -> p (i h f)")[:, 0:GROUP * H * DH].rearrange("p (i h f) -> p i h f", h=H, f=DH)
+
         def empty_main(n, on_vector=False):
             g, i = divmod(n, GROUP)
-            out = out_tile(g)[:, :, i, :, 0:DH]
             bank = main[n][:].rearrange("p (a h) f -> p a h f", h=H)
-            if on_vector:
-                nc.vector.tensor_copy(out=out, in_=bank)
+            if g < DENSE_V:
+                parts = [(out_tile(g)[:, :, i, :, 0:DH], bank)]
             else:
-                nc.scalar.copy(out=out, in_=bank)
+                parts = [(v_rows(g)[:, i], bank[:, 1]), (out_tile(g)[:, 0, i, :, 0:DH], bank[:, 0])]
+            for out, in_ in parts:
+                if on_vector:
+                    nc.vector.tensor_copy(out=out, in_=in_)
+                else:
+                    nc.scalar.copy(out=out, in_=in_)
 
         def spill_rope(n, lo, count):
             spill[n] = work.tile([P, count, H * DR], F32, name="spill", bufs=2)
@@ -326,7 +339,7 @@ def tile_multilatentattention_pa_t_kernel(tc, x_bytes, x_scale, w_down, w_up, ou
 
         def store_v(n, count):
             g, i = divmod(n, GROUP)
-            nc.sync.dma_start(out=v_view[g][:, H * i:H * (i + count)], in_=kv[g][:, 1, i:i + count, :, 0:DH].rearrange("p i h f -> p (i h) f"))
+            nc.sync.dma_start(out=v_view[g][:, H * i:H * (i + count)], in_=v_rows(g)[:, i:i + count].rearrange("p i h f -> p (i h) f"))
 
         def store_k(n, count):
             g, i = divmod(n, GROUP)
@@ -372,12 +385,11 @@ def tile_multilatentattention_pa_t_kernel(tc, x_bytes, x_scale, w_down, w_up, ou
             empty_down(n)
 
         wide = list(range(18, N_TILES))
-        for r in range(1, N_GROUPS - 1):
+        for r in range(1, N_GROUPS - 2):
             now = GROUP * r + 2
             mid = now - GROUP
             old = GROUP * (r - 2)
             ahead = now + GROUP
-            last = r == N_GROUPS - 2
             open_x(now, GROUP)
             if old >= 0:
                 expand_rope(old, GROUP)
@@ -416,9 +428,40 @@ def tile_multilatentattention_pa_t_kernel(tc, x_bytes, x_scale, w_down, w_up, ou
             if r == 1:
                 quant_up()
             quant_x(now, GROUP)
-        empty_main(19)
+
+        open_x(26, GROUP)
+        expand_rope(16, GROUP)
+        spill_rope(16, 0, GROUP)
+        open_products(16, GROUP, 22)
+        products_aside(16, 0, GROUP)
+        rope_add(nc.gpsimd, 16, GROUP)
+        empty_main(15)
+        store_v(12, GROUP)
+        store_k(12, GROUP)
+        for n in (16, 17):
+            expand_main(n)
+            empty_main(n)
+        turn(28)
+        turn(29)
+        for n in (22, 23):
+            down(n)
+            empty_down(n)
+        for n in (18, 19):
+            expand_main(n)
+            empty_main(n)
         store_v(16, GROUP)
         store_k(16, GROUP)
+        for n in (24, 25):
+            down(n)
+            empty_down(n)
+        scale_x(26)
+        scale_x(27)
+        turn(30)
+        turn(31)
+        scale_x(28)
+        scale_x(29)
+        quant_lat(20, GROUP)
+        quant_x(26, GROUP)
 
         open_x(30, 2)
         expand_rope(20, GROUP, "xt")
@@ -448,21 +491,21 @@ def tile_multilatentattention_pa_t_kernel(tc, x_bytes, x_scale, w_down, w_up, ou
         quant_lat(24, GROUP)
         quant_x(30, 2)
         quant_lat(28, 2)
+        expand_main(24)
         expand_rope(24, GROUP, "xt")
-        for n in (24, 25):
+        for n in (25, 26, 27):
             expand_main(n)
+        for n in (24, 25):
             empty_main(n)
         store_v(24, 2)
         down(30)
         down(31)
-        expand_main(26)
+        for n in (26, 27):
+            empty_main(n)
         expand_rope(28, 2, "xt")
-        expand_main(27)
         expand_main(28, "xt")
         empty_down(30)
         empty_down(31)
-        empty_main(26)
-        empty_main(27)
         expand_main(29)
         empty_main(29)
         open_products(24, GROUP)

@@ -67,8 +67,6 @@ def tile_multilatentattention_pa_t_kernel(tc, x_bytes, x_scale, w_down, w_up, ou
         warm = const.tile([P, 1], F32)
         nc.vector.memset(warm[:], 0.0)
         nc.scalar.activation(out=warm[:], in_=warm[:], func=ACT.Sin)
-        zeros = const.tile([P, K_PASS], BF16)
-        nc.vector.memset(zeros[:], 0.0)
 
         pos = const.tile([P, POS_GROUPS, GROUP], F32)
         nc.gpsimd.iota(pos[:], pattern=[[P * GROUP, POS_GROUPS], [1, GROUP]], base=0, channel_multiplier=GROUP, allow_small_or_imprecise_dtypes=True)
@@ -154,7 +152,7 @@ def tile_multilatentattention_pa_t_kernel(tc, x_bytes, x_scale, w_down, w_up, ou
         def warm_up(count):
             bank = psum.tile([P, K_PASS], F32, name="product")
             for i in range(count):
-                nc.tensor.matmul(out=bank[:], lhsT=zeros[:, 0:P], rhs=zeros[:], start=True, stop=True)
+                nc.tensor.matmul(out=bank[:], lhsT=xbf[6][:, 0:P], rhs=xbf[6][:, 0:K_PASS], start=True, stop=True)
 
         xbf = {}
         xt = {}
@@ -208,8 +206,8 @@ def tile_multilatentattention_pa_t_kernel(tc, x_bytes, x_scale, w_down, w_up, ou
             gs = slice(passes[0], passes[-1] + 1)
             nc.vector.tensor_tensor(
                 out=values[:, i, gs].rearrange("p g (a c) -> p g a c", c=4 * SCALE_RUN),
-                in0=xt[n, passes[0]][:, gs].rearrange("p g r u -> p g (r u)").bitcast(BF16).rearrange("p g (a c) -> p g a c", c=4 * SCALE_RUN),
-                in1=scale_run[:, gs].rearrange("p g r t -> p g (r t)").unsqueeze(2).to_broadcast([P, len(passes), P // SCALE_RUN, 4 * SCALE_RUN]),
+                in1=xt[n, passes[0]][:, gs].rearrange("p g r u -> p g (r u)").bitcast(BF16).rearrange("p g (a c) -> p g a c", c=4 * SCALE_RUN),
+                in0=scale_run[:, gs].rearrange("p g r t -> p g (r t)").unsqueeze(2).to_broadcast([P, len(passes), P // SCALE_RUN, 4 * SCALE_RUN]),
                 op=ALU.mult,
             )
 
@@ -451,13 +449,13 @@ def tile_multilatentattention_pa_t_kernel(tc, x_bytes, x_scale, w_down, w_up, ou
             empty_main(n)
         store_v(16, GROUP)
         store_k(16, GROUP)
-        for n in (24, 25):
-            down(n)
-            empty_down(n)
         scale_x(26)
         scale_x(27)
         turn(30)
         turn(31)
+        for n in (24, 25):
+            down(n)
+            empty_down(n)
         scale_x(28)
         scale_x(29)
         quant_lat(20, GROUP)
@@ -468,66 +466,58 @@ def tile_multilatentattention_pa_t_kernel(tc, x_bytes, x_scale, w_down, w_up, ou
         for n in (20, 21):
             expand_main(n)
             empty_main(n)
-        down(26)
-        down(27)
-        expand_main(22)
-        expand_main(23)
-        empty_down(26)
-        empty_down(27)
-        empty_main(22)
-        empty_main(23)
+        for n in range(26, 30):
+            down(n)
+            empty_down(n)
         open_products(20, GROUP)
         products_direct(20, 0, GROUP)
         rope_add(nc.gpsimd, 20, GROUP)
         store_v(20, 2)
         store_k(20, 2)
+        for n in (22, 23):
+            expand_main(n)
+            empty_main(n)
         store_v(22, 2)
         store_k(22, 2)
         scale_x(30)
         scale_x(31)
-        for n in (28, 29):
-            down(n)
-            empty_down(n)
         quant_lat(24, GROUP)
         quant_x(30, 2)
         quant_lat(28, 2)
         expand_main(24)
+        empty_main(24)
         expand_rope(24, GROUP, "xt")
-        for n in (25, 26, 27):
-            expand_main(n)
-        for n in (24, 25):
-            empty_main(n)
-        store_v(24, 2)
-        down(30)
-        down(31)
-        for n in (26, 27):
-            empty_main(n)
-        expand_rope(28, 2, "xt")
-        expand_main(28, "xt")
-        empty_down(30)
-        empty_down(31)
-        expand_main(29)
-        empty_main(29)
+        expand_main(25)
+        empty_main(25)
+        for n in (30, 31):
+            down(n)
+            empty_down(n)
         open_products(24, GROUP)
         products_direct(24, 0, 2)
         products_direct(24, 2, 2)
         rope_add(nc.vector, 24, 2)
-        store_k(24, 2)
         rope_add(nc.vector, 24, 2, 2)
-        open_products(28, 2)
-        products_direct(28, 0, 2)
+        store_v(24, 2)
+        store_k(24, 2)
+        expand_main(26, "xt")
+        expand_rope(28, 2, "xt")
+        for n in (27, 28, 29):
+            expand_main(n)
+            empty_main(n)
+        empty_main(26, on_vector=True)
         store_v(26, 2)
         store_k(26, 2)
         quant_lat(30, 2)
-        rope_add(nc.vector, 28, 2)
-        empty_main(28, on_vector=True)
-        store_k(28, 2)
-        store_v(28, 2)
+        open_products(28, 2)
+        products_direct(28, 0, 2)
         expand_rope(30, 2, "xt")
         expand_main(30)
         expand_main(31)
         open_products(30, 2)
         products_direct(30, 0, 2)
+        store_v(28, 2)
+        rope_add(nc.vector, 28, 2)
+        store_k(28, 2)
         empty_main(30)
         empty_main(31)
         rope_add(nc.vector, 30, 2)

@@ -206,8 +206,8 @@ def tile_multilatentattention_pa_t_kernel(tc, x_bytes, x_scale, w_down, w_up, ou
             gs = slice(passes[0], passes[-1] + 1)
             nc.vector.tensor_tensor(
                 out=values[:, i, gs].rearrange("p g (a c) -> p g a c", c=4 * SCALE_RUN),
-                in1=xt[n, passes[0]][:, gs].rearrange("p g r u -> p g (r u)").bitcast(BF16).rearrange("p g (a c) -> p g a c", c=4 * SCALE_RUN),
-                in0=scale_run[:, gs].rearrange("p g r t -> p g (r t)").unsqueeze(2).to_broadcast([P, len(passes), P // SCALE_RUN, 4 * SCALE_RUN]),
+                in0=xt[n, passes[0]][:, gs].rearrange("p g r u -> p g (r u)").bitcast(BF16).rearrange("p g (a c) -> p g a c", c=4 * SCALE_RUN),
+                in1=scale_run[:, gs].rearrange("p g r t -> p g (r t)").unsqueeze(2).to_broadcast([P, len(passes), P // SCALE_RUN, 4 * SCALE_RUN]),
                 op=ALU.mult,
             )
 
@@ -368,7 +368,6 @@ def tile_multilatentattention_pa_t_kernel(tc, x_bytes, x_scale, w_down, w_up, ou
         for n in range(1, 5):
             turn(n + 3)
             scale_x(n)
-        warm_up(3)
         scale_x(5)
         turn(8)
         turn(9)
@@ -399,13 +398,13 @@ def tile_multilatentattention_pa_t_kernel(tc, x_bytes, x_scale, w_down, w_up, ou
                     empty_main(old - 1)
                     store_v(old - GROUP, GROUP)
                     store_k(old - GROUP, GROUP)
-                for i in range(2):
-                    expand_main(old + i)
-                    empty_main(old + i)
+                expand_main(old)
+                empty_main(old)
                 turn(now + 2)
                 turn(now + 3)
-            if wide and r > 1:
                 widen(wide.pop(0), 1)
+                expand_main(old + 1)
+                empty_main(old + 1)
             for n in range(mid, mid + GROUP):
                 down(n)
                 empty_down(n)
@@ -436,11 +435,12 @@ def tile_multilatentattention_pa_t_kernel(tc, x_bytes, x_scale, w_down, w_up, ou
         empty_main(15)
         store_v(12, GROUP)
         store_k(12, GROUP)
-        for n in (16, 17):
-            expand_main(n)
-            empty_main(n)
+        expand_main(16)
+        empty_main(16)
         turn(28)
         turn(29)
+        expand_main(17)
+        empty_main(17)
         for n in (22, 23):
             down(n)
             empty_down(n)

@@ -28,7 +28,6 @@ N_POS = POS_GROUPS * GROUP
 N_TILES = N_GROUPS * GROUP
 TURN_BANKS = 4
 PRODUCT_BANKS = 4
-SCALE_RUN = 32
 DENSE_V = 5
 
 
@@ -68,6 +67,9 @@ def tile_multilatentattention_pa_t_kernel(tc, x_bytes, x_scale, w_down, w_up, ou
         nc.vector.memset(warm[:], 0.0)
         nc.scalar.activation(out=warm[:], in_=warm[:], func=ACT.Sin)
 
+        ones = const.tile([P, 1], F32)
+        nc.vector.memset(ones[:], 1.0)
+
         pos = const.tile([P, POS_GROUPS, GROUP], F32)
         nc.gpsimd.iota(pos[:], pattern=[[P * GROUP, POS_GROUPS], [1, GROUP]], base=0, channel_multiplier=GROUP, allow_small_or_imprecise_dtypes=True)
         offset = const.tile([P, P], F32)
@@ -94,8 +96,6 @@ def tile_multilatentattention_pa_t_kernel(tc, x_bytes, x_scale, w_down, w_up, ou
         halves = [slice(0, HALF // 8), slice(HALF // 8, HALF // 4)]
         for h in halves:
             nc.vector.tensor_scalar(out=whole[:, h], in0=turns[:, h], scalar1=-0.125, scalar2=None, op0=ALU.add)
-        scale_run = const.tile([P, 2, SCALE_RUN, 4], F32)
-        nc.vector.tensor_copy(out=scale_run[:], in_=scale_cols[:].unsqueeze(2).to_broadcast([P, 2, SCALE_RUN, 4]))
         for h in halves:
             nc.vector.tensor_tensor(out=frac[:, h], in0=turns[:, h], in1=whole[:, h], op=ALU.subtract)
 
@@ -149,12 +149,8 @@ def tile_multilatentattention_pa_t_kernel(tc, x_bytes, x_scale, w_down, w_up, ou
             nc.vector.quantize_mx(out=wu_rope_codes[:].bitcast(FP8X4), scales=wu_rope_scales[:], in_=wu_grp[1])
             nc.vector.quantize_mx(out=wu_main_codes[:].bitcast(FP8X4), scales=wu_main_scales[:], in_=wu_grp[0])
 
-        def warm_up(count):
-            bank = psum.tile([P, K_PASS], F32, name="product")
-            for i in range(count):
-                nc.tensor.matmul(out=bank[:], lhsT=xbf[6][:, 0:P], rhs=xbf[6][:, 0:K_PASS], start=True, stop=True)
-
         xbf = {}
+        xsorted = {}
         xt = {}
         xg = {}
         xc = {}
@@ -179,19 +175,26 @@ def tile_multilatentattention_pa_t_kernel(tc, x_bytes, x_scale, w_down, w_up, ou
             for i in range(count):
                 xbf[n + i] = wide[:, i]
 
-        def widen_aside(n, count, spent, lo=0):
-            wide = xg[spent][0][:, lo:lo + count].rearrange("p i g c -> p i (g c)")
-            nc.gpsimd.tensor_copy(out=wide.rearrange("p i d -> p (i d)"), in_=x_bytes_of(n, count))
-            for i in range(count):
-                xbf[n + i] = wide[:, i]
+        def widen_sorted(n):
+            wide = work.tile([P, 2, 2 * P, 2], BF16, name="xsort", bufs=2)
+            nc.vector.tensor_scalar(
+                out=wide[:].rearrange("p u w e -> p w u e"),
+                in0=x_bytes_of(n, 1).rearrange("p (w u e) -> p w u e", u=2, e=2),
+                scalar1=ones[:], scalar2=None, op0=ALU.mult,
+            )
+            xsorted[n] = wide[:].rearrange("p u w e -> p u (w e)").bitcast(F32)
+
+        def words_of(n, g, u):
+            if n in xsorted:
+                return xsorted[n][:, u, g * P:(g + 1) * P]
+            return xbf[n][:, g * K_PASS:(g + 1) * K_PASS].bitcast(F32)[:, u::2]
 
         def turn(n, passes=(0, 1)):
-            bank = psum.tile([P, 2, P, 2], F32, name="xt", bufs=TURN_BANKS)
+            bank = psum.tile([P, 2, 2, P], F32, name="xt", bufs=TURN_BANKS)
             xt[n, passes[0]] = bank
             for g in passes:
-                values = xbf[n][:, g * K_PASS:(g + 1) * K_PASS]
                 for u in range(2):
-                    nc.tensor.transpose(bank[:, g, :, u], values.bitcast(F32)[:, u::2], ident[:])
+                    nc.tensor.transpose(bank[:, u, g, :], words_of(n, g, u), ident[:])
 
         def open_x(lo, count):
             values = work.tile([P, count, 2, P * 4], BF16, name="xg", align_bytes=64, bufs=4)
@@ -205,9 +208,9 @@ def tile_multilatentattention_pa_t_kernel(tc, x_bytes, x_scale, w_down, w_up, ou
             values, i = xg[n]
             gs = slice(passes[0], passes[-1] + 1)
             nc.vector.tensor_tensor(
-                out=values[:, i, gs].rearrange("p g (a c) -> p g a c", c=4 * SCALE_RUN),
-                in0=xt[n, passes[0]][:, gs].rearrange("p g r u -> p g (r u)").bitcast(BF16).rearrange("p g (a c) -> p g a c", c=4 * SCALE_RUN),
-                in1=scale_run[:, gs].rearrange("p g r t -> p g (r t)").unsqueeze(2).to_broadcast([P, len(passes), P // SCALE_RUN, 4 * SCALE_RUN]),
+                out=values[:, i, gs].rearrange("p g (r u e) -> p g r u e", u=2, e=2),
+                in0=xt[n, passes[0]][:, :, gs].bitcast(BF16).rearrange("p u g (r e) -> p g r u e", e=2),
+                in1=scale_cols[:, gs].rearrange("p g (u e) -> p g u e", e=2).unsqueeze(2).to_broadcast([P, len(passes), P, 2, 2]),
                 op=ALU.mult,
             )
 
@@ -356,8 +359,8 @@ def tile_multilatentattention_pa_t_kernel(tc, x_bytes, x_scale, w_down, w_up, ou
         widen(10)
         tables()
         widen(12)
-        open_x(0, 4)
-        open_x(4, 2)
+        open_x(0, 2)
+        open_x(2, 4)
         turn(0, (0,))
         turn(0, (1,))
         turn(1)
@@ -372,16 +375,17 @@ def tile_multilatentattention_pa_t_kernel(tc, x_bytes, x_scale, w_down, w_up, ou
         turn(8)
         turn(9)
         widen(14)
-        widen(16)
+        widen(16, 1)
         quant_down()
-        quant_x(0, 4)
-        quant_x(4, 2)
-        group_up(4, 0)
+        quant_x(0, 2)
+        quant_x(2, 4)
+        group_up(2, 0)
         for n in range(2):
             down(n)
             empty_down(n)
 
-        wide = list(range(18, N_TILES))
+        sort = [17, 21, 25, 29, 31]
+        wide = [n for n in range(17, N_TILES) if n not in sort]
         for r in range(1, N_GROUPS - 2):
             now = GROUP * r + 2
             mid = now - GROUP
@@ -402,7 +406,8 @@ def tile_multilatentattention_pa_t_kernel(tc, x_bytes, x_scale, w_down, w_up, ou
                 empty_main(old)
                 turn(now + 2)
                 turn(now + 3)
-                widen(wide.pop(0), 1)
+                if wide:
+                    widen(wide.pop(0), 1)
                 expand_main(old + 1)
                 empty_main(old + 1)
             for n in range(mid, mid + GROUP):
@@ -412,7 +417,7 @@ def tile_multilatentattention_pa_t_kernel(tc, x_bytes, x_scale, w_down, w_up, ou
             scale_x(now + 1)
             turn(ahead)
             turn(ahead + 1)
-            for i in range(3 if r == 1 else 2):
+            for i in range(2 if r == 1 else 1):
                 if wide:
                     widen(wide.pop(0), 1)
             if old >= 0:
@@ -425,6 +430,9 @@ def tile_multilatentattention_pa_t_kernel(tc, x_bytes, x_scale, w_down, w_up, ou
             if r == 1:
                 quant_up()
             quant_x(now, GROUP)
+            for i in range(1):
+                if sort:
+                    widen_sorted(sort.pop(0))
 
         open_x(26, GROUP)
         expand_rope(16, GROUP)

@@ -53,22 +53,22 @@ def tile_multilatentattention_pa_t_kernel(tc, x_bytes, x_scale, w_down, w_up, ou
         nc.sync.dma_start(out=x_tiles[0][:, 0:1], in_=x_view[0][:, 0:1])
         nc.sync.dma_start(out=scale_cols[:], in_=x_scale.rearrange("a b (g p t) -> p (a b g) t", p=P, t=4))
         nc.sync.dma_start(out=x_tiles[0][:, 1:2], in_=x_view[0][:, 1:2])
-        nc.sync.dma_start(out=x_tiles[0][:, 2:4], in_=x_view[0][:, 2:4])
+        nc.sync.dma_start(out=x_tiles[0][:, 2:3], in_=x_view[0][:, 2:3])
         nc.sync.dma_start(out=wd_raw[0][:], in_=wd_view[0])
+        nc.sync.dma_start(out=x_tiles[0][:, 3:4], in_=x_view[0][:, 3:4])
         nc.sync.dma_start(out=x_tiles[1][:], in_=x_view[1])
         nc.sync.dma_start(out=wd_raw[1][:], in_=wd_view[1])
         nc.sync.dma_start(out=x_tiles[2][:], in_=x_view[2])
         nc.sync.dma_start(out=x_tiles[3][:], in_=x_view[3])
-        nc.sync.dma_start(out=wu_raw[:], in_=w_up.rearrange("(p j) n -> p j n", j=4))
+        wu_view = w_up.rearrange("(q t r) n -> r q t n", t=4, r=8)
+        for r in range(8):
+            nc.sync.dma_start(out=wu_raw[r:P:8], in_=wu_view[r])
         for g in range(4, N_GROUPS):
             nc.sync.dma_start(out=x_tiles[g][:], in_=x_view[g])
 
         warm = const.tile([P, 1], F32)
         nc.vector.memset(warm[:], 0.0)
         nc.scalar.activation(out=warm[:], in_=warm[:], func=ACT.Sin)
-
-        ones = const.tile([P, 1], F32)
-        nc.vector.memset(ones[:], 1.0)
 
         pos = const.tile([P, POS_GROUPS, GROUP], F32)
         nc.gpsimd.iota(pos[:], pattern=[[P * GROUP, POS_GROUPS], [1, GROUP]], base=0, channel_multiplier=GROUP, allow_small_or_imprecise_dtypes=True)
@@ -89,26 +89,20 @@ def tile_multilatentattention_pa_t_kernel(tc, x_bytes, x_scale, w_down, w_up, ou
                 out=turns[:, b], in0=low[:].rearrange("p a n -> p n a"),
                 scalar1=ROPE_BASE ** (-4 * b / HALF), scalar2=None, op0=ALU.mult,
             )
-        whole = const.tile(shape, I32, name="whole_then_wd", align_bytes=64)
-        frac = const.tile(shape, F32)
-        mag = const.tile([P, 2] + shape[1:], F32)
+        whole = const.tile([P, 2] + shape[1:], I32, name="whole_then_wd", align_bytes=64)
+        frac = const.tile([P, 2] + shape[1:], F32)
         trig = const.tile([P, N_POS, 4, HALF], F32)
-        halves = [slice(0, HALF // 8), slice(HALF // 8, HALF // 4)]
-        for h in halves:
-            nc.vector.tensor_scalar(out=whole[:, h], in0=turns[:, h], scalar1=-0.125, scalar2=None, op0=ALU.add)
-        for h in halves:
-            nc.vector.tensor_tensor(out=frac[:, h], in0=turns[:, h], in1=whole[:, h], op=ALU.subtract)
+        for c in range(2):
+            nc.vector.tensor_scalar(out=whole[:, c], in0=turns[:], scalar1=0.25 * (1 - c), scalar2=None, op0=ALU.add)
+        for c in range(2):
+            nc.vector.tensor_tensor(out=frac[:, c], in0=turns[:], in1=whole[:, c], op=ALU.subtract)
 
-        def table_arg(c):
-            nc.scalar.activation(out=mag[:, c], in_=frac[:], func=ACT.Abs, scale=2 * math.pi, bias=-c * math.pi / 2)
-
-        def tables():
-            for c, arg, sign in ((0, 0, 1.0), (1, 1, 1.0), (2, 1, -1.0), (3, 0, 1.0)):
-                nc.scalar.activation(
-                    out=trig[:, :, c].rearrange("p n (b a) -> p n b a", a=4),
-                    in_=mag[:, arg].rearrange("p b n a -> p n b a"),
-                    func=ACT.Sin, scale=-sign, bias=sign * math.pi / 2,
-                )
+        def table(entry, c, sign):
+            nc.scalar.activation(
+                out=trig[:, :, entry].rearrange("p n (b a) -> p n b a", a=4),
+                in_=frac[:, c].rearrange("p b n a -> p n b a"),
+                func=ACT.Sin, scale=sign * 2 * math.pi, bias=(1 - c) * math.pi / 2,
+            )
 
         wd_grp = const.tile([P, 2, DL * 4], BF16, align_bytes=64, name="whole_then_wd")
         wd_codes = const.tile([P, 2, DL], U32, align_bytes=64)
@@ -123,7 +117,10 @@ def tile_multilatentattention_pa_t_kernel(tc, x_bytes, x_scale, w_down, w_up, ou
             nc.gpsimd.tensor_scalar(out=out, in0=in0, scalar1=1.0, scalar2=0.0, op0=ALU.mult, op1=ALU.add)
 
         def group_down(g):
-            group(wd_grp[:, g].rearrange("p (t m j) -> p t m j", t=4, j=4), wd_raw[g][:].rearrange("p j (m t) -> p t m j", t=4))
+            group(
+                wd_grp[:, g].rearrange("p (t q r j) -> p q t r j", t=4, r=8, j=4),
+                wd_raw[g][:].rearrange("p j (q t r) -> p q t r j", t=4, r=8),
+            )
 
         def quant_down():
             nc.vector.quantize_mx(
@@ -150,7 +147,6 @@ def tile_multilatentattention_pa_t_kernel(tc, x_bytes, x_scale, w_down, w_up, ou
             nc.vector.quantize_mx(out=wu_main_codes[:].bitcast(FP8X4), scales=wu_main_scales[:], in_=wu_grp[0])
 
         xbf = {}
-        xsorted = {}
         xt = {}
         xg = {}
         xc = {}
@@ -175,26 +171,13 @@ def tile_multilatentattention_pa_t_kernel(tc, x_bytes, x_scale, w_down, w_up, ou
             for i in range(count):
                 xbf[n + i] = wide[:, i]
 
-        def widen_sorted(n):
-            wide = work.tile([P, 2, 2 * P, 2], BF16, name="xsort", bufs=2)
-            nc.vector.tensor_scalar(
-                out=wide[:].rearrange("p u w e -> p w u e"),
-                in0=x_bytes_of(n, 1).rearrange("p (w u e) -> p w u e", u=2, e=2),
-                scalar1=ones[:], scalar2=None, op0=ALU.mult,
-            )
-            xsorted[n] = wide[:].rearrange("p u w e -> p u (w e)").bitcast(F32)
-
-        def words_of(n, g, u):
-            if n in xsorted:
-                return xsorted[n][:, u, g * P:(g + 1) * P]
-            return xbf[n][:, g * K_PASS:(g + 1) * K_PASS].bitcast(F32)[:, u::2]
-
         def turn(n, passes=(0, 1)):
             bank = psum.tile([P, 2, 2, P], F32, name="xt", bufs=TURN_BANKS)
             xt[n, passes[0]] = bank
             for g in passes:
+                values = xbf[n][:, g * K_PASS:(g + 1) * K_PASS]
                 for u in range(2):
-                    nc.tensor.transpose(bank[:, u, g, :], words_of(n, g, u), ident[:])
+                    nc.tensor.transpose(bank[:, u, g, :], values.bitcast(F32)[:, u::2], ident[:])
 
         def open_x(lo, count):
             values = work.tile([P, count, 2, P * 4], BF16, name="xg", align_bytes=64, bufs=4)
@@ -248,7 +231,7 @@ def tile_multilatentattention_pa_t_kernel(tc, x_bytes, x_scale, w_down, w_up, ou
 
         def quant_lat(n, count):
             g, i = divmod(n, GROUP)
-            if i == 0:
+            if g not in lc:
                 codes = work.tile([P, GROUP, P], U32, name="lcodes", align_bytes=64)
                 scales = work.tile([P, GROUP, P], U8, name="lscales", align_bytes=64)
                 lc[g] = (codes, scales)
@@ -346,18 +329,28 @@ def tile_multilatentattention_pa_t_kernel(tc, x_bytes, x_scale, w_down, w_up, ou
             g, i = divmod(n, GROUP)
             nc.sync.dma_start(out=k_view[g][:, i:i + count], in_=kv[g][:, 0, i:i + count].rearrange("p i h f -> p i (h f)"))
 
+        def first(n):
+            down(n)
+            empty_down(n)
+
+        def second(n):
+            expand_main(n)
+            empty_main(n)
+
         widen(0, 1, parts=2)
         widen(1, 1)
         group_down(0)
         group_down(1)
-        widen(2)
-        table_arg(0)
-        table_arg(1)
+        widen(2, 1)
+        table(0, 0, 1.0)
+        table(1, 1, 1.0)
+        widen(3, 1)
         widen(4)
         widen(6)
         widen(8)
         widen(10)
-        tables()
+        table(2, 1, -1.0)
+        table(3, 0, 1.0)
         widen(12)
         open_x(0, 2)
         open_x(2, 4)
@@ -375,7 +368,7 @@ def tile_multilatentattention_pa_t_kernel(tc, x_bytes, x_scale, w_down, w_up, ou
         turn(8)
         turn(9)
         widen(14)
-        widen(16, 1)
+        widen(16)
         quant_down()
         quant_x(0, 2)
         quant_x(2, 4)
@@ -384,8 +377,7 @@ def tile_multilatentattention_pa_t_kernel(tc, x_bytes, x_scale, w_down, w_up, ou
             down(n)
             empty_down(n)
 
-        sort = [17, 21, 25, 29, 31]
-        wide = [n for n in range(17, N_TILES) if n not in sort]
+        wide = list(range(18, N_TILES))
         for r in range(1, N_GROUPS - 2):
             now = GROUP * r + 2
             mid = now - GROUP
@@ -406,20 +398,23 @@ def tile_multilatentattention_pa_t_kernel(tc, x_bytes, x_scale, w_down, w_up, ou
                 empty_main(old)
                 turn(now + 2)
                 turn(now + 3)
-                if wide:
-                    widen(wide.pop(0), 1)
+                widen(wide.pop(0), 1)
                 expand_main(old + 1)
                 empty_main(old + 1)
-            for n in range(mid, mid + GROUP):
-                down(n)
-                empty_down(n)
+            before = 2 if r == 1 else GROUP
+            for n in range(mid, mid + before):
+                first(n)
             scale_x(now)
             scale_x(now + 1)
             turn(ahead)
             turn(ahead + 1)
-            for i in range(2 if r == 1 else 1):
+            for i in range(2):
                 if wide:
                     widen(wide.pop(0), 1)
+            for n in range(mid + before, mid + GROUP):
+                first(n)
+            if r == 1:
+                widen(wide.pop(0), 1)
             if old >= 0:
                 expand_main(old + 2)
                 expand_main(old + 3)
@@ -430,9 +425,6 @@ def tile_multilatentattention_pa_t_kernel(tc, x_bytes, x_scale, w_down, w_up, ou
             if r == 1:
                 quant_up()
             quant_x(now, GROUP)
-            for i in range(1):
-                if sort:
-                    widen_sorted(sort.pop(0))
 
         open_x(26, GROUP)
         expand_rope(16, GROUP)
@@ -471,63 +463,63 @@ def tile_multilatentattention_pa_t_kernel(tc, x_bytes, x_scale, w_down, w_up, ou
 
         open_x(30, 2)
         expand_rope(20, GROUP, "xt")
-        for n in (20, 21):
-            expand_main(n)
-            empty_main(n)
-        for n in range(26, 30):
-            down(n)
-            empty_down(n)
+        second(20)
+        second(21)
         open_products(20, GROUP)
         products_direct(20, 0, GROUP)
+        quant_lat(24, 2)
         rope_add(nc.gpsimd, 20, GROUP)
         store_v(20, 2)
         store_k(20, 2)
-        for n in (22, 23):
-            expand_main(n)
-            empty_main(n)
+        first(26)
+        first(27)
+        second(22)
+        second(23)
         store_v(22, 2)
         store_k(22, 2)
         scale_x(30)
+        expand_rope(24, 2, "xt")
         scale_x(31)
-        quant_lat(24, GROUP)
+        first(28)
+        first(29)
+        quant_lat(26, 2)
         quant_x(30, 2)
-        quant_lat(28, 2)
-        expand_main(24)
-        empty_main(24)
-        expand_rope(24, GROUP, "xt")
-        expand_main(25)
-        empty_main(25)
-        for n in (30, 31):
-            down(n)
-            empty_down(n)
-        open_products(24, GROUP)
+        second(24)
+        second(25)
+        open_products(24, 2)
         products_direct(24, 0, 2)
-        products_direct(24, 2, 2)
-        rope_add(nc.vector, 24, 2)
-        rope_add(nc.vector, 24, 2, 2)
+        rope_add(nc.gpsimd, 24, 2)
         store_v(24, 2)
         store_k(24, 2)
+        expand_rope(26, 2, "xt")
+        first(30)
+        first(31)
         expand_main(26, "xt")
-        expand_rope(28, 2, "xt")
-        for n in (27, 28, 29):
-            expand_main(n)
-            empty_main(n)
+        expand_main(27, "xt")
+        open_products(26, 2)
+        products_direct(26, 0, 2)
+        quant_lat(28, 2)
+        rope_add(nc.gpsimd, 26, 2)
         empty_main(26, on_vector=True)
+        quant_lat(30, 2)
+        empty_main(27)
         store_v(26, 2)
         store_k(26, 2)
-        quant_lat(30, 2)
+        expand_rope(28, 2, "xt")
+        second(28)
+        second(29)
         open_products(28, 2)
         products_direct(28, 0, 2)
         expand_rope(30, 2, "xt")
         expand_main(30)
-        expand_main(31)
+        expand_main(31, "xt")
+        rope_add(nc.gpsimd, 28, 2)
+        store_v(28, 2)
+        store_k(28, 2)
         open_products(30, 2)
         products_direct(30, 0, 2)
-        store_v(28, 2)
-        rope_add(nc.vector, 28, 2)
-        store_k(28, 2)
         empty_main(30)
-        empty_main(31)
+        empty_main(31, on_vector=True)
         rope_add(nc.vector, 30, 2)
-        store_k(30, 2)
         store_v(30, 2)
+        store_k(30, 2)

@@ -26,9 +26,14 @@ N_GROUPS = B * S // (P * GROUP)
 POS_GROUPS = S // (P * GROUP)
 N_POS = POS_GROUPS * GROUP
 N_TILES = N_GROUPS * GROUP
+BLOCKS = P // 8
 TURN_BANKS = 4
 PRODUCT_BANKS = 4
-DENSE_V = 5
+SHIFT = 2
+WIDE_BUFS = 8
+DENSE_V = N_GROUPS - 3
+FAST = 24
+VECTOR_BLOCKS = 4
 
 
 def tile_multilatentattention_pa_t_kernel(tc, x_bytes, x_scale, w_down, w_up, out_k, out_v):
@@ -51,12 +56,13 @@ def tile_multilatentattention_pa_t_kernel(tc, x_bytes, x_scale, w_down, w_up, ou
         x_tiles = [xin.tile([P, GROUP, D], U8, name="xb") for g in range(N_GROUPS)]
         scale_cols = const.tile([P, 2, 4], F32)
         nc.sync.dma_start(out=x_tiles[0][:, 0:1], in_=x_view[0][:, 0:1])
-        nc.sync.dma_start(out=scale_cols[:], in_=x_scale.rearrange("a b (g p t) -> p (a b g) t", p=P, t=4))
         nc.sync.dma_start(out=x_tiles[0][:, 1:2], in_=x_view[0][:, 1:2])
+        nc.sync.dma_start(out=scale_cols[:], in_=x_scale.rearrange("a b (g p t) -> p (a b g) t", p=P, t=4))
         nc.sync.dma_start(out=x_tiles[0][:, 2:3], in_=x_view[0][:, 2:3])
         nc.sync.dma_start(out=wd_raw[0][:], in_=wd_view[0])
         nc.sync.dma_start(out=x_tiles[0][:, 3:4], in_=x_view[0][:, 3:4])
-        nc.sync.dma_start(out=x_tiles[1][:], in_=x_view[1])
+        nc.sync.dma_start(out=x_tiles[1][:, 0:2], in_=x_view[1][:, 0:2])
+        nc.sync.dma_start(out=x_tiles[1][:, 2:4], in_=x_view[1][:, 2:4])
         nc.sync.dma_start(out=wd_raw[1][:], in_=wd_view[1])
         nc.sync.dma_start(out=x_tiles[2][:], in_=x_view[2])
         nc.sync.dma_start(out=x_tiles[3][:], in_=x_view[3])
@@ -65,10 +71,6 @@ def tile_multilatentattention_pa_t_kernel(tc, x_bytes, x_scale, w_down, w_up, ou
             nc.sync.dma_start(out=wu_raw[r:P:8], in_=wu_view[r])
         for g in range(4, N_GROUPS):
             nc.sync.dma_start(out=x_tiles[g][:], in_=x_view[g])
-
-        warm = const.tile([P, 1], F32)
-        nc.vector.memset(warm[:], 0.0)
-        nc.scalar.activation(out=warm[:], in_=warm[:], func=ACT.Sin)
 
         pos = const.tile([P, POS_GROUPS, GROUP], F32)
         nc.gpsimd.iota(pos[:], pattern=[[P * GROUP, POS_GROUPS], [1, GROUP]], base=0, channel_multiplier=GROUP, allow_small_or_imprecise_dtypes=True)
@@ -82,26 +84,35 @@ def tile_multilatentattention_pa_t_kernel(tc, x_bytes, x_scale, w_down, w_up, ou
             )
         ident = const.tile([P, P], F32)
         nc.vector.tensor_scalar(out=ident[:], in0=offset[:], scalar1=0.0, scalar2=None, op0=ALU.is_equal)
-        shape = [P, HALF // 4, N_POS, 4]
-        turns = const.tile(shape, F32)
-        for b in range(HALF // 4):
+        turns = const.tile([P, N_POS, HALF], F32)
+        for b in reversed(range(HALF // 4)):
             nc.vector.tensor_scalar(
-                out=turns[:, b], in0=low[:].rearrange("p a n -> p n a"),
+                out=turns[:, :, 4 * b:4 * b + 4], in0=low[:].rearrange("p a n -> p n a"),
                 scalar1=ROPE_BASE ** (-4 * b / HALF), scalar2=None, op0=ALU.mult,
             )
-        whole = const.tile([P, 2] + shape[1:], I32, name="whole_then_wd", align_bytes=64)
-        frac = const.tile([P, 2] + shape[1:], F32)
+        whole = const.tile([P, 2, N_POS, FAST], I32, name="whole_then_wd", align_bytes=64)
+        frac = const.tile([P, 2, N_POS, FAST], F32)
         trig = const.tile([P, N_POS, 4, HALF], F32)
         for c in range(2):
-            nc.vector.tensor_scalar(out=whole[:, c], in0=turns[:], scalar1=0.25 * (1 - c), scalar2=None, op0=ALU.add)
+            nc.vector.tensor_scalar(out=whole[:, c], in0=turns[:, :, 0:FAST], scalar1=0.25 * (1 - c), scalar2=None, op0=ALU.add)
         for c in range(2):
-            nc.vector.tensor_tensor(out=frac[:, c], in0=turns[:], in1=whole[:, c], op=ALU.subtract)
+            nc.vector.tensor_tensor(out=frac[:, c], in0=turns[:, :, 0:FAST], in1=whole[:, c], op=ALU.subtract)
 
-        def table(entry, c, sign):
+        is_sine = (0, 1, 1, 0)
+        sign = (1.0, 1.0, -1.0, 1.0)
+
+        def table_fast(entry):
+            c = is_sine[entry]
             nc.scalar.activation(
-                out=trig[:, :, entry].rearrange("p n (b a) -> p n b a", a=4),
-                in_=frac[:, c].rearrange("p b n a -> p n b a"),
-                func=ACT.Sin, scale=sign * 2 * math.pi, bias=(1 - c) * math.pi / 2,
+                out=trig[:, :, entry, 0:FAST], in_=frac[:, c],
+                func=ACT.Sin, scale=sign[entry] * 2 * math.pi, bias=(1 - c) * math.pi / 2,
+            )
+
+        def table_slow(entry):
+            c = is_sine[entry]
+            nc.scalar.activation(
+                out=trig[:, :, entry, FAST:], in_=turns[:, :, FAST:],
+                func=ACT.Sin, scale=(2 * c - 1) * sign[entry] * 2 * math.pi, bias=(1 - c) * math.pi / 2,
             )
 
         wd_grp = const.tile([P, 2, DL * 4], BF16, align_bytes=64, name="whole_then_wd")
@@ -113,13 +124,16 @@ def tile_multilatentattention_pa_t_kernel(tc, x_bytes, x_scale, w_down, w_up, ou
         wu_rope_scales = const.tile([P, H * DR], U8, align_bytes=64)
         wu_grp = {}
 
-        def group(out, in0):
-            nc.gpsimd.tensor_scalar(out=out, in0=in0, scalar1=1.0, scalar2=0.0, op0=ALU.mult, op1=ALU.add)
+        def group_aside(out, in_):
+            nc.gpsimd.tensor_scalar(out=out, in0=in_, scalar1=1.0, scalar2=0.0, op0=ALU.mult, op1=ALU.add)
 
-        def group_down(g):
+        def group_direct(out, in_):
+            nc.vector.tensor_copy(out=out, in_=in_)
+
+        def group_down(g, blocks, group):
             group(
-                wd_grp[:, g].rearrange("p (t q r j) -> p q t r j", t=4, r=8, j=4),
-                wd_raw[g][:].rearrange("p j (q t r) -> p q t r j", t=4, r=8),
+                wd_grp[:, g].rearrange("p (t q r j) -> p q t r j", t=4, r=8, j=4)[:, blocks],
+                wd_raw[g][:].rearrange("p j (q t r) -> p q t r j", t=4, r=8)[:, blocks],
             )
 
         def quant_down():
@@ -134,17 +148,19 @@ def tile_multilatentattention_pa_t_kernel(tc, x_bytes, x_scale, w_down, w_up, ou
         def spent_room(spent):
             return xg[spent][0][:].rearrange("p i g c -> p (i g c)")
 
-        def group_up(spent, spent_before):
-            wu_grp[0] = spent_room(spent)[:, 0:16 * DH]
-            wu_grp[1] = spent_room(spent_before)[:, 0:4 * H * DR]
-            main_grp = wu_grp[0].rearrange("p (a h f j) -> p a h f j", a=2, h=H, j=4)
-            group(main_grp[:, 0], up[:, :, 0:DH, :])
-            group(main_grp[:, 1], up[:, :, DH + DR:, :])
-            group(wu_grp[1].rearrange("p (h f j) -> p h f j", h=H, j=4), up[:, :, DH:DH + DR, :])
+        def group_up_main(spent):
+            wu_grp["main"] = spent_room(spent)[:, 0:16 * DH]
+            main_grp = wu_grp["main"].rearrange("p (a h f j) -> p a h f j", a=2, h=H, j=4)
+            group_aside(main_grp[:, 0], up[:, :, 0:DH, :])
+            group_aside(main_grp[:, 1], up[:, :, DH + DR:, :])
+
+        def group_up_rope(spent):
+            wu_grp["rope"] = spent_room(spent)[:, 0:4 * H * DR]
+            group_direct(wu_grp["rope"].rearrange("p (h f j) -> p h f j", h=H, j=4), up[:, :, DH:DH + DR, :])
 
         def quant_up():
-            nc.vector.quantize_mx(out=wu_rope_codes[:].bitcast(FP8X4), scales=wu_rope_scales[:], in_=wu_grp[1])
-            nc.vector.quantize_mx(out=wu_main_codes[:].bitcast(FP8X4), scales=wu_main_scales[:], in_=wu_grp[0])
+            nc.vector.quantize_mx(out=wu_rope_codes[:].bitcast(FP8X4), scales=wu_rope_scales[:], in_=wu_grp["rope"])
+            nc.vector.quantize_mx(out=wu_main_codes[:].bitcast(FP8X4), scales=wu_main_scales[:], in_=wu_grp["main"])
 
         xbf = {}
         xt = {}
@@ -163,7 +179,7 @@ def tile_multilatentattention_pa_t_kernel(tc, x_bytes, x_scale, w_down, w_up, ou
             return x_tiles[n // GROUP][:, n % GROUP:n % GROUP + count].rearrange("p i d -> p (i d)").bitcast(FP8)
 
         def widen(n, count=2, parts=1):
-            wide = work.tile([P, count, D], BF16, name="xbf", bufs=8)
+            wide = work.tile([P, count, D], BF16, name="xbf", bufs=WIDE_BUFS)
             width = count * D // parts
             for part in range(parts):
                 cols = slice(part * width, (part + 1) * width)
@@ -223,7 +239,7 @@ def tile_multilatentattention_pa_t_kernel(tc, x_bytes, x_scale, w_down, w_up, ou
                         stop=(g == 1),
                     )
 
-        def empty_down(n, engine=None):
+        def empty_down(n):
             g, i = divmod(n, GROUP)
             if i == 0:
                 lg[g] = work.tile([P, GROUP, P, 4], BF16, name="lg", align_bytes=64)
@@ -284,9 +300,9 @@ def tile_multilatentattention_pa_t_kernel(tc, x_bytes, x_scale, w_down, w_up, ou
                 else:
                     nc.scalar.copy(out=out, in_=in_)
 
-        def spill_rope(n, lo, count):
-            spill[n] = work.tile([P, count, H * DR], F32, name="spill", bufs=2)
-            nc.scalar.copy(out=spill[n][:], in_=rope[n][:, lo:lo + count])
+        def spill_rope(n):
+            spill[n] = work.tile([P, GROUP, H * DR], F32, name="spill", bufs=2)
+            nc.scalar.copy(out=spill[n][:], in_=rope[n][:])
 
         def open_products(n, count, spent=None):
             if spent is None:
@@ -296,30 +312,35 @@ def tile_multilatentattention_pa_t_kernel(tc, x_bytes, x_scale, w_down, w_up, ou
                 room = spent_room(spent).bitcast(F32)[:, 0:count * H * 2 * DR]
             products[n] = room.rearrange("p (i h a c f) -> p i h a c f", h=H, a=2, c=2, f=HALF)
 
-        def rope_products(engine, source, n, lo, count):
+        def rope_products(engine, source, n, count):
             shape = [P, count, H, 2, 2, HALF]
-            first = (n + lo) % N_POS
+            at = n % N_POS
             engine.tensor_tensor(
-                out=products[n][:, lo:lo + count],
+                out=products[n],
                 in0=source.rearrange("p i (h a f) -> p i h a f", h=H, a=2).unsqueeze(4).to_broadcast(shape),
-                in1=trig[:, first:first + count].rearrange("p i (a c) f -> p i a c f", a=2).unsqueeze(2).to_broadcast(shape),
+                in1=trig[:, at:at + count].rearrange("p i (a c) f -> p i a c f", a=2).unsqueeze(2).to_broadcast(shape),
                 op=ALU.mult,
             )
 
-        def products_aside(n, lo, count):
-            rope_products(nc.gpsimd, spill[n][:], n, lo, count)
-
-        def products_direct(n, lo, count):
-            rope_products(nc.vector, rope[n][:, lo:lo + count], n, lo, count)
-
-        def rope_add(engine, n, count, lo=0):
-            g, i = divmod(n + lo, GROUP)
+        def rope_add(engine, n, count):
+            g, i = divmod(n, GROUP)
             engine.tensor_tensor(
                 out=out_tile(g)[:, 0, i:i + count, :, DH:].rearrange("p i h f -> p (i h) f"),
-                in0=products[n][:, lo:lo + count, :, 0].rearrange("p i h c f -> p (i h) (c f)"),
-                in1=products[n][:, lo:lo + count, :, 1].rearrange("p i h c f -> p (i h) (c f)"),
+                in0=products[n][:, :, :, 0].rearrange("p i h c f -> p (i h) (c f)"),
+                in1=products[n][:, :, :, 1].rearrange("p i h c f -> p (i h) (c f)"),
                 op=ALU.add,
             )
+
+        def rope_aside(n, spent):
+            expand_rope(n, GROUP)
+            spill_rope(n)
+            open_products(n, GROUP, spent)
+            rope_products(nc.gpsimd, spill[n][:], n, GROUP)
+            rope_add(nc.gpsimd, n, GROUP)
+
+        def products_direct(n, count):
+            open_products(n, count)
+            rope_products(nc.vector, rope[n][:], n, count)
 
         def store_v(n, count):
             g, i = divmod(n, GROUP)
@@ -329,6 +350,10 @@ def tile_multilatentattention_pa_t_kernel(tc, x_bytes, x_scale, w_down, w_up, ou
             g, i = divmod(n, GROUP)
             nc.sync.dma_start(out=k_view[g][:, i:i + count], in_=kv[g][:, 0, i:i + count].rearrange("p i h f -> p i (h f)"))
 
+        def store(n, count):
+            store_v(n, count)
+            store_k(n, count)
+
         def first(n):
             down(n)
             empty_down(n)
@@ -337,23 +362,27 @@ def tile_multilatentattention_pa_t_kernel(tc, x_bytes, x_scale, w_down, w_up, ou
             expand_main(n)
             empty_main(n)
 
+        table_slow(1)
+        table_slow(0)
         widen(0, 1, parts=2)
         widen(1, 1)
-        group_down(0)
-        group_down(1)
+        group_down(0, slice(0, BLOCKS), group_aside)
+        group_down(1, slice(0, BLOCKS - VECTOR_BLOCKS), group_aside)
         widen(2, 1)
-        table(0, 0, 1.0)
-        table(1, 1, 1.0)
+        table_fast(0)
+        table_fast(1)
+        table_slow(2)
         widen(3, 1)
         widen(4)
         widen(6)
-        widen(8)
-        widen(10)
-        table(2, 1, -1.0)
-        table(3, 0, 1.0)
-        widen(12)
-        open_x(0, 2)
-        open_x(2, 4)
+        table_fast(2)
+        table_fast(3)
+        table_slow(3)
+        for n in (8, 10, 12):
+            widen(n)
+        head = GROUP + SHIFT
+        open_x(0, SHIFT)
+        open_x(SHIFT, GROUP)
         turn(0, (0,))
         turn(0, (1,))
         turn(1)
@@ -361,165 +390,142 @@ def tile_multilatentattention_pa_t_kernel(tc, x_bytes, x_scale, w_down, w_up, ou
         scale_x(0, (0,))
         turn(3)
         scale_x(0, (1,))
-        for n in range(1, 5):
+        for n in range(1, head - 1):
             turn(n + 3)
             scale_x(n)
-        scale_x(5)
-        turn(8)
-        turn(9)
+        scale_x(head - 1)
+        turn(head + 2)
+        turn(head + 3)
         widen(14)
         widen(16)
+        group_down(1, slice(BLOCKS - VECTOR_BLOCKS, BLOCKS), group_direct)
+        quant_x(0, SHIFT)
         quant_down()
-        quant_x(0, 2)
-        quant_x(2, 4)
-        group_up(2, 0)
-        for n in range(2):
-            down(n)
-            empty_down(n)
+        quant_x(SHIFT, GROUP)
+        group_up_main(SHIFT)
+        for n in range(SHIFT):
+            first(n)
 
-        wide = list(range(18, N_TILES))
+        to_widen = list(range(18, N_TILES))
         for r in range(1, N_GROUPS - 2):
-            now = GROUP * r + 2
+            now = GROUP * r + SHIFT
             mid = now - GROUP
             old = GROUP * (r - 2)
             ahead = now + GROUP
             open_x(now, GROUP)
             if old >= 0:
-                expand_rope(old, GROUP)
-                spill_rope(old, 0, GROUP)
-                open_products(old, GROUP, mid)
-                products_aside(old, 0, GROUP)
-                rope_add(nc.gpsimd, old, GROUP)
+                rope_aside(old, mid)
                 if old > 0:
                     empty_main(old - 1)
-                    store_v(old - GROUP, GROUP)
-                    store_k(old - GROUP, GROUP)
-                expand_main(old)
-                empty_main(old)
+                    store(old - GROUP, GROUP)
+                second(old)
                 turn(now + 2)
                 turn(now + 3)
-                widen(wide.pop(0), 1)
-                expand_main(old + 1)
-                empty_main(old + 1)
-            before = 2 if r == 1 else GROUP
+                widen(to_widen.pop(0), 1)
+                second(old + 1)
+            before = GROUP if old >= 0 else 2
             for n in range(mid, mid + before):
                 first(n)
             scale_x(now)
             scale_x(now + 1)
             turn(ahead)
             turn(ahead + 1)
-            for i in range(2):
-                if wide:
-                    widen(wide.pop(0), 1)
+            for n in to_widen[:2]:
+                widen(n, 1)
+            to_widen = to_widen[2:]
             for n in range(mid + before, mid + GROUP):
                 first(n)
-            if r == 1:
-                widen(wide.pop(0), 1)
             if old >= 0:
                 expand_main(old + 2)
                 expand_main(old + 3)
                 empty_main(old + 2)
+            else:
+                widen(to_widen.pop(0), 1)
             scale_x(now + 2)
             scale_x(now + 3)
+            if old < 0:
+                group_up_rope(0)
             quant_lat(old + GROUP, GROUP)
-            if r == 1:
+            if old < 0:
                 quant_up()
             quant_x(now, GROUP)
 
-        open_x(26, GROUP)
-        expand_rope(16, GROUP)
-        spill_rope(16, 0, GROUP)
-        open_products(16, GROUP, 22)
-        products_aside(16, 0, GROUP)
-        rope_add(nc.gpsimd, 16, GROUP)
-        empty_main(15)
-        store_v(12, GROUP)
-        store_k(12, GROUP)
-        expand_main(16)
-        empty_main(16)
-        turn(28)
-        turn(29)
-        expand_main(17)
-        empty_main(17)
-        for n in (22, 23):
-            down(n)
-            empty_down(n)
-        for n in (18, 19):
-            expand_main(n)
-            empty_main(n)
-        store_v(16, GROUP)
-        store_k(16, GROUP)
-        scale_x(26)
-        scale_x(27)
-        turn(30)
-        turn(31)
-        for n in (24, 25):
-            down(n)
-            empty_down(n)
-        scale_x(28)
-        scale_x(29)
-        quant_lat(20, GROUP)
-        quant_x(26, GROUP)
+        now = N_TILES - SHIFT - GROUP
+        mid = now - GROUP
+        old = mid - GROUP - SHIFT
+        open_x(now, GROUP)
+        rope_aside(old, mid)
+        empty_main(old - 1)
+        store(old - GROUP, GROUP)
+        second(old)
+        turn(now + 2)
+        turn(now + 3)
+        second(old + 1)
+        first(mid)
+        first(mid + 1)
+        second(old + 2)
+        second(old + 3)
+        store(old, GROUP)
+        scale_x(now)
+        scale_x(now + 1)
+        turn(now + 4)
+        turn(now + 5)
+        first(mid + 2)
+        first(mid + 3)
+        scale_x(now + 2)
+        scale_x(now + 3)
+        quant_lat(old + GROUP, GROUP)
+        quant_x(now, GROUP)
 
-        open_x(30, 2)
-        expand_rope(20, GROUP, "xt")
-        second(20)
-        second(21)
-        open_products(20, GROUP)
-        products_direct(20, 0, GROUP)
-        quant_lat(24, 2)
-        rope_add(nc.gpsimd, 20, GROUP)
-        store_v(20, 2)
-        store_k(20, 2)
-        first(26)
-        first(27)
-        second(22)
-        second(23)
-        store_v(22, 2)
-        store_k(22, 2)
-        scale_x(30)
-        expand_rope(24, 2, "xt")
-        scale_x(31)
-        first(28)
-        first(29)
-        quant_lat(26, 2)
-        quant_x(30, 2)
-        second(24)
-        second(25)
-        open_products(24, 2)
-        products_direct(24, 0, 2)
-        rope_add(nc.gpsimd, 24, 2)
-        store_v(24, 2)
-        store_k(24, 2)
-        expand_rope(26, 2, "xt")
-        first(30)
-        first(31)
-        expand_main(26, "xt")
-        expand_main(27, "xt")
-        open_products(26, 2)
-        products_direct(26, 0, 2)
-        quant_lat(28, 2)
-        rope_add(nc.gpsimd, 26, 2)
-        empty_main(26, on_vector=True)
-        quant_lat(30, 2)
-        empty_main(27)
-        store_v(26, 2)
-        store_k(26, 2)
-        expand_rope(28, 2, "xt")
-        second(28)
-        second(29)
-        open_products(28, 2)
-        products_direct(28, 0, 2)
-        expand_rope(30, 2, "xt")
-        expand_main(30)
-        expand_main(31, "xt")
-        rope_add(nc.gpsimd, 28, 2)
-        store_v(28, 2)
-        store_k(28, 2)
-        open_products(30, 2)
-        products_direct(30, 0, 2)
-        empty_main(30)
-        empty_main(31, on_vector=True)
-        rope_add(nc.vector, 30, 2)
-        store_v(30, 2)
-        store_k(30, 2)
+        a, b, c, d, e, f = range(N_TILES - 12, N_TILES, 2)
+        open_x(f, 2)
+        expand_rope(a, GROUP, "xt")
+        second(a)
+        second(a + 1)
+        products_direct(a, GROUP)
+        quant_lat(c, 2)
+        rope_add(nc.gpsimd, a, GROUP)
+        store(a, 2)
+        first(d)
+        first(d + 1)
+        second(b)
+        second(b + 1)
+        store(b, 2)
+        scale_x(f)
+        expand_rope(c, 2, "xt")
+        scale_x(f + 1)
+        first(e)
+        first(e + 1)
+        quant_lat(d, 2)
+        quant_x(f, 2)
+        second(c)
+        second(c + 1)
+        products_direct(c, 2)
+        rope_add(nc.gpsimd, c, 2)
+        store(c, 2)
+        expand_rope(d, 2, "xt")
+        first(f)
+        first(f + 1)
+        expand_main(d, "xt")
+        expand_main(d + 1, "xt")
+        products_direct(d, 2)
+        quant_lat(e, 2)
+        rope_add(nc.gpsimd, d, 2)
+        empty_main(d, on_vector=True)
+        quant_lat(f, 2)
+        empty_main(d + 1)
+        store(d, 2)
+        expand_rope(e, 2, "xt")
+        second(e)
+        second(e + 1)
+        products_direct(e, 2)
+        expand_rope(f, 2, "xt")
+        expand_main(f)
+        expand_main(f + 1, "xt")
+        rope_add(nc.gpsimd, e, 2)
+        store(e, 2)
+        products_direct(f, 2)
+        empty_main(f)
+        empty_main(f + 1, on_vector=True)
+        rope_add(nc.vector, f, 2)
+        store(f, 2)

@@ -22,66 +22,73 @@ P = 128
 K_PASS = 4 * P
 GROUP = 4
 HALF = DR // 2
-N_GROUPS = B * S // (P * GROUP)
-POS_GROUPS = S // (P * GROUP)
-N_POS = POS_GROUPS * GROUP
-N_TILES = N_GROUPS * GROUP
-BLOCKS = P // 8
-TURN_BANKS = 4
-PRODUCT_BANKS = 4
-SHIFT = 2
-WIDE_BUFS = 8
-DENSE_V = N_GROUPS - 3
+N_POS = S // P
+N_TILES = B * N_POS
+N_GROUPS = N_TILES // GROUP
 FAST = 24
-VECTOR_BLOCKS = 4
+WIDE_BUFS = {1: 4, 2: 7}
+ASIDE_BLOCKS = 56
+XG_BUFS = 4
 
 
 def tile_multilatentattention_pa_t_kernel(tc, x_bytes, x_scale, w_down, w_up, out_k, out_v):
     nc = tc.nc
-    x_view = x_bytes.rearrange("b (g q i) d -> (b g) q i d", q=P, i=GROUP)
-    k_view = out_k.rearrange("b (g q i) h f -> (b g) q i (h f)", q=P, i=GROUP)
-    v_view = out_v.rearrange("b (g q i) h f -> (b g) q (i h) f", q=P, i=GROUP)
+    x_view = x_bytes.rearrange("b (q i) d -> b q i d", i=N_POS)
+    k_view = out_k.rearrange("b (q i) h f -> b q i (h f)", i=N_POS)
+    v_view = out_v.rearrange("b (q i) h f -> b q i (h f)", i=N_POS)
     wd_view = w_down.rearrange("(g p j) c -> g p j c", p=P, j=4)
+    wu_view = w_up.rearrange("(m t r) n -> r m t n", t=4, r=2)
 
     with ExitStack() as ctx:
         const = ctx.enter_context(tc.tile_pool(name="const", bufs=1))
-        xin = ctx.enter_context(tc.tile_pool(name="xin", bufs=N_GROUPS))
         work = ctx.enter_context(tc.tile_pool(name="work", bufs=3))
-        outp = ctx.enter_context(tc.tile_pool(name="outp", bufs=3))
-        psum = ctx.enter_context(tc.psum_pool(name="psum", bufs=PRODUCT_BANKS))
+        psum = ctx.enter_context(tc.psum_pool(name="psum", bufs=4))
         ctx.enter_context(tc.manual_schedule())
 
         wd_raw = [const.tile([P, 4, DL], BF16, name="wd_raw%d" % g) for g in range(2)]
         wu_raw = const.tile([P, 4, N_UP], BF16)
-        x_tiles = [xin.tile([P, GROUP, D], U8, name="xb") for g in range(N_GROUPS)]
         scale_cols = const.tile([P, 2, 4], F32)
-        nc.sync.dma_start(out=x_tiles[0][:, 0:1], in_=x_view[0][:, 0:1])
-        nc.sync.dma_start(out=x_tiles[0][:, 1:2], in_=x_view[0][:, 1:2])
-        nc.sync.dma_start(out=scale_cols[:], in_=x_scale.rearrange("a b (g p t) -> p (a b g) t", p=P, t=4))
-        nc.sync.dma_start(out=x_tiles[0][:, 2:3], in_=x_view[0][:, 2:3])
-        nc.sync.dma_start(out=wd_raw[0][:], in_=wd_view[0])
-        nc.sync.dma_start(out=x_tiles[0][:, 3:4], in_=x_view[0][:, 3:4])
-        nc.sync.dma_start(out=x_tiles[1][:, 0:2], in_=x_view[1][:, 0:2])
-        nc.sync.dma_start(out=x_tiles[1][:, 2:4], in_=x_view[1][:, 2:4])
-        nc.sync.dma_start(out=wd_raw[1][:], in_=wd_view[1])
-        nc.sync.dma_start(out=x_tiles[2][:], in_=x_view[2])
-        nc.sync.dma_start(out=x_tiles[3][:], in_=x_view[3])
-        wu_view = w_up.rearrange("(q t r) n -> r q t n", t=4, r=8)
-        for r in range(8):
-            nc.sync.dma_start(out=wu_raw[r:P:8], in_=wu_view[r])
-        for g in range(4, N_GROUPS):
-            nc.sync.dma_start(out=x_tiles[g][:], in_=x_view[g])
+        raw = {}
 
-        pos = const.tile([P, POS_GROUPS, GROUP], F32)
-        nc.gpsimd.iota(pos[:], pattern=[[P * GROUP, POS_GROUPS], [1, GROUP]], base=0, channel_multiplier=GROUP, allow_small_or_imprecise_dtypes=True)
+        def load_x(n, count):
+            room = const.tile([P, count, D], U8, name="xb%d" % n)
+            b, i = divmod(n, N_POS)
+            nc.sync.dma_start(out=room[:], in_=x_view[b][:, i:i + count])
+            for j in range(count):
+                raw[n + j] = (room, j)
+
+        def load_scales():
+            nc.sync.dma_start(out=scale_cols[:], in_=x_scale.rearrange("a b (g p t) -> p (a b g) t", p=P, t=4))
+
+        def load_down(g):
+            nc.sync.dma_start(out=wd_raw[g][:], in_=wd_view[g])
+
+        def load_up():
+            for r in range(2):
+                nc.sync.dma_start(out=wu_raw[r:P:2], in_=wu_view[r])
+
+        load_x(0, 1)
+        load_x(1, 1)
+        load_scales()
+        load_x(2, 1)
+        load_down(0)
+        load_x(3, 1)
+        load_x(4, 2)
+        load_x(6, 2)
+        load_down(1)
+        load_x(8, 4)
+        load_x(12, 4)
+        load_up()
+        for n in range(16, N_TILES, GROUP):
+            load_x(n, GROUP)
+
+        pos = const.tile([P, N_POS], F32)
+        nc.gpsimd.iota(pos[:], pattern=[[1, N_POS]], base=0, channel_multiplier=N_POS, allow_small_or_imprecise_dtypes=True)
         offset = const.tile([P, P], F32)
         nc.gpsimd.iota(offset[:], pattern=[[1, P]], base=0, channel_multiplier=-1, allow_small_or_imprecise_dtypes=True)
         low = const.tile([P, 4, N_POS], F32)
         for a in range(4):
-            nc.vector.tensor_scalar(
-                out=low[:, a], in0=pos[:].rearrange("p a b -> p (a b)"),
-                scalar1=ROPE_BASE ** (-a / HALF) / (2 * math.pi), scalar2=None, op0=ALU.mult,
-            )
+            nc.vector.tensor_scalar(out=low[:, a], in0=pos[:], scalar1=ROPE_BASE ** (-a / HALF) / (2 * math.pi), scalar2=None, op0=ALU.mult)
         ident = const.tile([P, P], F32)
         nc.vector.tensor_scalar(out=ident[:], in0=offset[:], scalar1=0.0, scalar2=None, op0=ALU.is_equal)
         turns = const.tile([P, N_POS, HALF], F32)
@@ -115,52 +122,56 @@ def tile_multilatentattention_pa_t_kernel(tc, x_bytes, x_scale, w_down, w_up, ou
                 func=ACT.Sin, scale=(2 * c - 1) * sign[entry] * 2 * math.pi, bias=(1 - c) * math.pi / 2,
             )
 
-        wd_grp = const.tile([P, 2, DL * 4], BF16, align_bytes=64, name="whole_then_wd")
-        wd_codes = const.tile([P, 2, DL], U32, align_bytes=64)
-        wd_scales = const.tile([P, 2, DL], U8, align_bytes=64)
-        wu_main_codes = const.tile([P, 4 * DH], U32, align_bytes=64)
-        wu_main_scales = const.tile([P, 4 * DH], U8, align_bytes=64)
-        wu_rope_codes = const.tile([P, H * DR], U32, align_bytes=64)
-        wu_rope_scales = const.tile([P, H * DR], U8, align_bytes=64)
-        wu_grp = {}
+        wd_grp = const.tile([P, 4, 2, P * 4], BF16, align_bytes=64, name="whole_then_wd")
+        wd_codes = const.tile([P, 4, 2, P], U32, align_bytes=64)
+        wd_scales = const.tile([P, 4, 2, P], U8, align_bytes=64)
+        wu_codes = const.tile([P, N_UP], U32, align_bytes=64)
+        wu_scales = const.tile([P, N_UP], U8, align_bytes=64)
+        K_COLS = slice(0, H * DH)
+        V_COLS = slice(H * DH, 2 * H * DH)
+        R_COLS = slice(2 * H * DH, N_UP)
 
-        def group_aside(out, in_):
+        def copy_aside(out, in_):
             nc.gpsimd.tensor_scalar(out=out, in0=in_, scalar1=1.0, scalar2=0.0, op0=ALU.mult, op1=ALU.add)
 
-        def group_direct(out, in_):
+        def copy_direct(out, in_):
             nc.vector.tensor_copy(out=out, in_=in_)
 
-        def group_down(g, blocks, group):
-            group(
-                wd_grp[:, g].rearrange("p (t q r j) -> p q t r j", t=4, r=8, j=4)[:, blocks],
-                wd_raw[g][:].rearrange("p j (q t r) -> p q t r j", t=4, r=8)[:, blocks],
+        def copy_scalar(out, in_):
+            nc.scalar.copy(out=out, in_=in_)
+
+        def group_down(g, lo, hi, copy):
+            copy(
+                wd_grp[:, :, g].rearrange("p t (m r j) -> p m t r j", r=2, j=4)[:, lo:hi],
+                wd_raw[g][:].rearrange("p j (m t r) -> p m t r j", t=4, r=2)[:, lo:hi],
             )
 
-        def quant_down():
+        def quant_down(lo, hi):
             nc.vector.quantize_mx(
-                out=wd_codes[:].rearrange("p g c -> p (g c)").bitcast(FP8X4),
-                scales=wd_scales[:].rearrange("p g c -> p (g c)"),
-                in_=wd_grp[:].rearrange("p g c -> p (g c)"),
+                out=wd_codes[:, lo:hi].rearrange("p t g c -> p (t g c)").bitcast(FP8X4),
+                scales=wd_scales[:, lo:hi].rearrange("p t g c -> p (t g c)"),
+                in_=wd_grp[:, lo:hi].rearrange("p t g c -> p (t g c)"),
             )
 
         up = wu_raw[:].rearrange("p j (h f) -> p h f j", h=H)
+        wu_grp = {}
 
-        def spent_room(spent):
-            return xg[spent][0][:].rearrange("p i g c -> p (i g c)")
+        def spent_room(n):
+            values, i = xg[n]
+            return values[:, i:].rearrange("p i g c -> p (i g c)")
 
-        def group_up_main(spent):
-            wu_grp["main"] = spent_room(spent)[:, 0:16 * DH]
-            main_grp = wu_grp["main"].rearrange("p (a h f j) -> p a h f j", a=2, h=H, j=4)
-            group_aside(main_grp[:, 0], up[:, :, 0:DH, :])
-            group_aside(main_grp[:, 1], up[:, :, DH + DR:, :])
+        def group_up(spent, part, copy):
+            cols, lo, hi = part
+            wu_grp[lo] = spent_room(spent)[:, 0:4 * H * (hi - lo)]
+            copy(wu_grp[lo].rearrange("p (h f j) -> p h f j", h=H, j=4), up[:, :, lo:hi, :])
 
-        def group_up_rope(spent):
-            wu_grp["rope"] = spent_room(spent)[:, 0:4 * H * DR]
-            group_direct(wu_grp["rope"].rearrange("p (h f j) -> p h f j", h=H, j=4), up[:, :, DH:DH + DR, :])
+        UP_K = (K_COLS, 0, DH)
+        UP_R = (R_COLS, DH, DH + DR)
+        UP_V = (V_COLS, DH + DR, 2 * DH + DR)
 
-        def quant_up():
-            nc.vector.quantize_mx(out=wu_rope_codes[:].bitcast(FP8X4), scales=wu_rope_scales[:], in_=wu_grp["rope"])
-            nc.vector.quantize_mx(out=wu_main_codes[:].bitcast(FP8X4), scales=wu_main_scales[:], in_=wu_grp["main"])
+        def quant_up(part):
+            cols, lo, hi = part
+            nc.vector.quantize_mx(out=wu_codes[:, cols].bitcast(FP8X4), scales=wu_scales[:, cols], in_=wu_grp[lo])
 
         xbf = {}
         xt = {}
@@ -169,26 +180,33 @@ def tile_multilatentattention_pa_t_kernel(tc, x_bytes, x_scale, w_down, w_up, ou
         lat = {}
         lg = {}
         lc = {}
-        main = {}
+        bank_k = {}
+        bank_v = {}
         rope = {}
-        kv = {}
+        k_out = {}
+        v_out = {}
         spill = {}
         products = {}
 
-        def x_bytes_of(n, count):
-            return x_tiles[n // GROUP][:, n % GROUP:n % GROUP + count].rearrange("p i d -> p (i d)").bitcast(FP8)
-
-        def widen(n, count=2, parts=1):
-            wide = work.tile([P, count, D], BF16, name="xbf", bufs=WIDE_BUFS)
+        def widen(n, count=1, parts=1, aside=False, spent=None):
+            if spent is None:
+                wide = work.tile([P, count, D], BF16, name="xbf%d" % count, bufs=WIDE_BUFS[count])
+            else:
+                wide = spent_room(spent)[:, 0:count * D].rearrange("p (i d) -> p i d", d=D)
+            room, j = raw[n]
+            source = room[:, j:j + count].rearrange("p i d -> p (i d)").bitcast(FP8)
             width = count * D // parts
             for part in range(parts):
                 cols = slice(part * width, (part + 1) * width)
-                nc.scalar.copy(out=wide[:].rearrange("p i d -> p (i d)")[:, cols], in_=x_bytes_of(n, count)[:, cols])
+                if aside:
+                    nc.gpsimd.tensor_copy(out=wide[:].rearrange("p i d -> p (i d)")[:, cols], in_=source[:, cols])
+                else:
+                    nc.scalar.copy(out=wide[:].rearrange("p i d -> p (i d)")[:, cols], in_=source[:, cols])
             for i in range(count):
                 xbf[n + i] = wide[:, i]
 
         def turn(n, passes=(0, 1)):
-            bank = psum.tile([P, 2, 2, P], F32, name="xt", bufs=TURN_BANKS)
+            bank = psum.tile([P, 2, 2, P], F32, name="turned")
             xt[n, passes[0]] = bank
             for g in passes:
                 values = xbf[n][:, g * K_PASS:(g + 1) * K_PASS]
@@ -196,7 +214,7 @@ def tile_multilatentattention_pa_t_kernel(tc, x_bytes, x_scale, w_down, w_up, ou
                     nc.tensor.transpose(bank[:, u, g, :], values.bitcast(F32)[:, u::2], ident[:])
 
         def open_x(lo, count):
-            values = work.tile([P, count, 2, P * 4], BF16, name="xg", align_bytes=64, bufs=4)
+            values = work.tile([P, count, 2, P * 4], BF16, name="xg", align_bytes=64, bufs=XG_BUFS)
             codes = work.tile([P, count, 2, P], U32, name="xcodes", align_bytes=64)
             scales = work.tile([P, count, 2, P], U8, name="xscales", align_bytes=64)
             for i in range(count):
@@ -222,8 +240,8 @@ def tile_multilatentattention_pa_t_kernel(tc, x_bytes, x_scale, w_down, w_up, ou
                 in_=values[:, i:i + count].rearrange("p i g c -> p (i g c)"),
             )
 
-        def down(n):
-            bank = psum.tile([P, 4, P], F32, name="product")
+        def down(n, tag="product"):
+            bank = psum.tile([P, 4, P], F32, name=tag)
             lat[n] = bank
             codes, scales = xc[n]
             i = xg[n][1]
@@ -231,19 +249,16 @@ def tile_multilatentattention_pa_t_kernel(tc, x_bytes, x_scale, w_down, w_up, ou
                 for g in range(2):
                     nc.tensor.matmul_mx(
                         out=bank[:, t, :],
-                        lhsT=wd_codes[:, g, t * P:(t + 1) * P].bitcast(FP8X4),
-                        lhsT_scale=wd_scales[:, g, t * P:(t + 1) * P],
-                        rhs=codes[:, i, g].bitcast(FP8X4),
-                        rhs_scale=scales[:, i, g],
-                        start=(g == 0),
-                        stop=(g == 1),
+                        lhsT=wd_codes[:, t, g].bitcast(FP8X4), lhsT_scale=wd_scales[:, t, g],
+                        rhs=codes[:, i, g].bitcast(FP8X4), rhs_scale=scales[:, i, g],
+                        start=(g == 0), stop=(g == 1),
                     )
 
-        def empty_down(n):
+        def empty_down(n, copy=copy_scalar):
             g, i = divmod(n, GROUP)
-            if i == 0:
+            if g not in lg:
                 lg[g] = work.tile([P, GROUP, P, 4], BF16, name="lg", align_bytes=64)
-            nc.scalar.copy(out=lg[g][:, i], in_=lat[n][:].rearrange("p t r -> p r t"))
+            copy(lg[g][:, i], lat[n][:].rearrange("p t r -> p r t"))
 
         def quant_lat(n, count):
             g, i = divmod(n, GROUP)
@@ -258,47 +273,51 @@ def tile_multilatentattention_pa_t_kernel(tc, x_bytes, x_scale, w_down, w_up, ou
                 in_=lg[g][:, i:i + count].rearrange("p i r t -> p (i r t)"),
             )
 
-        def expand(out, n, w_codes, w_scales):
-            g, i = divmod(n, GROUP)
-            codes, scales = lc[g]
-            nc.tensor.matmul_mx(
-                out=out,
-                lhsT=codes[:, i].bitcast(FP8X4), lhsT_scale=scales[:, i],
-                rhs=w_codes[:].bitcast(FP8X4), rhs_scale=w_scales[:],
-                start=True, stop=True,
-            )
+        def expand(n, count, cols, tag):
+            bank = psum.tile([P, count, cols.stop - cols.start], F32, name=tag)
+            for j in range(count):
+                g, i = divmod(n + j, GROUP)
+                codes, scales = lc[g]
+                nc.tensor.matmul_mx(
+                    out=bank[:, j],
+                    lhsT=codes[:, i].bitcast(FP8X4), lhsT_scale=scales[:, i],
+                    rhs=wu_codes[:, cols].bitcast(FP8X4), rhs_scale=wu_scales[:, cols],
+                    start=True, stop=True,
+                )
+            return bank
 
-        def expand_main(n, tag="product"):
-            main[n] = psum.tile([P, 4, DH], F32, name=tag)
-            expand(main[n][:].rearrange("p a f -> p (a f)"), n, wu_main_codes, wu_main_scales)
+        def up_k(n, count=2, tag="product"):
+            bank_k[n] = expand(n, count, K_COLS, tag)
 
-        def expand_rope(n, count, tag="product"):
-            rope[n] = psum.tile([P, count, H * DR], F32, name=tag)
-            for i in range(count):
-                expand(rope[n][:, i], n + i, wu_rope_codes, wu_rope_scales)
+        def up_v(n, count=2, tag="product"):
+            bank_v[n] = expand(n, count, V_COLS, tag)
 
-        def out_tile(g):
-            if g not in kv:
-                kv[g] = outp.tile([P, 2, GROUP, H, DH + DR], F32, name="kv")
-            return kv[g]
+        def up_rope(n, count, tag="product"):
+            rope[n] = expand(n, count, R_COLS, tag)
 
-        def v_rows(g):
-            if g < DENSE_V:
-                return out_tile(g)[:, 1, :, :, 0:DH]
-            return out_tile(g)[:, 1].rearrange("p i h f -> p (i h f)")[:, 0:GROUP * H * DH].rearrange("p (i h f) -> p i h f", h=H, f=DH)
-
-        def empty_main(n, on_vector=False):
-            g, i = divmod(n, GROUP)
-            bank = main[n][:].rearrange("p (a h) f -> p a h f", h=H)
-            if g < DENSE_V:
-                parts = [(out_tile(g)[:, :, i, :, 0:DH], bank)]
+        def open_k(n, spent=None):
+            if spent is None:
+                room = work.tile([P, GROUP * H * (DH + DR)], F32, name="k_out")
+                room = room[:]
             else:
-                parts = [(v_rows(g)[:, i], bank[:, 1]), (out_tile(g)[:, 0, i, :, 0:DH], bank[:, 0])]
-            for out, in_ in parts:
-                if on_vector:
-                    nc.vector.tensor_copy(out=out, in_=in_)
-                else:
-                    nc.scalar.copy(out=out, in_=in_)
+                room = spent_room(spent).bitcast(F32)[:, 0:GROUP * H * (DH + DR)]
+            k_out[n // GROUP] = room.rearrange("p (i h f) -> p i h f", h=H, f=DH + DR)
+
+        def k_tile(g):
+            return k_out[g]
+
+        def v_tile(g):
+            if g not in v_out:
+                v_out[g] = work.tile([P, GROUP, H * DH], F32, name="v_out")
+            return v_out[g]
+
+        def empty_k(n, count=2, copy=copy_scalar):
+            g, i = divmod(n, GROUP)
+            copy(k_tile(g)[:, i:i + count, :, 0:DH], bank_k[n][:].rearrange("p i (h f) -> p i h f", h=H))
+
+        def empty_v(n, count=2, copy=copy_scalar):
+            g, i = divmod(n, GROUP)
+            copy(v_tile(g)[:, i:i + count], bank_v[n][:])
 
         def spill_rope(n):
             spill[n] = work.tile([P, GROUP, H * DR], F32, name="spill", bufs=2)
@@ -306,7 +325,7 @@ def tile_multilatentattention_pa_t_kernel(tc, x_bytes, x_scale, w_down, w_up, ou
 
         def open_products(n, count, spent=None):
             if spent is None:
-                room = work.tile([P, count * H * 2 * DR], F32, name="products", bufs=2)
+                room = work.tile([P, count * H * 2 * DR], F32, name="products", bufs=3)
                 room = room[:]
             else:
                 room = spent_room(spent).bitcast(F32)[:, 0:count * H * 2 * DR]
@@ -325,14 +344,14 @@ def tile_multilatentattention_pa_t_kernel(tc, x_bytes, x_scale, w_down, w_up, ou
         def rope_add(engine, n, count):
             g, i = divmod(n, GROUP)
             engine.tensor_tensor(
-                out=out_tile(g)[:, 0, i:i + count, :, DH:].rearrange("p i h f -> p (i h) f"),
+                out=k_tile(g)[:, i:i + count, :, DH:].rearrange("p i h f -> p (i h) f"),
                 in0=products[n][:, :, :, 0].rearrange("p i h c f -> p (i h) (c f)"),
                 in1=products[n][:, :, :, 1].rearrange("p i h c f -> p (i h) (c f)"),
                 op=ALU.add,
             )
 
         def rope_aside(n, spent):
-            expand_rope(n, GROUP)
+            up_rope(n, GROUP)
             spill_rope(n)
             open_products(n, GROUP, spent)
             rope_products(nc.gpsimd, spill[n][:], n, GROUP)
@@ -344,45 +363,46 @@ def tile_multilatentattention_pa_t_kernel(tc, x_bytes, x_scale, w_down, w_up, ou
 
         def store_v(n, count):
             g, i = divmod(n, GROUP)
-            nc.sync.dma_start(out=v_view[g][:, H * i:H * (i + count)], in_=v_rows(g)[:, i:i + count].rearrange("p i h f -> p (i h) f"))
+            b, at = divmod(n, N_POS)
+            nc.sync.dma_start(out=v_view[b][:, at:at + count], in_=v_out[g][:, i:i + count])
 
         def store_k(n, count):
             g, i = divmod(n, GROUP)
-            nc.sync.dma_start(out=k_view[g][:, i:i + count], in_=kv[g][:, 0, i:i + count].rearrange("p i h f -> p i (h f)"))
+            b, at = divmod(n, N_POS)
+            nc.sync.dma_start(out=k_view[b][:, at:at + count], in_=k_out[g][:, i:i + count].rearrange("p i h f -> p i (h f)"))
 
-        def store(n, count):
-            store_v(n, count)
-            store_k(n, count)
+        def first(n, tag="product", copy=copy_scalar):
+            down(n, tag)
+            empty_down(n, copy)
 
-        def first(n):
-            down(n)
-            empty_down(n)
+        def second_v(n, count=2, tag="product", copy=copy_scalar):
+            up_v(n, count, tag)
+            empty_v(n, count, copy)
 
-        def second(n):
-            expand_main(n)
-            empty_main(n)
+        def second_k(n, count=2, tag="product", copy=copy_scalar):
+            up_k(n, count, tag)
+            empty_k(n, count, copy)
 
         table_slow(1)
         table_slow(0)
-        widen(0, 1, parts=2)
-        widen(1, 1)
-        group_down(0, slice(0, BLOCKS), group_aside)
-        group_down(1, slice(0, BLOCKS - VECTOR_BLOCKS), group_aside)
-        widen(2, 1)
+        widen(0, parts=2)
+        widen(1)
+        group_down(0, 0, 64, copy_aside)
+        group_down(1, 0, ASIDE_BLOCKS, copy_aside)
+        widen(2)
         table_fast(0)
         table_fast(1)
         table_slow(2)
-        widen(3, 1)
-        widen(4)
-        widen(6)
+        widen(3)
+        widen(4, 2)
+        widen(6, 2)
         table_fast(2)
         table_fast(3)
         table_slow(3)
         for n in (8, 10, 12):
-            widen(n)
-        head = GROUP + SHIFT
-        open_x(0, SHIFT)
-        open_x(SHIFT, GROUP)
+            widen(n, 2)
+        open_x(0, 2)
+        open_x(2, GROUP)
         turn(0, (0,))
         turn(0, (1,))
         turn(1)
@@ -390,142 +410,162 @@ def tile_multilatentattention_pa_t_kernel(tc, x_bytes, x_scale, w_down, w_up, ou
         scale_x(0, (0,))
         turn(3)
         scale_x(0, (1,))
-        for n in range(1, head - 1):
+        for n in range(1, 5):
             turn(n + 3)
             scale_x(n)
-        scale_x(head - 1)
-        turn(head + 2)
-        turn(head + 3)
-        widen(14)
-        widen(16)
-        group_down(1, slice(BLOCKS - VECTOR_BLOCKS, BLOCKS), group_direct)
-        quant_x(0, SHIFT)
-        quant_down()
-        quant_x(SHIFT, GROUP)
-        group_up_main(SHIFT)
-        for n in range(SHIFT):
-            first(n)
+        scale_x(5)
+        turn(8)
+        group_down(1, ASIDE_BLOCKS, 64, copy_direct)
+        quant_x(0, 1)
+        quant_down(0, 2)
+        quant_down(2, 4)
+        quant_x(1, 1)
+        quant_x(2, GROUP)
+        group_up(2, UP_V, copy_aside)
+        group_up(3, UP_K, copy_aside)
+        group_up(4, UP_R, copy_aside)
+        turn(9)
+        widen(14, 2)
+        first(0)
+        first(1)
+        to_widen = list(range(16, N_TILES))
+        share = {1: 4, 2: 4, 3: 2, 4: 2, 5: 2}
 
-        to_widen = list(range(18, N_TILES))
+        def widen_next(todo):
+            while todo > 0:
+                n = to_widen[0]
+                count = 2 if todo >= 2 and n % 2 == 0 and n + 1 in to_widen else 1
+                widen(n, count)
+                for step in range(count):
+                    to_widen.pop(0)
+                todo = todo - count
+
+        def products_aside(n, spent=None):
+            up_rope(n, GROUP)
+            spill_rope(n)
+            open_products(n, GROUP, spent)
+            rope_products(nc.gpsimd, spill[n][:], n, GROUP)
+
+        def finish_k(n):
+            second_k(n)
+            second_k(n + 2)
+            store_k(n, GROUP)
+
         for r in range(1, N_GROUPS - 2):
-            now = GROUP * r + SHIFT
+            now = GROUP * r + 2
             mid = now - GROUP
             old = GROUP * (r - 2)
+            older = old - GROUP
             ahead = now + GROUP
             open_x(now, GROUP)
+            if older >= 0:
+                open_k(older, mid)
+                rope_add(nc.gpsimd, older, GROUP)
             if old >= 0:
-                rope_aside(old, mid)
-                if old > 0:
-                    empty_main(old - 1)
-                    store(old - GROUP, GROUP)
-                second(old)
-                turn(now + 2)
-                turn(now + 3)
-                widen(to_widen.pop(0), 1)
-                second(old + 1)
-            before = GROUP if old >= 0 else 2
-            for n in range(mid, mid + before):
+                products_aside(old, None if older >= 0 else mid)
+                second_v(old)
+                second_v(old + 2)
+                store_v(old, GROUP)
+            for n in range(now, now + GROUP):
+                scale_x(n)
+            if r == 1:
+                widen_next(2)
+            for n in range(mid, mid + GROUP):
                 first(n)
-            scale_x(now)
-            scale_x(now + 1)
-            turn(ahead)
-            turn(ahead + 1)
-            for n in to_widen[:2]:
-                widen(n, 1)
-            to_widen = to_widen[2:]
-            for n in range(mid + before, mid + GROUP):
-                first(n)
-            if old >= 0:
-                expand_main(old + 2)
-                expand_main(old + 3)
-                empty_main(old + 2)
-            else:
-                widen(to_widen.pop(0), 1)
-            scale_x(now + 2)
-            scale_x(now + 3)
-            if old < 0:
-                group_up_rope(0)
+            if older >= 0:
+                finish_k(older)
+            for n in range(ahead, ahead + GROUP):
+                turn(n)
+            widen_next(share.get(r, 0))
             quant_lat(old + GROUP, GROUP)
-            if old < 0:
-                quant_up()
+            if r == 1:
+                quant_up(UP_R)
+                quant_up(UP_V)
+                quant_up(UP_K)
             quant_x(now, GROUP)
-
-        now = N_TILES - SHIFT - GROUP
+        now = N_TILES - 2 - GROUP
         mid = now - GROUP
-        old = mid - GROUP - SHIFT
+        old = mid - 2 - GROUP
+        older = old - GROUP
         open_x(now, GROUP)
-        rope_aside(old, mid)
-        empty_main(old - 1)
-        store(old - GROUP, GROUP)
-        second(old)
-        turn(now + 2)
-        turn(now + 3)
-        second(old + 1)
+        open_k(older, mid)
+        open_k(old)
+        rope_add(nc.gpsimd, older, GROUP)
+        products_aside(old)
+        finish_k(older)
+        second_v(old)
+        second_v(old + 2)
+        store_v(old, GROUP)
+        for n in range(now, now + GROUP):
+            scale_x(n)
         first(mid)
         first(mid + 1)
-        second(old + 2)
-        second(old + 3)
-        store(old, GROUP)
-        scale_x(now)
-        scale_x(now + 1)
-        turn(now + 4)
-        turn(now + 5)
+        second_k(old)
+        second_k(old + 2)
         first(mid + 2)
         first(mid + 3)
-        scale_x(now + 2)
-        scale_x(now + 3)
         quant_lat(old + GROUP, GROUP)
+        rope_add(nc.vector, old, GROUP)
+        store_k(old, GROUP)
         quant_x(now, GROUP)
-
         a, b, c, d, e, f = range(N_TILES - 12, N_TILES, 2)
+        for n in (a, c, e):
+            open_k(n)
         open_x(f, 2)
-        expand_rope(a, GROUP, "xt")
-        second(a)
-        second(a + 1)
-        products_direct(a, GROUP)
         quant_lat(c, 2)
-        rope_add(nc.gpsimd, a, GROUP)
-        store(a, 2)
+        up_rope(a, 2, "turned")
+        up_rope(b, 2, "turned")
+        second_v(a)
+        second_v(b)
+        store_v(a, GROUP)
+        turn(f)
+        turn(f + 1)
+        products_direct(a, 2)
+        rope_add(nc.gpsimd, a, 2)
+        products_direct(b, 2)
+        rope_add(nc.gpsimd, b, 2)
+        second_k(a)
+        store_k(a, 2)
+        up_rope(c, 2, "turned")
+        second_k(b)
+        store_k(b, 2)
+        products_direct(c, 2)
+        rope_add(nc.gpsimd, c, 2)
+        second_v(c)
+        store_v(c, 2)
         first(d)
         first(d + 1)
-        second(b)
-        second(b + 1)
-        store(b, 2)
+        second_k(c)
+        store_k(c, 2)
         scale_x(f)
-        expand_rope(c, 2, "xt")
         scale_x(f + 1)
         first(e)
         first(e + 1)
         quant_lat(d, 2)
         quant_x(f, 2)
-        second(c)
-        second(c + 1)
-        products_direct(c, 2)
-        rope_add(nc.gpsimd, c, 2)
-        store(c, 2)
-        expand_rope(d, 2, "xt")
-        first(f)
-        first(f + 1)
-        expand_main(d, "xt")
-        expand_main(d + 1, "xt")
+        up_rope(d, 2, "turned")
+        second_v(d, tag="turned")
+        store_v(d, 2)
         products_direct(d, 2)
+        second_k(d, tag="turned")
         quant_lat(e, 2)
-        rope_add(nc.gpsimd, d, 2)
-        empty_main(d, on_vector=True)
-        quant_lat(f, 2)
-        empty_main(d + 1)
-        store(d, 2)
-        expand_rope(e, 2, "xt")
-        second(e)
-        second(e + 1)
+        rope_add(nc.vector, d, 2)
+        store_k(d, 2)
+        first(f)
+        down(f + 1)
+        up_rope(e, 2, "turned")
+        second_v(e)
+        store_v(e, 2)
+        empty_down(f + 1, copy_direct)
         products_direct(e, 2)
-        expand_rope(f, 2, "xt")
-        expand_main(f)
-        expand_main(f + 1, "xt")
-        rope_add(nc.gpsimd, e, 2)
-        store(e, 2)
+        quant_lat(f, 2)
+        rope_add(nc.vector, e, 2)
+        second_k(e)
+        store_k(e, 2)
+        up_rope(f, 2, "turned")
+        second_v(f, tag="turned")
+        store_v(f, 2)
         products_direct(f, 2)
-        empty_main(f)
-        empty_main(f + 1, on_vector=True)
+        second_k(f)
         rope_add(nc.vector, f, 2)
-        store(f, 2)
+        store_k(f, 2)

@@ -123,10 +123,10 @@ def tile_multilatentattention_pa_t_kernel(tc, x_bytes, x_scale, w_down, w_up, ou
             )
 
         wd_grp = const.tile([P, 4, 2, P * 4], BF16, align_bytes=64, name="whole_then_wd")
-        wd_codes = const.tile([P, 4, 2, P], U32, align_bytes=64)
-        wd_scales = const.tile([P, 4, 2, P], U8, align_bytes=64)
-        wu_codes = const.tile([P, N_UP], U32, align_bytes=64)
-        wu_scales = const.tile([P, N_UP], U8, align_bytes=64)
+        wd_codes = const.tile([P, 4, 2, P], U32, align_bytes=256)
+        wd_scales = const.tile([P, 4, 2, P], U8, align_bytes=256)
+        wu_codes = const.tile([P, N_UP], U32, align_bytes=256)
+        wu_scales = const.tile([P, N_UP], U8, align_bytes=256)
         K_COLS = slice(0, H * DH)
         V_COLS = slice(H * DH, 2 * H * DH)
         R_COLS = slice(2 * H * DH, N_UP)
@@ -215,8 +215,8 @@ def tile_multilatentattention_pa_t_kernel(tc, x_bytes, x_scale, w_down, w_up, ou
 
         def open_x(lo, count):
             values = work.tile([P, count, 2, P * 4], BF16, name="xg", align_bytes=64, bufs=XG_BUFS)
-            codes = work.tile([P, count, 2, P], U32, name="xcodes", align_bytes=64)
-            scales = work.tile([P, count, 2, P], U8, name="xscales", align_bytes=64)
+            codes = work.tile([P, count, 2, P], U32, name="xcodes", align_bytes=256)
+            scales = work.tile([P, count, 2, P], U8, name="xscales", align_bytes=256)
             for i in range(count):
                 xg[lo + i] = (values, i)
                 xc[lo + i] = (codes, scales)
@@ -263,8 +263,8 @@ def tile_multilatentattention_pa_t_kernel(tc, x_bytes, x_scale, w_down, w_up, ou
         def quant_lat(n, count):
             g, i = divmod(n, GROUP)
             if g not in lc:
-                codes = work.tile([P, GROUP, P], U32, name="lcodes", align_bytes=64)
-                scales = work.tile([P, GROUP, P], U8, name="lscales", align_bytes=64)
+                codes = work.tile([P, GROUP, P], U32, name="lcodes", align_bytes=256)
+                scales = work.tile([P, GROUP, P], U8, name="lscales", align_bytes=256)
                 lc[g] = (codes, scales)
             codes, scales = lc[g]
             nc.vector.quantize_mx(

@@ -26,9 +26,10 @@ N_POS = S // P
 N_TILES = B * N_POS
 N_GROUPS = N_TILES // GROUP
 FAST = 24
-WIDE_BUFS = {1: 4, 2: 7}
+WIDE_BUFS = {1: 6, 2: 7}
 ASIDE_BLOCKS = 56
 XG_BUFS = 4
+ASIDE_TILES = ()
 
 
 def tile_multilatentattention_pa_t_kernel(tc, x_bytes, x_scale, w_down, w_up, out_k, out_v):
@@ -47,7 +48,8 @@ def tile_multilatentattention_pa_t_kernel(tc, x_bytes, x_scale, w_down, w_up, ou
 
         wd_raw = [const.tile([P, 4, DL], BF16, name="wd_raw%d" % g) for g in range(2)]
         wu_raw = const.tile([P, 4, N_UP], BF16)
-        scale_cols = const.tile([P, 2, 4], F32)
+        scale_rows = const.tile([P, 2, 8], F32)
+        scale_cols = scale_rows[:, :, 0:4]
         raw = {}
 
         def load_x(n, count):
@@ -58,7 +60,7 @@ def tile_multilatentattention_pa_t_kernel(tc, x_bytes, x_scale, w_down, w_up, ou
                 raw[n + j] = (room, j)
 
         def load_scales():
-            nc.sync.dma_start(out=scale_cols[:], in_=x_scale.rearrange("a b (g p t) -> p (a b g) t", p=P, t=4))
+            nc.sync.dma_start(out=scale_cols, in_=x_scale.rearrange("a b (g p t) -> p (a b g) t", p=P, t=4))
 
         def load_down(g):
             nc.sync.dma_start(out=wd_raw[g][:], in_=wd_view[g])
@@ -82,28 +84,30 @@ def tile_multilatentattention_pa_t_kernel(tc, x_bytes, x_scale, w_down, w_up, ou
         for n in range(16, N_TILES, GROUP):
             load_x(n, GROUP)
 
-        pos = const.tile([P, N_POS], F32)
-        nc.gpsimd.iota(pos[:], pattern=[[1, N_POS]], base=0, channel_multiplier=N_POS, allow_small_or_imprecise_dtypes=True)
         offset = const.tile([P, P], F32)
         nc.gpsimd.iota(offset[:], pattern=[[1, P]], base=0, channel_multiplier=-1, allow_small_or_imprecise_dtypes=True)
+        lift = const.tile([P, 1], F32)
+        nc.vector.tensor_scalar(out=lift[:], in0=offset[:, 0:1], scalar1=-(N_POS + 1.0), scalar2=None, op0=ALU.mult)
+        ident = const.tile([P, P], F32)
         low = const.tile([P, 4, N_POS], F32)
         for a in range(4):
-            nc.vector.tensor_scalar(out=low[:, a], in0=pos[:], scalar1=ROPE_BASE ** (-a / HALF) / (2 * math.pi), scalar2=None, op0=ALU.mult)
-        ident = const.tile([P, P], F32)
-        nc.vector.tensor_scalar(out=ident[:], in0=offset[:], scalar1=0.0, scalar2=None, op0=ALU.is_equal)
+            nc.vector.tensor_scalar(
+                out=low[:, a], in0=offset[:, 0:N_POS], scalar1=lift[:], scalar2=ROPE_BASE ** (-a / HALF) / (2 * math.pi),
+                op0=ALU.add, op1=ALU.mult,
+            )
         turns = const.tile([P, N_POS, HALF], F32)
         for b in reversed(range(HALF // 4)):
             nc.vector.tensor_scalar(
                 out=turns[:, :, 4 * b:4 * b + 4], in0=low[:].rearrange("p a n -> p n a"),
                 scalar1=ROPE_BASE ** (-4 * b / HALF), scalar2=None, op0=ALU.mult,
             )
-        whole = const.tile([P, 2, N_POS, FAST], I32, name="whole_then_wd", align_bytes=64)
+        whole = const.tile([P, N_POS, FAST], I32, name="whole_then_wd", align_bytes=64)
         frac = const.tile([P, 2, N_POS, FAST], F32)
         trig = const.tile([P, N_POS, 4, HALF], F32)
-        for c in range(2):
-            nc.vector.tensor_scalar(out=whole[:, c], in0=turns[:, :, 0:FAST], scalar1=0.25 * (1 - c), scalar2=None, op0=ALU.add)
-        for c in range(2):
-            nc.vector.tensor_tensor(out=frac[:, c], in0=turns[:, :, 0:FAST], in1=whole[:, c], op=ALU.subtract)
+        nc.vector.tensor_copy(out=whole[:], in_=turns[:, :, 0:FAST])
+        nc.vector.tensor_scalar(out=ident[:], in0=offset[:], scalar1=0.0, scalar2=None, op0=ALU.is_equal)
+        nc.vector.tensor_tensor(out=frac[:, 1], in0=turns[:, :, 0:FAST], in1=whole[:], op=ALU.subtract)
+        nc.vector.scalar_tensor_tensor(out=frac[:, 0], in0=frac[:, 1], scalar=-1.0, in1=frac[:, 1], op0=ALU.mult, op1=ALU.max)
 
         is_sine = (0, 1, 1, 0)
         sign = (1.0, 1.0, -1.0, 1.0)
@@ -112,7 +116,7 @@ def tile_multilatentattention_pa_t_kernel(tc, x_bytes, x_scale, w_down, w_up, ou
             c = is_sine[entry]
             nc.scalar.activation(
                 out=trig[:, :, entry, 0:FAST], in_=frac[:, c],
-                func=ACT.Sin, scale=sign[entry] * 2 * math.pi, bias=(1 - c) * math.pi / 2,
+                func=ACT.Sin, scale=(2 * c - 1) * sign[entry] * 2 * math.pi, bias=(1 - c) * math.pi / 2,
             )
 
         def table_slow(entry):
@@ -121,6 +125,10 @@ def tile_multilatentattention_pa_t_kernel(tc, x_bytes, x_scale, w_down, w_up, ou
                 out=trig[:, :, entry, FAST:], in_=turns[:, :, FAST:],
                 func=ACT.Sin, scale=(2 * c - 1) * sign[entry] * 2 * math.pi, bias=(1 - c) * math.pi / 2,
             )
+
+        def table_aside():
+            nc.gpsimd.tensor_scalar(out=trig[:, :, 2], in0=trig[:, :, 1], scalar1=-1.0, scalar2=0.0, op0=ALU.mult, op1=ALU.add)
+            nc.gpsimd.tensor_scalar(out=trig[:, :, 3], in0=trig[:, :, 0], scalar1=1.0, scalar2=0.0, op0=ALU.mult, op1=ALU.add)
 
         wd_grp = const.tile([P, 4, 2, P * 4], BF16, align_bytes=64, name="whole_then_wd")
         wd_codes = const.tile([P, 4, 2, P], U32, align_bytes=256)
@@ -175,6 +183,8 @@ def tile_multilatentattention_pa_t_kernel(tc, x_bytes, x_scale, w_down, w_up, ou
 
         xbf = {}
         xt = {}
+        wide_of = {}
+        ordered = {}
         xg = {}
         xc = {}
         lat = {}
@@ -202,16 +212,24 @@ def tile_multilatentattention_pa_t_kernel(tc, x_bytes, x_scale, w_down, w_up, ou
                     nc.gpsimd.tensor_copy(out=wide[:].rearrange("p i d -> p (i d)")[:, cols], in_=source[:, cols])
                 else:
                     nc.scalar.copy(out=wide[:].rearrange("p i d -> p (i d)")[:, cols], in_=source[:, cols])
+            wide_of[n] = wide[:].rearrange("p i d -> p (i d)")
             for i in range(count):
                 xbf[n + i] = wide[:, i]
 
-        def turn(n, passes=(0, 1)):
-            bank = psum.tile([P, 2, 2, P], F32, name="turned")
+        def turn(n, passes=(0, 1), tag="turned"):
+            bank = psum.tile([P, 2, 2, P], F32, name=tag)
             xt[n, passes[0]] = bank
             for g in passes:
                 values = xbf[n][:, g * K_PASS:(g + 1) * K_PASS]
                 for u in range(2):
-                    nc.tensor.transpose(bank[:, u, g, :], values.bitcast(F32)[:, u::2], ident[:])
+                    words = ordered[n][:, g, u] if n in ordered else values.bitcast(F32)[:, u::2]
+                    nc.tensor.transpose(bank[:, u, g, :], words, ident[:])
+
+        def sort_words(n, count):
+            room = work.tile([P, count * 2, 2, P], U32, name="sorted", bufs=1)
+            nc.gpsimd.tensor_copy(out=room[:], in_=wide_of[n].bitcast(U32).rearrange("p (m r u) -> p m u r", r=P, u=2))
+            for i in range(count):
+                ordered[n + i] = room[:, 2 * i:2 * i + 2].bitcast(F32)
 
         def open_x(lo, count):
             values = work.tile([P, count, 2, P * 4], BF16, name="xg", align_bytes=64, bufs=XG_BUFS)
@@ -226,8 +244,19 @@ def tile_multilatentattention_pa_t_kernel(tc, x_bytes, x_scale, w_down, w_up, ou
             gs = slice(passes[0], passes[-1] + 1)
             nc.vector.tensor_tensor(
                 out=values[:, i, gs].rearrange("p g (r u e) -> p g r u e", u=2, e=2),
-                in0=xt[n, passes[0]][:, :, gs].bitcast(BF16).rearrange("p u g (r e) -> p g r u e", e=2),
+                in0=xt[n, passes[0] if (n, passes[0]) in xt else 0][:, :, gs].bitcast(BF16).rearrange("p u g (r e) -> p g r u e", e=2),
                 in1=scale_cols[:, gs].rearrange("p g (u e) -> p g u e", e=2).unsqueeze(2).to_broadcast([P, len(passes), P, 2, 2]),
+                op=ALU.mult,
+            )
+
+        def scale_aside(n, g):
+            values, i = xg[n]
+            words = work.tile([P, P, 2], F32, name="words", bufs=1)
+            nc.scalar.copy(out=words[:], in_=xt[n, 0][:, :, g].rearrange("p u r -> p r u"))
+            return lambda: nc.gpsimd.tensor_tensor(
+                out=values[:, i, g].rearrange("p (r t) -> p r t", t=4),
+                in0=words[:].bitcast(BF16),
+                in1=scale_cols[:, g].unsqueeze(1).to_broadcast([P, P, 4]),
                 op=ALU.mult,
             )
 
@@ -253,6 +282,27 @@ def tile_multilatentattention_pa_t_kernel(tc, x_bytes, x_scale, w_down, w_up, ou
                         rhs=codes[:, i, g].bitcast(FP8X4), rhs_scale=scales[:, i, g],
                         start=(g == 0), stop=(g == 1),
                     )
+
+        def down_pair(n, tag="product"):
+            tiles = (n, n + 1)
+            for m in tiles:
+                lat[m] = psum.tile([P, 4, P], F32, name=tag)
+            for t in range(4):
+                for g in range(2):
+                    for m in tiles:
+                        codes, scales = xc[m]
+                        i = xg[m][1]
+                        nc.tensor.matmul_mx(
+                            out=lat[m][:, t, :],
+                            lhsT=wd_codes[:, t, g].bitcast(FP8X4), lhsT_scale=wd_scales[:, t, g],
+                            rhs=codes[:, i, g].bitcast(FP8X4), rhs_scale=scales[:, i, g],
+                            start=(g == 0), stop=(g == 1),
+                        )
+
+        def first_pair(n):
+            down_pair(n)
+            empty_down(n)
+            empty_down(n + 1)
 
         def empty_down(n, copy=copy_scalar):
             g, i = divmod(n, GROUP)
@@ -319,8 +369,8 @@ def tile_multilatentattention_pa_t_kernel(tc, x_bytes, x_scale, w_down, w_up, ou
             g, i = divmod(n, GROUP)
             copy(v_tile(g)[:, i:i + count], bank_v[n][:])
 
-        def spill_rope(n):
-            spill[n] = work.tile([P, GROUP, H * DR], F32, name="spill", bufs=2)
+        def spill_rope(n, count=GROUP):
+            spill[n] = work.tile([P, count, H * DR], F32, name="spill", bufs=2)
             nc.scalar.copy(out=spill[n][:], in_=rope[n][:])
 
         def open_products(n, count, spent=None):
@@ -361,10 +411,10 @@ def tile_multilatentattention_pa_t_kernel(tc, x_bytes, x_scale, w_down, w_up, ou
             open_products(n, count)
             rope_products(nc.vector, rope[n][:], n, count)
 
-        def store_v(n, count):
+        def store_v(n, count, queue=nc.sync):
             g, i = divmod(n, GROUP)
             b, at = divmod(n, N_POS)
-            nc.sync.dma_start(out=v_view[b][:, at:at + count], in_=v_out[g][:, i:i + count])
+            queue.dma_start(out=v_view[b][:, at:at + count], in_=v_out[g][:, i:i + count])
 
         def store_k(n, count):
             g, i = divmod(n, GROUP)
@@ -396,6 +446,7 @@ def tile_multilatentattention_pa_t_kernel(tc, x_bytes, x_scale, w_down, w_up, ou
         widen(3)
         widen(4, 2)
         widen(6, 2)
+        group_down(1, ASIDE_BLOCKS, 64, copy_scalar)
         table_fast(2)
         table_fast(3)
         table_slow(3)
@@ -415,21 +466,23 @@ def tile_multilatentattention_pa_t_kernel(tc, x_bytes, x_scale, w_down, w_up, ou
             scale_x(n)
         scale_x(5)
         turn(8)
-        group_down(1, ASIDE_BLOCKS, 64, copy_direct)
         quant_x(0, 1)
         quant_down(0, 2)
         quant_down(2, 4)
         quant_x(1, 1)
         quant_x(2, GROUP)
         group_up(2, UP_V, copy_aside)
-        group_up(3, UP_K, copy_aside)
-        group_up(4, UP_R, copy_aside)
         turn(9)
+        open_x(6, GROUP)
+        scale_aside(9, 1)()
+        group_up(3, UP_R, copy_aside)
         widen(14, 2)
         first(0)
         first(1)
+        first(2)
+        first(3)
         to_widen = list(range(16, N_TILES))
-        share = {1: 4, 2: 4, 3: 2, 4: 2, 5: 2}
+        share = {1: 5, 2: 4, 3: 3, 4: 2, 5: 2}
 
         def widen_next(todo):
             while todo > 0:
@@ -457,21 +510,23 @@ def tile_multilatentattention_pa_t_kernel(tc, x_bytes, x_scale, w_down, w_up, ou
             old = GROUP * (r - 2)
             older = old - GROUP
             ahead = now + GROUP
-            open_x(now, GROUP)
+            if now not in xg:
+                open_x(now, GROUP)
             if older >= 0:
                 open_k(older, mid)
                 rope_add(nc.gpsimd, older, GROUP)
+            if old == 0:
+                group_up(mid, UP_K, copy_aside)
             if old >= 0:
-                products_aside(old, None if older >= 0 else mid)
+                products_aside(old)
                 second_v(old)
                 second_v(old + 2)
                 store_v(old, GROUP)
             for n in range(now, now + GROUP):
-                scale_x(n)
-            if r == 1:
-                widen_next(2)
+                scale_x(n, (0,) if n == 9 else (0, 1))
             for n in range(mid, mid + GROUP):
-                first(n)
+                if n not in lat:
+                    first(n)
             if older >= 0:
                 finish_k(older)
             for n in range(ahead, ahead + GROUP):
@@ -481,6 +536,7 @@ def tile_multilatentattention_pa_t_kernel(tc, x_bytes, x_scale, w_down, w_up, ou
             if r == 1:
                 quant_up(UP_R)
                 quant_up(UP_V)
+            if r == 2:
                 quant_up(UP_K)
             quant_x(now, GROUP)
         now = N_TILES - 2 - GROUP

@@ -26,7 +26,7 @@ N_POS = S // P
 N_TILES = B * N_POS
 N_GROUPS = N_TILES // GROUP
 FAST = 24
-WIDE_BUFS = {1: 6, 2: 7}
+WIDE_BUFS = {1: 2, 2: 5, 4: 7}
 ASIDE_BLOCKS = 56
 XG_BUFS = 4
 ASIDE_TILES = ()
@@ -198,38 +198,25 @@ def tile_multilatentattention_pa_t_kernel(tc, x_bytes, x_scale, w_down, w_up, ou
         spill = {}
         products = {}
 
-        def widen(n, count=1, parts=1, aside=False, spent=None):
-            if spent is None:
-                wide = work.tile([P, count, D], BF16, name="xbf%d" % count, bufs=WIDE_BUFS[count])
-            else:
-                wide = spent_room(spent)[:, 0:count * D].rearrange("p (i d) -> p i d", d=D)
-            room, j = raw[n]
-            source = room[:, j:j + count].rearrange("p i d -> p (i d)").bitcast(FP8)
-            width = count * D // parts
-            for part in range(parts):
-                cols = slice(part * width, (part + 1) * width)
-                if aside:
-                    nc.gpsimd.tensor_copy(out=wide[:].rearrange("p i d -> p (i d)")[:, cols], in_=source[:, cols])
-                else:
-                    nc.scalar.copy(out=wide[:].rearrange("p i d -> p (i d)")[:, cols], in_=source[:, cols])
-            wide_of[n] = wide[:].rearrange("p i d -> p (i d)")
+        def widen(n, count=1, passes=(0, 1)):
+            width = count * len(passes) * P
+            room = work.tile([P, 2, width, 2], BF16, name="wide%d" % width, bufs=WIDE_BUFS[width // P])
+            source, j = raw[n]
+            codes = source[:, j:j + count].bitcast(FP8).rearrange("p i (m u e) -> p u (i m) e", u=2, e=2)
+            codes = codes[:, :, P * passes[0]:P * passes[0] + width]
+            nc.scalar.copy(out=room[:], in_=codes)
             for i in range(count):
-                xbf[n + i] = wide[:, i]
+                for at, g in enumerate(passes):
+                    lo = P * (len(passes) * i + at)
+                    xbf[n + i, g] = room[:, :, lo:lo + P]
 
         def turn(n, passes=(0, 1), tag="turned"):
             bank = psum.tile([P, 2, 2, P], F32, name=tag)
             xt[n, passes[0]] = bank
             for g in passes:
-                values = xbf[n][:, g * K_PASS:(g + 1) * K_PASS]
                 for u in range(2):
-                    words = ordered[n][:, g, u] if n in ordered else values.bitcast(F32)[:, u::2]
+                    words = xbf[n, g][:, u].rearrange("p m e -> p (m e)").bitcast(F32)
                     nc.tensor.transpose(bank[:, u, g, :], words, ident[:])
-
-        def sort_words(n, count):
-            room = work.tile([P, count * 2, 2, P], U32, name="sorted", bufs=1)
-            nc.gpsimd.tensor_copy(out=room[:], in_=wide_of[n].bitcast(U32).rearrange("p (m r u) -> p m u r", r=P, u=2))
-            for i in range(count):
-                ordered[n + i] = room[:, 2 * i:2 * i + 2].bitcast(F32)
 
         def open_x(lo, count):
             values = work.tile([P, count, 2, P * 4], BF16, name="xg", align_bytes=64, bufs=XG_BUFS)
@@ -435,7 +422,8 @@ def tile_multilatentattention_pa_t_kernel(tc, x_bytes, x_scale, w_down, w_up, ou
 
         table_slow(1)
         table_slow(0)
-        widen(0, parts=2)
+        widen(0, 1, (0,))
+        widen(0, 1, (1,))
         widen(1)
         group_down(0, 0, 64, copy_aside)
         group_down(1, 0, ASIDE_BLOCKS, copy_aside)

@@ -19,17 +19,19 @@ FLOPS = 2 * B * S * D * DL + 2 * B * S * DL * N_UP
 ROPE_BASE = 10000.0
 
 P = 128
-K_PASS = 4 * P
 GROUP = 4
 HALF = DR // 2
 N_POS = S // P
 N_TILES = B * N_POS
-N_GROUPS = N_TILES // GROUP
 FAST = 24
+SLOW = HALF - FAST
+BLOCKS = DL // 8
 WIDE_BUFS = {1: 2, 2: 5, 4: 7}
-ASIDE_BLOCKS = 56
 XG_BUFS = 4
-ASIDE_TILES = ()
+K_BUFS = 3
+V_BUFS = 3
+PROD_BUFS = 3
+ASIDE_BLOCKS = 56
 
 
 def tile_multilatentattention_pa_t_kernel(tc, x_bytes, x_scale, w_down, w_up, out_k, out_v):
@@ -47,8 +49,8 @@ def tile_multilatentattention_pa_t_kernel(tc, x_bytes, x_scale, w_down, w_up, ou
         ctx.enter_context(tc.manual_schedule())
 
         wd_raw = [const.tile([P, 4, DL], BF16, name="wd_raw%d" % g) for g in range(2)]
-        wu_raw = const.tile([P, 4, N_UP], BF16)
-        scale_rows = const.tile([P, 2, 8], F32)
+        wu_raw = const.tile([P, 4, N_UP], BF16, name="wu_raw")
+        scale_rows = const.tile([P, 2, 8], F32, name="scale_rows")
         scale_cols = scale_rows[:, :, 0:4]
         raw = {}
 
@@ -84,68 +86,64 @@ def tile_multilatentattention_pa_t_kernel(tc, x_bytes, x_scale, w_down, w_up, ou
         for n in range(16, N_TILES, GROUP):
             load_x(n, GROUP)
 
-        offset = const.tile([P, P], F32)
+        position = const.tile([P, N_POS], F32, name="position")
+        nc.gpsimd.iota(position[:], pattern=[[1, N_POS]], base=0, channel_multiplier=N_POS, allow_small_or_imprecise_dtypes=True)
+        offset = const.tile([P, P], F32, name="offset")
         nc.gpsimd.iota(offset[:], pattern=[[1, P]], base=0, channel_multiplier=-1, allow_small_or_imprecise_dtypes=True)
-        lift = const.tile([P, 1], F32)
-        nc.vector.tensor_scalar(out=lift[:], in0=offset[:, 0:1], scalar1=-(N_POS + 1.0), scalar2=None, op0=ALU.mult)
-        ident = const.tile([P, P], F32)
-        low = const.tile([P, 4, N_POS], F32)
-        for a in range(4):
+        ident = const.tile([P, P], F32, name="ident")
+        turns = const.tile([P, N_POS, HALF], F32, name="turns")
+        for j in range(FAST, HALF):
             nc.vector.tensor_scalar(
-                out=low[:, a], in0=offset[:, 0:N_POS], scalar1=lift[:], scalar2=ROPE_BASE ** (-a / HALF) / (2 * math.pi),
-                op0=ALU.add, op1=ALU.mult,
+                out=turns[:, :, j], in0=position[:], scalar1=ROPE_BASE ** (-j / HALF) / (2 * math.pi), scalar2=None, op0=ALU.mult,
             )
-        turns = const.tile([P, N_POS, HALF], F32)
-        for b in reversed(range(HALF // 4)):
-            nc.vector.tensor_scalar(
-                out=turns[:, :, 4 * b:4 * b + 4], in0=low[:].rearrange("p a n -> p n a"),
-                scalar1=ROPE_BASE ** (-4 * b / HALF), scalar2=None, op0=ALU.mult,
-            )
-        whole = const.tile([P, N_POS, FAST], I32, name="whole_then_wd", align_bytes=64)
-        frac = const.tile([P, 2, N_POS, FAST], F32)
-        trig = const.tile([P, N_POS, 4, HALF], F32)
-        nc.vector.tensor_copy(out=whole[:], in_=turns[:, :, 0:FAST])
         nc.vector.tensor_scalar(out=ident[:], in0=offset[:], scalar1=0.0, scalar2=None, op0=ALU.is_equal)
-        nc.vector.tensor_tensor(out=frac[:, 1], in0=turns[:, :, 0:FAST], in1=whole[:], op=ALU.subtract)
-        nc.vector.scalar_tensor_tensor(out=frac[:, 0], in0=frac[:, 1], scalar=-1.0, in1=frac[:, 1], op0=ALU.mult, op1=ALU.max)
+        whole = const.tile([P, 2, N_POS, FAST], I32, name="whole_then_wd", align_bytes=64)
+        for lo in range(0, FAST, SLOW):
+            nc.vector.tensor_scalar(
+                out=turns[:, :, lo:lo + SLOW], in0=turns[:, :, FAST:],
+                scalar1=ROPE_BASE ** ((FAST - lo) / HALF), scalar2=None, op0=ALU.mult,
+            )
+        for c in (1, 0):
+            for lo in range(0, FAST, SLOW):
+                nc.vector.tensor_scalar(
+                    out=whole[:, c, :, lo:lo + SLOW], in0=turns[:, :, FAST:],
+                    scalar1=ROPE_BASE ** ((FAST - lo) / HALF), scalar2=0.25 * (1 - c), op0=ALU.mult, op1=ALU.add,
+                )
+        frac = const.tile([P, 2, N_POS, FAST], F32, name="frac")
+        trig = const.tile([P, N_POS, 4, HALF], F32, name="trig")
+        for c in (1, 0):
+            nc.vector.tensor_tensor(out=frac[:, c], in0=turns[:, :, 0:FAST], in1=whole[:, c], op=ALU.subtract)
 
         is_sine = (0, 1, 1, 0)
         sign = (1.0, 1.0, -1.0, 1.0)
 
-        def table_fast(entry):
+        def table(entry, fast):
             c = is_sine[entry]
             nc.scalar.activation(
-                out=trig[:, :, entry, 0:FAST], in_=frac[:, c],
-                func=ACT.Sin, scale=(2 * c - 1) * sign[entry] * 2 * math.pi, bias=(1 - c) * math.pi / 2,
+                out=trig[:, :, entry, 0:FAST] if fast else trig[:, :, entry, FAST:], in_=frac[:, c] if fast else turns[:, :, FAST:],
+                func=ACT.Sin, scale=(1 if fast or c else -1) * sign[entry] * 2 * math.pi, bias=(1 - c) * math.pi / 2,
             )
 
-        def table_slow(entry):
-            c = is_sine[entry]
-            nc.scalar.activation(
-                out=trig[:, :, entry, FAST:], in_=turns[:, :, FAST:],
-                func=ACT.Sin, scale=(2 * c - 1) * sign[entry] * 2 * math.pi, bias=(1 - c) * math.pi / 2,
-            )
-
-        def table_aside():
-            nc.gpsimd.tensor_scalar(out=trig[:, :, 2], in0=trig[:, :, 1], scalar1=-1.0, scalar2=0.0, op0=ALU.mult, op1=ALU.add)
-            nc.gpsimd.tensor_scalar(out=trig[:, :, 3], in0=trig[:, :, 0], scalar1=1.0, scalar2=0.0, op0=ALU.mult, op1=ALU.add)
+        def table_from(entry, source, engine):
+            engine.tensor_scalar(out=trig[:, :, entry], in0=trig[:, :, source], scalar1=sign[entry], scalar2=0.0, op0=ALU.mult, op1=ALU.add)
 
         wd_grp = const.tile([P, 4, 2, P * 4], BF16, align_bytes=64, name="whole_then_wd")
-        wd_codes = const.tile([P, 4, 2, P], U32, align_bytes=256)
-        wd_scales = const.tile([P, 4, 2, P], U8, align_bytes=256)
-        wu_codes = const.tile([P, N_UP], U32, align_bytes=256)
-        wu_scales = const.tile([P, N_UP], U8, align_bytes=256)
-        K_COLS = slice(0, H * DH)
-        V_COLS = slice(H * DH, 2 * H * DH)
-        R_COLS = slice(2 * H * DH, N_UP)
+        wd_codes = const.tile([P, 4, 2, P], U32, align_bytes=256, name="wd_codes")
+        wd_scales = const.tile([P, 4, 2, P], U8, align_bytes=256, name="wd_scales")
+        wu_grp = {}
+        wu_codes = const.tile([P, N_UP], U32, align_bytes=256, name="wu_codes")
+        wu_scales = const.tile([P, N_UP], U8, align_bytes=256, name="wu_scales")
+        UP_K = (slice(0, H * DH), 0, DH)
+        UP_V = (slice(H * DH, 2 * H * DH), DH + DR, 2 * DH + DR)
+        UP_R = (slice(2 * H * DH, N_UP), DH, DH + DR)
 
-        def copy_aside(out, in_):
+        def on_gpsimd(out, in_):
             nc.gpsimd.tensor_scalar(out=out, in0=in_, scalar1=1.0, scalar2=0.0, op0=ALU.mult, op1=ALU.add)
 
-        def copy_direct(out, in_):
+        def on_vector(out, in_):
             nc.vector.tensor_copy(out=out, in_=in_)
 
-        def copy_scalar(out, in_):
+        def on_scalar(out, in_):
             nc.scalar.copy(out=out, in_=in_)
 
         def group_down(g, lo, hi, copy):
@@ -161,61 +159,53 @@ def tile_multilatentattention_pa_t_kernel(tc, x_bytes, x_scale, w_down, w_up, ou
                 in_=wd_grp[:, lo:hi].rearrange("p t g c -> p (t g c)"),
             )
 
-        up = wu_raw[:].rearrange("p j (h f) -> p h f j", h=H)
-        wu_grp = {}
-
         def spent_room(n):
-            values, i = xg[n]
+            values, codes, scales, i = xg[n]
             return values[:, i:].rearrange("p i g c -> p (i g c)")
 
-        def group_up(spent, part, copy):
+        def group_up(part, spent, copy):
             cols, lo, hi = part
             wu_grp[lo] = spent_room(spent)[:, 0:4 * H * (hi - lo)]
-            copy(wu_grp[lo].rearrange("p (h f j) -> p h f j", h=H, j=4), up[:, :, lo:hi, :])
-
-        UP_K = (K_COLS, 0, DH)
-        UP_R = (R_COLS, DH, DH + DR)
-        UP_V = (V_COLS, DH + DR, 2 * DH + DR)
+            copy(
+                wu_grp[lo].rearrange("p (h f j) -> p h f j", h=H, j=4),
+                wu_raw[:].rearrange("p j (h f) -> p h f j", h=H)[:, :, lo:hi, :],
+            )
 
         def quant_up(part):
             cols, lo, hi = part
             nc.vector.quantize_mx(out=wu_codes[:, cols].bitcast(FP8X4), scales=wu_scales[:, cols], in_=wu_grp[lo])
 
-        xbf = {}
-        xt = {}
-        wide_of = {}
-        ordered = {}
+        wide = {}
+        turned = {}
         xg = {}
-        xc = {}
         lat = {}
         lg = {}
         lc = {}
-        bank_k = {}
-        bank_v = {}
-        rope = {}
         k_out = {}
         v_out = {}
-        spill = {}
         products = {}
 
-        def widen(n, count=1, passes=(0, 1)):
+        def widen(n, count=1, passes=(0, 1), engine=None):
             width = count * len(passes) * P
             room = work.tile([P, 2, width, 2], BF16, name="wide%d" % width, bufs=WIDE_BUFS[width // P])
             source, j = raw[n]
             codes = source[:, j:j + count].bitcast(FP8).rearrange("p i (m u e) -> p u (i m) e", u=2, e=2)
             codes = codes[:, :, P * passes[0]:P * passes[0] + width]
-            nc.scalar.copy(out=room[:], in_=codes)
+            if engine is None:
+                nc.scalar.copy(out=room[:], in_=codes)
+            else:
+                engine.tensor_copy(out=room[:], in_=codes)
             for i in range(count):
                 for at, g in enumerate(passes):
                     lo = P * (len(passes) * i + at)
-                    xbf[n + i, g] = room[:, :, lo:lo + P]
+                    wide[n + i, g] = room[:, :, lo:lo + P]
 
         def turn(n, passes=(0, 1), tag="turned"):
             bank = psum.tile([P, 2, 2, P], F32, name=tag)
-            xt[n, passes[0]] = bank
             for g in passes:
+                turned[n, g] = bank
                 for u in range(2):
-                    words = xbf[n, g][:, u].rearrange("p m e -> p (m e)").bitcast(F32)
+                    words = wide[n, g][:, u].rearrange("p m e -> p (m e)").bitcast(F32)
                     nc.tensor.transpose(bank[:, u, g, :], words, ident[:])
 
         def open_x(lo, count):
@@ -223,24 +213,23 @@ def tile_multilatentattention_pa_t_kernel(tc, x_bytes, x_scale, w_down, w_up, ou
             codes = work.tile([P, count, 2, P], U32, name="xcodes", align_bytes=256)
             scales = work.tile([P, count, 2, P], U8, name="xscales", align_bytes=256)
             for i in range(count):
-                xg[lo + i] = (values, i)
-                xc[lo + i] = (codes, scales)
+                xg[lo + i] = (values, codes, scales, i)
 
         def scale_x(n, passes=(0, 1)):
-            values, i = xg[n]
+            values, codes, scales, i = xg[n]
             gs = slice(passes[0], passes[-1] + 1)
             nc.vector.tensor_tensor(
                 out=values[:, i, gs].rearrange("p g (r u e) -> p g r u e", u=2, e=2),
-                in0=xt[n, passes[0] if (n, passes[0]) in xt else 0][:, :, gs].bitcast(BF16).rearrange("p u g (r e) -> p g r u e", e=2),
+                in0=turned[n, passes[0]][:, :, gs].bitcast(BF16).rearrange("p u g (r e) -> p g r u e", e=2),
                 in1=scale_cols[:, gs].rearrange("p g (u e) -> p g u e", e=2).unsqueeze(2).to_broadcast([P, len(passes), P, 2, 2]),
                 op=ALU.mult,
             )
 
         def scale_aside(n, g):
-            values, i = xg[n]
+            values, codes, scales, i = xg[n]
             words = work.tile([P, P, 2], F32, name="words", bufs=1)
-            nc.scalar.copy(out=words[:], in_=xt[n, 0][:, :, g].rearrange("p u r -> p r u"))
-            return lambda: nc.gpsimd.tensor_tensor(
+            nc.scalar.copy(out=words[:], in_=turned[n, g][:, :, g].rearrange("p u r -> p r u"))
+            nc.gpsimd.tensor_tensor(
                 out=values[:, i, g].rearrange("p (r t) -> p r t", t=4),
                 in0=words[:].bitcast(BF16),
                 in1=scale_cols[:, g].unsqueeze(1).to_broadcast([P, P, 4]),
@@ -248,8 +237,7 @@ def tile_multilatentattention_pa_t_kernel(tc, x_bytes, x_scale, w_down, w_up, ou
             )
 
         def quant_x(n, count):
-            values, i = xg[n]
-            codes, scales = xc[n]
+            values, codes, scales, i = xg[n]
             nc.vector.quantize_mx(
                 out=codes[:, i:i + count].rearrange("p i g r -> p (i g r)").bitcast(FP8X4),
                 scales=scales[:, i:i + count].rearrange("p i g r -> p (i g r)"),
@@ -259,8 +247,7 @@ def tile_multilatentattention_pa_t_kernel(tc, x_bytes, x_scale, w_down, w_up, ou
         def down(n, tag="product"):
             bank = psum.tile([P, 4, P], F32, name=tag)
             lat[n] = bank
-            codes, scales = xc[n]
-            i = xg[n][1]
+            values, codes, scales, i = xg[n]
             for t in range(4):
                 for g in range(2):
                     nc.tensor.matmul_mx(
@@ -270,32 +257,15 @@ def tile_multilatentattention_pa_t_kernel(tc, x_bytes, x_scale, w_down, w_up, ou
                         start=(g == 0), stop=(g == 1),
                     )
 
-        def down_pair(n, tag="product"):
-            tiles = (n, n + 1)
-            for m in tiles:
-                lat[m] = psum.tile([P, 4, P], F32, name=tag)
-            for t in range(4):
-                for g in range(2):
-                    for m in tiles:
-                        codes, scales = xc[m]
-                        i = xg[m][1]
-                        nc.tensor.matmul_mx(
-                            out=lat[m][:, t, :],
-                            lhsT=wd_codes[:, t, g].bitcast(FP8X4), lhsT_scale=wd_scales[:, t, g],
-                            rhs=codes[:, i, g].bitcast(FP8X4), rhs_scale=scales[:, i, g],
-                            start=(g == 0), stop=(g == 1),
-                        )
-
-        def first_pair(n):
-            down_pair(n)
-            empty_down(n)
-            empty_down(n + 1)
-
-        def empty_down(n, copy=copy_scalar):
+        def empty_down(n, copy=on_scalar):
             g, i = divmod(n, GROUP)
             if g not in lg:
-                lg[g] = work.tile([P, GROUP, P, 4], BF16, name="lg", align_bytes=64)
+                lg[g] = work.tile([P, GROUP, P, 4], BF16, name="lg", align_bytes=64, bufs=3)
             copy(lg[g][:, i], lat[n][:].rearrange("p t r -> p r t"))
+
+        def first(n, tag="product", copy=on_scalar):
+            down(n, tag)
+            empty_down(n, copy)
 
         def quant_lat(n, count):
             g, i = divmod(n, GROUP)
@@ -310,7 +280,8 @@ def tile_multilatentattention_pa_t_kernel(tc, x_bytes, x_scale, w_down, w_up, ou
                 in_=lg[g][:, i:i + count].rearrange("p i r t -> p (i r t)"),
             )
 
-        def expand(n, count, cols, tag):
+        def expand(n, count, part, tag):
+            cols = part[0]
             bank = psum.tile([P, count, cols.stop - cols.start], F32, name=tag)
             for j in range(count):
                 g, i = divmod(n + j, GROUP)
@@ -323,56 +294,43 @@ def tile_multilatentattention_pa_t_kernel(tc, x_bytes, x_scale, w_down, w_up, ou
                 )
             return bank
 
-        def up_k(n, count=2, tag="product"):
-            bank_k[n] = expand(n, count, K_COLS, tag)
-
-        def up_v(n, count=2, tag="product"):
-            bank_v[n] = expand(n, count, V_COLS, tag)
-
-        def up_rope(n, count, tag="product"):
-            rope[n] = expand(n, count, R_COLS, tag)
-
-        def open_k(n, spent=None):
-            if spent is None:
-                room = work.tile([P, GROUP * H * (DH + DR)], F32, name="k_out")
-                room = room[:]
-            else:
-                room = spent_room(spent).bitcast(F32)[:, 0:GROUP * H * (DH + DR)]
-            k_out[n // GROUP] = room.rearrange("p (i h f) -> p i h f", h=H, f=DH + DR)
-
-        def k_tile(g):
+        def k_tile(g, spent=None):
+            if g not in k_out:
+                if spent is None:
+                    room = work.tile([P, GROUP * H * (DH + DR)], F32, name="k_out", bufs=K_BUFS)
+                    room = room[:]
+                else:
+                    room = spent_room(spent).bitcast(F32)[:, 0:GROUP * H * (DH + DR)]
+                k_out[g] = room.rearrange("p (i h f) -> p i h f", h=H, f=DH + DR)
             return k_out[g]
 
         def v_tile(g):
             if g not in v_out:
-                v_out[g] = work.tile([P, GROUP, H * DH], F32, name="v_out")
+                v_out[g] = work.tile([P, GROUP, H * DH], F32, name="v_out", bufs=V_BUFS)
             return v_out[g]
 
-        def empty_k(n, count=2, copy=copy_scalar):
+        def second_k(n, count=2, tag="product", copy=on_scalar):
+            bank = expand(n, count, UP_K, tag)
             g, i = divmod(n, GROUP)
-            copy(k_tile(g)[:, i:i + count, :, 0:DH], bank_k[n][:].rearrange("p i (h f) -> p i h f", h=H))
+            copy(k_tile(g)[:, i:i + count, :, 0:DH], bank[:].rearrange("p i (h f) -> p i h f", h=H))
 
-        def empty_v(n, count=2, copy=copy_scalar):
+        def second_v(n, count=2, tag="product", copy=on_scalar):
+            bank = expand(n, count, UP_V, tag)
             g, i = divmod(n, GROUP)
-            copy(v_tile(g)[:, i:i + count], bank_v[n][:])
+            copy(v_tile(g)[:, i:i + count], bank[:])
 
-        def spill_rope(n, count=GROUP):
-            spill[n] = work.tile([P, count, H * DR], F32, name="spill", bufs=2)
-            nc.scalar.copy(out=spill[n][:], in_=rope[n][:])
-
-        def open_products(n, count, spent=None):
+        def rope_products(engine, source, n, count, spent=None):
             if spent is None:
-                room = work.tile([P, count * H * 2 * DR], F32, name="products", bufs=3)
+                room = work.tile([P, count * H * 2 * DR], F32, name="products", bufs=PROD_BUFS)
                 room = room[:]
             else:
                 room = spent_room(spent).bitcast(F32)[:, 0:count * H * 2 * DR]
-            products[n] = room.rearrange("p (i h a c f) -> p i h a c f", h=H, a=2, c=2, f=HALF)
-
-        def rope_products(engine, source, n, count):
+            room = room.rearrange("p (i h a c f) -> p i h a c f", h=H, a=2, c=2, f=HALF)
+            products[n] = room
             shape = [P, count, H, 2, 2, HALF]
             at = n % N_POS
             engine.tensor_tensor(
-                out=products[n],
+                out=room,
                 in0=source.rearrange("p i (h a f) -> p i h a f", h=H, a=2).unsqueeze(4).to_broadcast(shape),
                 in1=trig[:, at:at + count].rearrange("p i (a c) f -> p i a c f", a=2).unsqueeze(2).to_broadcast(shape),
                 op=ALU.mult,
@@ -387,57 +345,48 @@ def tile_multilatentattention_pa_t_kernel(tc, x_bytes, x_scale, w_down, w_up, ou
                 op=ALU.add,
             )
 
-        def rope_aside(n, spent):
-            up_rope(n, GROUP)
-            spill_rope(n)
-            open_products(n, GROUP, spent)
-            rope_products(nc.gpsimd, spill[n][:], n, GROUP)
-            rope_add(nc.gpsimd, n, GROUP)
+        def products_aside(n, count=GROUP, tag="product", spent=None):
+            bank = expand(n, count, UP_R, tag)
+            spill = work.tile([P, count, H * DR], F32, name="spill", bufs=2)
+            nc.scalar.copy(out=spill[:], in_=bank[:])
+            rope_products(nc.gpsimd, spill[:], n, count, spent)
+
+        rope = {}
+
+        def up_rope(n, count, tag="product"):
+            rope[n] = expand(n, count, UP_R, tag)
 
         def products_direct(n, count):
-            open_products(n, count)
             rope_products(nc.vector, rope[n][:], n, count)
 
-        def store_v(n, count, queue=nc.sync):
+        def store_v(n, count):
             g, i = divmod(n, GROUP)
             b, at = divmod(n, N_POS)
-            queue.dma_start(out=v_view[b][:, at:at + count], in_=v_out[g][:, i:i + count])
+            nc.sync.dma_start(out=v_view[b][:, at:at + count], in_=v_out[g][:, i:i + count])
 
         def store_k(n, count):
             g, i = divmod(n, GROUP)
             b, at = divmod(n, N_POS)
             nc.sync.dma_start(out=k_view[b][:, at:at + count], in_=k_out[g][:, i:i + count].rearrange("p i h f -> p i (h f)"))
 
-        def first(n, tag="product", copy=copy_scalar):
-            down(n, tag)
-            empty_down(n, copy)
-
-        def second_v(n, count=2, tag="product", copy=copy_scalar):
-            up_v(n, count, tag)
-            empty_v(n, count, copy)
-
-        def second_k(n, count=2, tag="product", copy=copy_scalar):
-            up_k(n, count, tag)
-            empty_k(n, count, copy)
-
-        table_slow(1)
-        table_slow(0)
+        table(1, False)
         widen(0, 1, (0,))
         widen(0, 1, (1,))
         widen(1)
-        group_down(0, 0, 64, copy_aside)
-        group_down(1, 0, ASIDE_BLOCKS, copy_aside)
+        group_down(0, 0, BLOCKS, on_gpsimd)
+        group_down(1, 0, ASIDE_BLOCKS, on_gpsimd)
         widen(2)
-        table_fast(0)
-        table_fast(1)
-        table_slow(2)
+        table(0, False)
+        table(1, True)
+        table(0, True)
         widen(3)
         widen(4, 2)
         widen(6, 2)
-        group_down(1, ASIDE_BLOCKS, 64, copy_scalar)
-        table_fast(2)
-        table_fast(3)
-        table_slow(3)
+        group_down(1, ASIDE_BLOCKS, BLOCKS, on_scalar)
+        table(2, True)
+        table(3, True)
+        table(2, False)
+        table(3, False)
         for n in (8, 10, 12):
             widen(n, 2)
         open_x(0, 2)
@@ -459,40 +408,19 @@ def tile_multilatentattention_pa_t_kernel(tc, x_bytes, x_scale, w_down, w_up, ou
         quant_down(2, 4)
         quant_x(1, 1)
         quant_x(2, GROUP)
-        group_up(2, UP_V, copy_aside)
+        group_up(UP_V, 2, on_gpsimd)
         turn(9)
         open_x(6, GROUP)
-        scale_aside(9, 1)()
-        group_up(3, UP_R, copy_aside)
+        scale_aside(9, 1)
+        group_up(UP_R, 3, on_gpsimd)
         widen(14, 2)
         first(0)
         first(1)
         first(2)
         first(3)
-        to_widen = list(range(16, N_TILES))
-        share = {1: 5, 2: 4, 3: 3, 4: 2, 5: 2}
 
-        def widen_next(todo):
-            while todo > 0:
-                n = to_widen[0]
-                count = 2 if todo >= 2 and n % 2 == 0 and n + 1 in to_widen else 1
-                widen(n, count)
-                for step in range(count):
-                    to_widen.pop(0)
-                todo = todo - count
-
-        def products_aside(n, spent=None):
-            up_rope(n, GROUP)
-            spill_rope(n)
-            open_products(n, GROUP, spent)
-            rope_products(nc.gpsimd, spill[n][:], n, GROUP)
-
-        def finish_k(n):
-            second_k(n)
-            second_k(n + 2)
-            store_k(n, GROUP)
-
-        for r in range(1, N_GROUPS - 2):
+        share = {1: ((16, 2), (18, 2), (20, 1)), 2: ((21, 1), (22, 2), (24, 1)), 3: ((25, 1), (26, 2)), 4: ((28, 2),), 5: ((30, 2),)}
+        for r in range(1, 6):
             now = GROUP * r + 2
             mid = now - GROUP
             old = GROUP * (r - 2)
@@ -501,10 +429,10 @@ def tile_multilatentattention_pa_t_kernel(tc, x_bytes, x_scale, w_down, w_up, ou
             if now not in xg:
                 open_x(now, GROUP)
             if older >= 0:
-                open_k(older, mid)
+                k_tile(older // GROUP, mid)
                 rope_add(nc.gpsimd, older, GROUP)
             if old == 0:
-                group_up(mid, UP_K, copy_aside)
+                group_up(UP_K, mid, on_gpsimd)
             if old >= 0:
                 products_aside(old)
                 second_v(old)
@@ -516,10 +444,13 @@ def tile_multilatentattention_pa_t_kernel(tc, x_bytes, x_scale, w_down, w_up, ou
                 if n not in lat:
                     first(n)
             if older >= 0:
-                finish_k(older)
+                second_k(older)
+                second_k(older + 2)
+                store_k(older, GROUP)
             for n in range(ahead, ahead + GROUP):
                 turn(n)
-            widen_next(share.get(r, 0))
+            for n, count in share[r]:
+                widen(n, count)
             quant_lat(old + GROUP, GROUP)
             if r == 1:
                 quant_up(UP_R)
@@ -527,34 +458,31 @@ def tile_multilatentattention_pa_t_kernel(tc, x_bytes, x_scale, w_down, w_up, ou
             if r == 2:
                 quant_up(UP_K)
             quant_x(now, GROUP)
-        now = N_TILES - 2 - GROUP
-        mid = now - GROUP
-        old = mid - 2 - GROUP
-        older = old - GROUP
-        open_x(now, GROUP)
-        open_k(older, mid)
-        open_k(old)
-        rope_add(nc.gpsimd, older, GROUP)
-        products_aside(old)
-        finish_k(older)
-        second_v(old)
-        second_v(old + 2)
-        store_v(old, GROUP)
-        for n in range(now, now + GROUP):
+
+        open_x(26, GROUP)
+        k_tile(3, 22)
+        k_tile(4)
+        rope_add(nc.gpsimd, 12, GROUP)
+        products_aside(16)
+        second_k(12)
+        second_k(14)
+        store_k(12, GROUP)
+        second_v(16)
+        second_v(18)
+        store_v(16, GROUP)
+        for n in range(26, 30):
             scale_x(n)
-        first(mid)
-        first(mid + 1)
-        second_k(old)
-        second_k(old + 2)
-        first(mid + 2)
-        first(mid + 3)
-        quant_lat(old + GROUP, GROUP)
-        rope_add(nc.vector, old, GROUP)
-        store_k(old, GROUP)
-        quant_x(now, GROUP)
+        first(22)
+        first(23)
+        second_k(16)
+        second_k(18)
+        first(24)
+        first(25)
+        quant_lat(20, GROUP)
+        rope_add(nc.vector, 16, GROUP)
+        store_k(16, GROUP)
+        quant_x(26, GROUP)
         a, b, c, d, e, f = range(N_TILES - 12, N_TILES, 2)
-        for n in (a, c, e):
-            open_k(n)
         open_x(f, 2)
         quant_lat(c, 2)
         up_rope(a, 2, "turned")
@@ -600,7 +528,7 @@ def tile_multilatentattention_pa_t_kernel(tc, x_bytes, x_scale, w_down, w_up, ou
         up_rope(e, 2, "turned")
         second_v(e)
         store_v(e, 2)
-        empty_down(f + 1, copy_direct)
+        empty_down(f + 1, on_vector)
         products_direct(e, 2)
         quant_lat(f, 2)
         rope_add(nc.vector, e, 2)

@@ -45,7 +45,7 @@ def tile_multilatentattention_pa_t_kernel(tc, x_bytes, x_scale, w_down, w_up, ou
     with ExitStack() as ctx:
         const = ctx.enter_context(tc.tile_pool(name="const", bufs=1))
         work = ctx.enter_context(tc.tile_pool(name="work", bufs=3))
-        psum = ctx.enter_context(tc.psum_pool(name="psum", bufs=4))
+        psum = ctx.enter_context(tc.psum_pool(name="psum", bufs=1))
         ctx.enter_context(tc.manual_schedule())
 
         wd_raw = [const.tile([P, 4, DL], BF16, name="wd_raw%d" % g) for g in range(2)]
@@ -175,6 +175,15 @@ def tile_multilatentattention_pa_t_kernel(tc, x_bytes, x_scale, w_down, w_up, ou
             cols, lo, hi = part
             nc.vector.quantize_mx(out=wu_codes[:, cols].bitcast(FP8X4), scales=wu_scales[:, cols], in_=wu_grp[lo])
 
+        opened = []
+
+        def next_bank():
+            opened.append(4 + len(opened) % 4)
+            return opened[-1]
+
+        def open_bank(shape, number):
+            return psum.tile(shape, F32, name="bank%d" % (next_bank() if number is None else number))
+
         wide = {}
         turned = {}
         xg = {}
@@ -200,8 +209,8 @@ def tile_multilatentattention_pa_t_kernel(tc, x_bytes, x_scale, w_down, w_up, ou
                     lo = P * (len(passes) * i + at)
                     wide[n + i, g] = room[:, :, lo:lo + P]
 
-        def turn(n, passes=(0, 1), tag="turned"):
-            bank = psum.tile([P, 2, 2, P], F32, name=tag)
+        def turn(n, passes=(0, 1), tag=None):
+            bank = open_bank([P, 2, 2, P], n % 4 if tag is None else tag)
             for g in passes:
                 turned[n, g] = bank
                 for u in range(2):
@@ -244,8 +253,8 @@ def tile_multilatentattention_pa_t_kernel(tc, x_bytes, x_scale, w_down, w_up, ou
                 in_=values[:, i:i + count].rearrange("p i g c -> p (i g c)"),
             )
 
-        def down(n, tag="product"):
-            bank = psum.tile([P, 4, P], F32, name=tag)
+        def down(n, tag=None):
+            bank = open_bank([P, 4, P], tag)
             lat[n] = bank
             values, codes, scales, i = xg[n]
             for t in range(4):
@@ -263,7 +272,7 @@ def tile_multilatentattention_pa_t_kernel(tc, x_bytes, x_scale, w_down, w_up, ou
                 lg[g] = work.tile([P, GROUP, P, 4], BF16, name="lg", align_bytes=64, bufs=3)
             copy(lg[g][:, i], lat[n][:].rearrange("p t r -> p r t"))
 
-        def first(n, tag="product", copy=on_scalar):
+        def first(n, tag=None, copy=on_scalar):
             down(n, tag)
             empty_down(n, copy)
 
@@ -282,7 +291,7 @@ def tile_multilatentattention_pa_t_kernel(tc, x_bytes, x_scale, w_down, w_up, ou
 
         def expand(n, count, part, tag):
             cols = part[0]
-            bank = psum.tile([P, count, cols.stop - cols.start], F32, name=tag)
+            bank = open_bank([P, count, cols.stop - cols.start], tag)
             for j in range(count):
                 g, i = divmod(n + j, GROUP)
                 codes, scales = lc[g]
@@ -309,12 +318,12 @@ def tile_multilatentattention_pa_t_kernel(tc, x_bytes, x_scale, w_down, w_up, ou
                 v_out[g] = work.tile([P, GROUP, H * DH], F32, name="v_out", bufs=V_BUFS)
             return v_out[g]
 
-        def second_k(n, count=2, tag="product", copy=on_scalar):
+        def second_k(n, count=2, tag=None, copy=on_scalar):
             bank = expand(n, count, UP_K, tag)
             g, i = divmod(n, GROUP)
             copy(k_tile(g)[:, i:i + count, :, 0:DH], bank[:].rearrange("p i (h f) -> p i h f", h=H))
 
-        def second_v(n, count=2, tag="product", copy=on_scalar):
+        def second_v(n, count=2, tag=None, copy=on_scalar):
             bank = expand(n, count, UP_V, tag)
             g, i = divmod(n, GROUP)
             copy(v_tile(g)[:, i:i + count], bank[:])
@@ -345,7 +354,7 @@ def tile_multilatentattention_pa_t_kernel(tc, x_bytes, x_scale, w_down, w_up, ou
                 op=ALU.add,
             )
 
-        def products_aside(n, count=GROUP, tag="product", spent=None):
+        def products_aside(n, count=GROUP, tag=None, spent=None):
             bank = expand(n, count, UP_R, tag)
             spill = work.tile([P, count, H * DR], F32, name="spill", bufs=2)
             nc.scalar.copy(out=spill[:], in_=bank[:])
@@ -353,7 +362,7 @@ def tile_multilatentattention_pa_t_kernel(tc, x_bytes, x_scale, w_down, w_up, ou
 
         rope = {}
 
-        def up_rope(n, count, tag="product"):
+        def up_rope(n, count, tag=None):
             rope[n] = expand(n, count, UP_R, tag)
 
         def products_direct(n, count):
@@ -392,17 +401,15 @@ def tile_multilatentattention_pa_t_kernel(tc, x_bytes, x_scale, w_down, w_up, ou
         open_x(0, 2)
         open_x(2, GROUP)
         turn(0, (0,))
-        turn(0, (1,))
+        turn(0, (1,), 4)
         turn(1)
         turn(2)
-        scale_x(0, (0,))
         turn(3)
+        scale_x(0, (0,))
         scale_x(0, (1,))
-        for n in range(1, 5):
+        for n in range(1, 6):
             turn(n + 3)
             scale_x(n)
-        scale_x(5)
-        turn(8)
         quant_x(0, 1)
         quant_down(0, 2)
         quant_down(2, 4)
@@ -482,62 +489,62 @@ def tile_multilatentattention_pa_t_kernel(tc, x_bytes, x_scale, w_down, w_up, ou
         rope_add(nc.vector, 16, GROUP)
         store_k(16, GROUP)
         quant_x(26, GROUP)
-        a, b, c, d, e, f = range(N_TILES - 12, N_TILES, 2)
-        open_x(f, 2)
-        quant_lat(c, 2)
-        up_rope(a, 2, "turned")
-        up_rope(b, 2, "turned")
-        second_v(a)
-        second_v(b)
-        store_v(a, GROUP)
-        turn(f)
-        turn(f + 1)
-        products_direct(a, 2)
-        rope_add(nc.gpsimd, a, 2)
-        products_direct(b, 2)
-        rope_add(nc.gpsimd, b, 2)
-        second_k(a)
-        store_k(a, 2)
-        up_rope(c, 2, "turned")
-        second_k(b)
-        store_k(b, 2)
-        products_direct(c, 2)
-        rope_add(nc.gpsimd, c, 2)
-        second_v(c)
-        store_v(c, 2)
-        first(d)
-        first(d + 1)
-        second_k(c)
-        store_k(c, 2)
-        scale_x(f)
-        scale_x(f + 1)
-        first(e)
-        first(e + 1)
-        quant_lat(d, 2)
-        quant_x(f, 2)
-        up_rope(d, 2, "turned")
-        second_v(d, tag="turned")
-        store_v(d, 2)
-        products_direct(d, 2)
-        second_k(d, tag="turned")
-        quant_lat(e, 2)
-        rope_add(nc.vector, d, 2)
-        store_k(d, 2)
-        first(f)
-        down(f + 1)
-        up_rope(e, 2, "turned")
-        second_v(e)
-        store_v(e, 2)
-        empty_down(f + 1, on_vector)
-        products_direct(e, 2)
-        quant_lat(f, 2)
-        rope_add(nc.vector, e, 2)
-        second_k(e)
-        store_k(e, 2)
-        up_rope(f, 2, "turned")
-        second_v(f, tag="turned")
-        store_v(f, 2)
-        products_direct(f, 2)
-        second_k(f)
-        rope_add(nc.vector, f, 2)
-        store_k(f, 2)
+
+        open_x(30, 2)
+        quant_lat(24, 2)
+        up_rope(20, 2, 0)
+        up_rope(22, 2, 1)
+        second_v(20)
+        second_v(22)
+        store_v(20, GROUP)
+        products_direct(20, 2)
+        rope_add(nc.gpsimd, 20, 2)
+        products_direct(22, 2)
+        rope_add(nc.gpsimd, 22, 2)
+        second_k(20)
+        store_k(20, 2)
+        second_k(22)
+        store_k(22, 2)
+        turn(30)
+        turn(31)
+        first(26)
+        first(27)
+        up_rope(24, 2, 0)
+        scale_x(30)
+        products_direct(24, 2)
+        quant_lat(26, 2)
+        rope_add(nc.gpsimd, 24, 2)
+        second_v(24)
+        store_v(24, 2)
+        second_k(24)
+        store_k(24, 2)
+        scale_x(31)
+        first(28)
+        first(29)
+        up_rope(26, 2, 1)
+        second_v(26)
+        store_v(26, 2)
+        second_k(26)
+        quant_x(30, 1)
+        quant_x(31, 1)
+        products_direct(26, 2)
+        quant_lat(28, 2)
+        rope_add(nc.gpsimd, 26, 2)
+        store_k(26, 2)
+        first(30, 2, on_vector)
+        first(31, 3)
+        up_rope(28, 2, 0)
+        second_v(28)
+        store_v(28, 2)
+        second_k(28)
+        products_direct(28, 2)
+        quant_lat(30, 2)
+        rope_add(nc.vector, 28, 2)
+        store_k(28, 2)
+        up_rope(30, 2, 1)
+        second_v(30)
+        store_v(30, 2)
+        products_direct(30, 2)
+        second_k(30)
+        rope_add(nc.vector, 30, 2)
+        store_k(30, 2)

@@ -454,7 +454,7 @@ def tile_multilatentattention_pa_t_kernel(tc, x_bytes, x_scale, w_down, w_up, ou
                 second_k(older)
                 second_k(older + 2)
                 store_k(older, GROUP)
-            for n in range(ahead, ahead + GROUP):
+            for n in (ahead + 2, ahead + 1, ahead, ahead + 3):
                 turn(n)
             for n, count in share[r]:
                 widen(n, count)

import math
from contextlib import ExitStack

import concourse.mybir as mybir

F32 = mybir.dt.float32
BF16 = mybir.dt.bfloat16
U32 = mybir.dt.uint32
I32 = mybir.dt.int32
U8 = mybir.dt.uint8
FP8 = mybir.dt.float8_e4m3fn
FP8X4 = mybir.dt.float8_e4m3fn_x4
ALU = mybir.AluOpType
ACT = mybir.ActivationFunctionType

B, S, D, H, DH, DL, DR = 2, 2048, 1024, 2, 128, 512, 64
N_UP = H * (2 * DH + DR)
FLOPS = 2 * B * S * D * DL + 2 * B * S * DL * N_UP
ROPE_BASE = 10000.0

P = 128
GROUP = 4
HALF = DR // 2
N_POS = S // P
N_TILES = B * N_POS
FAST = 24
SLOW = HALF - FAST
BLOCKS = DL // 8
WIDE_BUFS = {1: 2, 2: 5, 4: 7}
XG_BUFS = 4
K_BUFS = 3
V_BUFS = 3
PROD_BUFS = 3
ASIDE_BLOCKS = 56


def tile_multilatentattention_pa_t_kernel(tc, x_bytes, x_scale, w_down, w_up, out_k, out_v):
    nc = tc.nc
    x_view = x_bytes.rearrange("b (q i) d -> b q i d", i=N_POS)
    k_view = out_k.rearrange("b (q i) h f -> b q i (h f)", i=N_POS)
    v_view = out_v.rearrange("b (q i) h f -> b q i (h f)", i=N_POS)
    wd_view = w_down.rearrange("(g p j) c -> g p j c", p=P, j=4)
    wu_view = w_up.rearrange("(m t r) n -> r m t n", t=4, r=2)

    with ExitStack() as ctx:
        const = ctx.enter_context(tc.tile_pool(name="const", bufs=1))
        work = ctx.enter_context(tc.tile_pool(name="work", bufs=3))
        psum = ctx.enter_context(tc.psum_pool(name="psum", bufs=1))
        ctx.enter_context(tc.manual_schedule())

        wd_raw = [const.tile([P, 4, DL], BF16, name="wd_raw%d" % g) for g in range(2)]
        wu_raw = const.tile([P, 4, N_UP], BF16, name="wu_raw")
        scale_rows = const.tile([P, 2, 8], F32, name="scale_rows")
        scale_cols = scale_rows[:, :, 0:4]
        raw = {}

        def load_x(n, count):
            room = const.tile([P, count, D], U8, name="xb%d" % n)
            b, i = divmod(n, N_POS)
            nc.sync.dma_start(out=room[:], in_=x_view[b][:, i:i + count])
            for j in range(count):
                raw[n + j] = (room, j)

        def load_scales():
            nc.sync.dma_start(out=scale_cols, in_=x_scale.rearrange("a b (g p t) -> p (a b g) t", p=P, t=4))

        def load_down(g):
            nc.sync.dma_start(out=wd_raw[g][:], in_=wd_view[g])

        def load_up():
            for r in range(2):
                nc.sync.dma_start(out=wu_raw[r:P:2], in_=wu_view[r])

        load_x(0, 1)
        load_x(1, 1)
        load_scales()
        load_x(2, 1)
        load_down(0)
        load_x(3, 1)
        load_x(4, 2)
        load_x(6, 2)
        load_down(1)
        load_x(8, 4)
        load_x(12, 4)
        load_up()
        for n in range(16, N_TILES, GROUP):
            load_x(n, GROUP)

        position = const.tile([P, N_POS], F32, name="position")
        nc.gpsimd.iota(position[:], pattern=[[1, N_POS]], base=0, channel_multiplier=N_POS, allow_small_or_imprecise_dtypes=True)
        offset = const.tile([P, P], F32, name="offset")
        nc.gpsimd.iota(offset[:], pattern=[[1, P]], base=0, channel_multiplier=-1, allow_small_or_imprecise_dtypes=True)
        ident = const.tile([P, P], F32, name="ident")
        turns = const.tile([P, N_POS, HALF], F32, name="turns")
        for j in range(FAST, HALF):
            nc.vector.tensor_scalar(
                out=turns[:, :, j], in0=position[:], scalar1=ROPE_BASE ** (-j / HALF) / (2 * math.pi), scalar2=None, op0=ALU.mult,
            )
        nc.vector.tensor_scalar(out=ident[:], in0=offset[:], scalar1=0.0, scalar2=None, op0=ALU.is_equal)
        whole = const.tile([P, 2, N_POS, FAST], I32, name="whole_then_wd", align_bytes=64)
        for lo in range(0, FAST, SLOW):
            nc.vector.tensor_scalar(
                out=turns[:, :, lo:lo + SLOW], in0=turns[:, :, FAST:],
                scalar1=ROPE_BASE ** ((FAST - lo) / HALF), scalar2=None, op0=ALU.mult,
            )
        for c in (1, 0):
            for lo in range(0, FAST, SLOW):
                nc.vector.tensor_scalar(
                    out=whole[:, c, :, lo:lo + SLOW], in0=turns[:, :, FAST:],
                    scalar1=ROPE_BASE ** ((FAST - lo) / HALF), scalar2=0.25 * (1 - c), op0=ALU.mult, op1=ALU.add,
                )
        frac = const.tile([P, 2, N_POS, FAST], F32, name="frac")
        trig = const.tile([P, N_POS, 4, HALF], F32, name="trig")
        for c in (1, 0):
            nc.vector.tensor_tensor(out=frac[:, c], in0=turns[:, :, 0:FAST], in1=whole[:, c], op=ALU.subtract)

        is_sine = (0, 1, 1, 0)
        sign = (1.0, 1.0, -1.0, 1.0)

        def table(entry, fast):
            c = is_sine[entry]
            nc.scalar.activation(
                out=trig[:, :, entry, 0:FAST] if fast else trig[:, :, entry, FAST:], in_=frac[:, c] if fast else turns[:, :, FAST:],
                func=ACT.Sin, scale=(1 if fast or c else -1) * sign[entry] * 2 * math.pi, bias=(1 - c) * math.pi / 2,
            )

        def table_from(entry, source, engine):
            engine.tensor_scalar(out=trig[:, :, entry], in0=trig[:, :, source], scalar1=sign[entry], scalar2=0.0, op0=ALU.mult, op1=ALU.add)

        wd_grp = const.tile([P, 4, 2, P * 4], BF16, align_bytes=64, name="whole_then_wd")
        wd_codes = const.tile([P, 4, 2, P], U32, align_bytes=256, name="wd_codes")
        wd_scales = const.tile([P, 4, 2, P], U8, align_bytes=256, name="wd_scales")
        wu_grp = {}
        wu_codes = const.tile([P, N_UP], U32, align_bytes=256, name="wu_codes")
        wu_scales = const.tile([P, N_UP], U8, align_bytes=256, name="wu_scales")
        UP_K = (slice(0, H * DH), 0, DH)
        UP_V = (slice(H * DH, 2 * H * DH), DH + DR, 2 * DH + DR)
        UP_R = (slice(2 * H * DH, N_UP), DH, DH + DR)

        def on_gpsimd(out, in_):
            nc.gpsimd.tensor_scalar(out=out, in0=in_, scalar1=1.0, scalar2=0.0, op0=ALU.mult, op1=ALU.add)

        def on_vector(out, in_):
            nc.vector.tensor_copy(out=out, in_=in_)

        def on_scalar(out, in_):
            nc.scalar.copy(out=out, in_=in_)

        def group_down(g, lo, hi, copy):
            copy(
                wd_grp[:, :, g].rearrange("p t (m r j) -> p m t r j", r=2, j=4)[:, lo:hi],
                wd_raw[g][:].rearrange("p j (m t r) -> p m t r j", t=4, r=2)[:, lo:hi],
            )

        def quant_down(lo, hi):
            nc.vector.quantize_mx(
                out=wd_codes[:, lo:hi].rearrange("p t g c -> p (t g c)").bitcast(FP8X4),
                scales=wd_scales[:, lo:hi].rearrange("p t g c -> p (t g c)"),
                in_=wd_grp[:, lo:hi].rearrange("p t g c -> p (t g c)"),
            )

        def spent_room(n):
            values, codes, scales, i = xg[n]
            return values[:, i:].rearrange("p i g c -> p (i g c)")

        def group_up(part, spent, copy):
            cols, lo, hi = part
            wu_grp[lo] = spent_room(spent)[:, 0:4 * H * (hi - lo)]
            copy(
                wu_grp[lo].rearrange("p (h f j) -> p h f j", h=H, j=4),
                wu_raw[:].rearrange("p j (h f) -> p h f j", h=H)[:, :, lo:hi, :],
            )

        def quant_up(part):
            cols, lo, hi = part
            nc.vector.quantize_mx(out=wu_codes[:, cols].bitcast(FP8X4), scales=wu_scales[:, cols], in_=wu_grp[lo])

        opened = []

        def next_bank():
            opened.append(4 + len(opened) % 4)
            return opened[-1]

        def open_bank(shape, number):
            return psum.tile(shape, F32, name="bank%d" % (next_bank() if number is None else number))

        wide = {}
        turned = {}
        xg = {}
        lat = {}
        lg = {}
        lc = {}
        k_out = {}
        v_out = {}
        products = {}

        def widen(n, count=1, passes=(0, 1), engine=None):
            width = count * len(passes) * P
            room = work.tile([P, 2, width, 2], BF16, name="wide%d" % width, bufs=WIDE_BUFS[width // P])
            source, j = raw[n]
            codes = source[:, j:j + count].bitcast(FP8).rearrange("p i (m u e) -> p u (i m) e", u=2, e=2)
            codes = codes[:, :, P * passes[0]:P * passes[0] + width]
            if engine is None:
                nc.scalar.copy(out=room[:], in_=codes)
            else:
                engine.tensor_copy(out=room[:], in_=codes)
            for i in range(count):
                for at, g in enumerate(passes):
                    lo = P * (len(passes) * i + at)
                    wide[n + i, g] = room[:, :, lo:lo + P]

        def turn(n, passes=(0, 1), tag=None):
            bank = open_bank([P, 2, 2, P], n % 4 if tag is None else tag)
            for g in passes:
                turned[n, g] = bank
                for u in range(2):
                    words = wide[n, g][:, u].rearrange("p m e -> p (m e)").bitcast(F32)
                    nc.tensor.transpose(bank[:, u, g, :], words, ident[:])

        def open_x(lo, count):
            values = work.tile([P, count, 2, P * 4], BF16, name="xg", align_bytes=64, bufs=XG_BUFS)
            codes = work.tile([P, count, 2, P], U32, name="xcodes", align_bytes=256)
            scales = work.tile([P, count, 2, P], U8, name="xscales", align_bytes=256)
            for i in range(count):
                xg[lo + i] = (values, codes, scales, i)

        def scale_x(n, passes=(0, 1)):
            values, codes, scales, i = xg[n]
            gs = slice(passes[0], passes[-1] + 1)
            nc.vector.tensor_tensor(
                out=values[:, i, gs].rearrange("p g (r u e) -> p g r u e", u=2, e=2),
                in0=turned[n, passes[0]][:, :, gs].bitcast(BF16).rearrange("p u g (r e) -> p g r u e", e=2),
                in1=scale_cols[:, gs].rearrange("p g (u e) -> p g u e", e=2).unsqueeze(2).to_broadcast([P, len(passes), P, 2, 2]),
                op=ALU.mult,
            )

        def scale_aside(n, g):
            values, codes, scales, i = xg[n]
            words = work.tile([P, P, 2], F32, name="words", bufs=1)
            nc.scalar.copy(out=words[:], in_=turned[n, g][:, :, g].rearrange("p u r -> p r u"))
            nc.gpsimd.tensor_tensor(
                out=values[:, i, g].rearrange("p (r t) -> p r t", t=4),
                in0=words[:].bitcast(BF16),
                in1=scale_cols[:, g].unsqueeze(1).to_broadcast([P, P, 4]),
                op=ALU.mult,
            )

        def quant_x(n, count):
            values, codes, scales, i = xg[n]
            nc.vector.quantize_mx(
                out=codes[:, i:i + count].rearrange("p i g r -> p (i g r)").bitcast(FP8X4),
                scales=scales[:, i:i + count].rearrange("p i g r -> p (i g r)"),
                in_=values[:, i:i + count].rearrange("p i g c -> p (i g c)"),
            )

        def down(n, tag=None):
            bank = open_bank([P, 4, P], tag)
            lat[n] = bank
            values, codes, scales, i = xg[n]
            for t in range(4):
                for g in range(2):
                    nc.tensor.matmul_mx(
                        out=bank[:, t, :],
                        lhsT=wd_codes[:, t, g].bitcast(FP8X4), lhsT_scale=wd_scales[:, t, g],
                        rhs=codes[:, i, g].bitcast(FP8X4), rhs_scale=scales[:, i, g],
                        start=(g == 0), stop=(g == 1),
                    )

        def empty_down(n, copy=on_scalar):
            g, i = divmod(n, GROUP)
            if g not in lg:
                lg[g] = work.tile([P, GROUP, P, 4], BF16, name="lg", align_bytes=64, bufs=3)
            copy(lg[g][:, i], lat[n][:].rearrange("p t r -> p r t"))

        def first(n, tag=None, copy=on_scalar):
            down(n, tag)
            empty_down(n, copy)

        def quant_lat(n, count):
            g, i = divmod(n, GROUP)
            if g not in lc:
                codes = work.tile([P, GROUP, P], U32, name="lcodes", align_bytes=256)
                scales = work.tile([P, GROUP, P], U8, name="lscales", align_bytes=256)
                lc[g] = (codes, scales)
            codes, scales = lc[g]
            nc.vector.quantize_mx(
                out=codes[:, i:i + count].rearrange("p i r -> p (i r)").bitcast(FP8X4),
                scales=scales[:, i:i + count].rearrange("p i r -> p (i r)"),
                in_=lg[g][:, i:i + count].rearrange("p i r t -> p (i r t)"),
            )

        def expand(n, count, part, tag):
            cols = part[0]
            bank = open_bank([P, count, cols.stop - cols.start], tag)
            for j in range(count):
                g, i = divmod(n + j, GROUP)
                codes, scales = lc[g]
                nc.tensor.matmul_mx(
                    out=bank[:, j],
                    lhsT=codes[:, i].bitcast(FP8X4), lhsT_scale=scales[:, i],
                    rhs=wu_codes[:, cols].bitcast(FP8X4), rhs_scale=wu_scales[:, cols],
                    start=True, stop=True,
                )
            return bank

        def k_tile(g, spent=None):
            if g not in k_out:
                if spent is None:
                    room = work.tile([P, GROUP * H * (DH + DR)], F32, name="k_out", bufs=K_BUFS)
                    room = room[:]
                else:
                    room = spent_room(spent).bitcast(F32)[:, 0:GROUP * H * (DH + DR)]
                k_out[g] = room.rearrange("p (i h f) -> p i h f", h=H, f=DH + DR)
            return k_out[g]

        def v_tile(g):
            if g not in v_out:
                v_out[g] = work.tile([P, GROUP, H * DH], F32, name="v_out", bufs=V_BUFS)
            return v_out[g]

        def second_k(n, count=2, tag=None, copy=on_scalar):
            bank = expand(n, count, UP_K, tag)
            g, i = divmod(n, GROUP)
            copy(k_tile(g)[:, i:i + count, :, 0:DH], bank[:].rearrange("p i (h f) -> p i h f", h=H))

        def second_v(n, count=2, tag=None, copy=on_scalar):
            bank = expand(n, count, UP_V, tag)
            g, i = divmod(n, GROUP)
            copy(v_tile(g)[:, i:i + count], bank[:])

        def rope_products(engine, source, n, count, spent=None):
            if spent is None:
                room = work.tile([P, count * H * 2 * DR], F32, name="products", bufs=PROD_BUFS)
                room = room[:]
            else:
                room = spent_room(spent).bitcast(F32)[:, 0:count * H * 2 * DR]
            room = room.rearrange("p (i h a c f) -> p i h a c f", h=H, a=2, c=2, f=HALF)
            products[n] = room
            shape = [P, count, H, 2, 2, HALF]
            at = n % N_POS
            engine.tensor_tensor(
                out=room,
                in0=source.rearrange("p i (h a f) -> p i h a f", h=H, a=2).unsqueeze(4).to_broadcast(shape),
                in1=trig[:, at:at + count].rearrange("p i (a c) f -> p i a c f", a=2).unsqueeze(2).to_broadcast(shape),
                op=ALU.mult,
            )

        def rope_add(engine, n, count):
            g, i = divmod(n, GROUP)
            engine.tensor_tensor(
                out=k_tile(g)[:, i:i + count, :, DH:].rearrange("p i h f -> p (i h) f"),
                in0=products[n][:, :, :, 0].rearrange("p i h c f -> p (i h) (c f)"),
                in1=products[n][:, :, :, 1].rearrange("p i h c f -> p (i h) (c f)"),
                op=ALU.add,
            )

        def products_aside(n, count=GROUP, tag=None, spent=None):
            bank = expand(n, count, UP_R, tag)
            spill = work.tile([P, count, H * DR], F32, name="spill", bufs=2)
            nc.scalar.copy(out=spill[:], in_=bank[:])
            rope_products(nc.gpsimd, spill[:], n, count, spent)

        rope = {}

        def up_rope(n, count, tag=None):
            rope[n] = expand(n, count, UP_R, tag)

        def products_direct(n, count):
            rope_products(nc.vector, rope[n][:], n, count)

        def store_v(n, count):
            g, i = divmod(n, GROUP)
            b, at = divmod(n, N_POS)
            nc.sync.dma_start(out=v_view[b][:, at:at + count], in_=v_out[g][:, i:i + count])

        def store_k(n, count):
            g, i = divmod(n, GROUP)
            b, at = divmod(n, N_POS)
            nc.sync.dma_start(out=k_view[b][:, at:at + count], in_=k_out[g][:, i:i + count].rearrange("p i h f -> p i (h f)"))

        table(1, False)
        widen(0, 1, (0,))
        widen(0, 1, (1,))
        widen(1)
        group_down(0, 0, BLOCKS, on_gpsimd)
        group_down(1, 0, ASIDE_BLOCKS, on_gpsimd)
        widen(2)
        table(0, False)
        table(1, True)
        table(0, True)
        widen(3)
        widen(4, 2)
        widen(6, 2)
        group_down(1, ASIDE_BLOCKS, BLOCKS, on_scalar)
        table(2, True)
        table(3, True)
        table(2, False)
        table(3, False)
        for n in (8, 10, 12):
            widen(n, 2)
        open_x(0, 2)
        open_x(2, GROUP)
        turn(0, (0,))
        turn(0, (1,), 4)
        turn(1)
        turn(2)
        turn(3)
        scale_x(0, (0,))
        scale_x(0, (1,))
        for n in range(1, 6):
            turn(n + 3)
            scale_x(n)
        quant_x(0, 1)
        quant_down(0, 2)
        quant_down(2, 4)
        quant_x(1, 1)
        quant_x(2, GROUP)
        group_up(UP_V, 2, on_gpsimd)
        turn(9)
        open_x(6, GROUP)
        scale_aside(9, 1)
        group_up(UP_R, 3, on_gpsimd)
        widen(14, 2)
        first(0)
        first(1)
        first(2)
        first(3)

        share = {1: ((16, 2), (18, 2), (20, 1)), 2: ((21, 1), (22, 2), (24, 1)), 3: ((25, 1), (26, 2)), 4: ((28, 2),), 5: ((30, 2),)}
        for r in range(1, 6):
            now = GROUP * r + 2
            mid = now - GROUP
            old = GROUP * (r - 2)
            older = old - GROUP
            ahead = now + GROUP
            if now not in xg:
                open_x(now, GROUP)
            if older >= 0:
                k_tile(older // GROUP, mid)
                rope_add(nc.gpsimd, older, GROUP)
            if old == 0:
                group_up(UP_K, mid, on_gpsimd)
            if old >= 0:
                products_aside(old)
                second_v(old)
                second_v(old + 2)
                store_v(old, GROUP)
            for n in range(now, now + GROUP):
                scale_x(n, (0,) if n == 9 else (0, 1))
            for n in range(mid, mid + GROUP):
                if n not in lat:
                    first(n)
            if older >= 0:
                second_k(older)
                second_k(older + 2)
                store_k(older, GROUP)
            for n in (ahead + 2, ahead + 1, ahead, ahead + 3):
                turn(n)
            for n, count in share[r]:
                widen(n, count)
            quant_lat(old + GROUP, GROUP)
            if r == 1:
                quant_up(UP_R)
                quant_up(UP_V)
            if r == 2:
                quant_up(UP_K)
            quant_x(now, GROUP)

        open_x(26, GROUP)
        k_tile(3, 22)
        k_tile(4)
        rope_add(nc.gpsimd, 12, GROUP)
        products_aside(16)
        second_k(12)
        second_k(14)
        store_k(12, GROUP)
        second_v(16)
        second_v(18)
        store_v(16, GROUP)
        for n in range(26, 30):
            scale_x(n)
        first(22)
        first(23)
        second_k(16)
        second_k(18)
        first(24)
        first(25)
        quant_lat(20, GROUP)
        rope_add(nc.vector, 16, GROUP)
        store_k(16, GROUP)
        quant_x(26, GROUP)

        open_x(30, 2)
        quant_lat(24, 2)
        up_rope(20, 2, 0)
        up_rope(22, 2, 1)
        second_v(20)
        second_v(22)
        store_v(20, GROUP)
        products_direct(20, 2)
        rope_add(nc.gpsimd, 20, 2)
        products_direct(22, 2)
        rope_add(nc.gpsimd, 22, 2)
        second_k(20)
        store_k(20, 2)
        second_k(22)
        store_k(22, 2)
        turn(30)
        turn(31)
        first(26)
        first(27)
        up_rope(24, 2, 0)
        scale_x(30)
        products_direct(24, 2)
        quant_lat(26, 2)
        rope_add(nc.gpsimd, 24, 2)
        second_v(24)
        store_v(24, 2)
        second_k(24)
        store_k(24, 2)
        scale_x(31)
        first(28)
        first(29)
        up_rope(26, 2, 1)
        second_v(26)
        store_v(26, 2)
        second_k(26)
        quant_x(30, 1)
        quant_x(31, 1)
        products_direct(26, 2)
        quant_lat(28, 2)
        rope_add(nc.gpsimd, 26, 2)
        store_k(26, 2)
        first(30, 2, on_vector)
        first(31, 3)
        up_rope(28, 2, 0)
        second_v(28)
        store_v(28, 2)
        second_k(28)
        products_direct(28, 2)
        quant_lat(30, 2)
        rope_add(nc.vector, 28, 2)
        store_k(28, 2)
        up_rope(30, 2, 1)
        second_v(30)
        store_v(30, 2)
        products_direct(30, 2)
        second_k(30)
        rope_add(nc.vector, 30, 2)
        store_k(30, 2)
